import numpy as np
import ml_dtypes


def mxq(x, axis, fmt="e4m3"):
    dtype, down = {"e4m3": (ml_dtypes.float8_e4m3fn, 7), "e5m2": (ml_dtypes.float8_e5m2, 14)}[fmt]
    v = np.moveaxis(np.asarray(x, np.float32).astype(ml_dtypes.bfloat16).astype(np.float64), axis, -1)
    blocks = v.reshape(v.shape[:-1] + (-1, 32))
    amax = np.abs(blocks).max(-1, keepdims=True)
    byte = np.maximum(np.where(amax > 0, np.frexp(amax)[1] - 1 + 127, 0) - down, 1)
    scale = np.exp2(byte - 127.0)
    codes = (blocks / scale).astype(np.float32).astype(dtype).astype(np.float64)
    return np.moveaxis((codes * scale).reshape(v.shape), -1, axis)


BF16 = ml_dtypes.bfloat16


def bf(x):
    return np.asarray(x, np.float32).astype(BF16)


def f64(x):
    return np.asarray(x).astype(np.float64)


C_COUNT, NC, ROW, COL = 4, 48, 1024, 1024


def setup_inputs():
    z = np.random.standard_normal((C_COUNT, ROW, COL))
    load = np.random.standard_normal((C_COUNT, ROW, 1))
    pattern = np.random.standard_normal((C_COUNT, 1, COL))
    offset = np.random.standard_normal((C_COUNT, ROW, 1))
    gate = 1.0 + 0.375 * np.random.standard_normal((C_COUNT, ROW, 1))
    return {"feat_gated": bf(gate * (z + 0.7 * load * pattern + 0.5 * offset))}


def reference(feat_gated):
    F = f64(feat_gated)
    Fc = F - F.mean(-1, keepdims=True)
    inv_norm = 1.0 / np.sqrt((Fc * Fc).sum(-1, keepdims=True))
    Fn = Fc * inv_norm
    Fq = mxq(Fn, 2, "e4m3")
    return Fq @ Fq.transpose(0, 2, 1)

@@ -1,0 +1,274 @@
+from contextlib import ExitStack
+
+import concourse.mybir as mybir
+from concourse.masks import make_identity
+
+FLOPS = 2 * 4 * 1024 * 1024 * 1024
+
+BF16 = mybir.dt.bfloat16
+F32 = mybir.dt.float32
+U32 = mybir.dt.uint32
+U8 = mybir.dt.uint8
+FP8X4 = mybir.dt.float8_e4m3fn_x4
+ALU = mybir.AluOpType
+ACT = mybir.ActivationFunctionType
+
+P = 128
+K = 1024
+ROWS = 1024
+PINNED = False
+NF = 8
+NPT = 4
+NPM = 4
+NG = 2
+NO = 16
+
+LOADS = ((0,), (1,), (2,), (3,), (4, 5, 6, 7), (8, 9, 10, 11), (12, 13, 14, 15), (16, 17, 18, 19), (20, 21, 22, 23), (24, 25, 26, 27), (28, 29, 30, 31))
+BATCHES = ((0,), (1,), (2, 3), (4, 5), (6, 7), (8, 9, 10, 11), (12, 13, 14, 15), (16, 17, 18, 19), (20, 21, 22, 23), (24, 25, 26, 27), (28, 29, 30, 31))
+PIECES = ((0,), (1,), (2, 3), (4, 5), (6, 7), (8, 9, 10, 11), (12, 13, 14, 15), (16, 17, 18, 19), (20, 21, 22, 23), (24, 25, 26, 27), (28, 29), (30,), (31,))
+GROUPS = ((0, 0, 0, 1, 0), (0, 1, 0, 2, 1), (0, 0, 1, 1, 1), (0, 2, 0, 4, 2), (0, 3, 0, 4, 2), (0, 0, 2, 2, 2), (0, 1, 2, 2, 2), (0, 4, 0, 4, 3), (0, 4, 4, 2, 3), (0, 5, 0, 4, 3), (0, 5, 4, 2, 3), (0, 0, 4, 2, 3), (0, 1, 4, 2, 3), (0, 2, 4, 2, 3), (0, 3, 4, 2, 3), (0, 6, 0, 4, 4), (0, 6, 4, 4, 4), (0, 7, 0, 4, 4), (0, 7, 4, 4, 4), (0, 0, 6, 2, 4), (0, 1, 6, 2, 4), (0, 2, 6, 2, 4), (0, 3, 6, 2, 4), (0, 4, 6, 2, 4), (0, 5, 6, 2, 4), (1, 0, 0, 4, 5), (1, 1, 0, 4, 5), (1, 2, 0, 4, 5), (1, 3, 0, 4, 5), (1, 4, 0, 4, 6), (1, 4, 4, 4, 6), (1, 5, 0, 4, 6), (1, 5, 4, 4, 6), (1, 6, 0, 4, 6), (1, 6, 4, 4, 6), (1, 7, 0, 4, 6), (1, 7, 4, 4, 6), (1, 0, 4, 4, 6), (1, 1, 4, 4, 6), (1, 2, 4, 4, 6), (1, 3, 4, 4, 6), (2, 0, 0, 4, 7), (2, 1, 0, 4, 7), (2, 2, 0, 4, 7), (2, 3, 0, 4, 7), (2, 4, 0, 4, 8), (2, 4, 4, 4, 8), (2, 5, 0, 4, 8), (2, 5, 4, 4, 8), (2, 6, 0, 4, 8), (2, 6, 4, 4, 8), (2, 7, 0, 4, 8), (2, 7, 4, 4, 8), (2, 0, 4, 4, 8), (2, 1, 4, 4, 8), (2, 2, 4, 4, 8), (2, 3, 4, 4, 8), (3, 0, 0, 4, 9), (3, 1, 0, 4, 9), (3, 2, 0, 4, 9), (3, 3, 0, 4, 9), (3, 4, 0, 4, 10), (3, 4, 4, 2, 10), (3, 5, 0, 4, 10), (3, 5, 4, 2, 10), (3, 0, 4, 2, 10), (3, 1, 4, 2, 10), (3, 2, 4, 2, 10), (3, 3, 4, 2, 10), (3, 6, 0, 4, 11), (3, 6, 4, 2, 11), (3, 6, 6, 1, 11), (3, 0, 6, 1, 11), (3, 1, 6, 1, 11), (3, 2, 6, 1, 11), (3, 3, 6, 1, 11), (3, 4, 6, 1, 11), (3, 5, 6, 1, 11), (3, 7, 0, 4, 12), (3, 7, 4, 4, 12), (3, 0, 7, 1, 12), (3, 1, 7, 1, 12), (3, 2, 7, 1, 12), (3, 3, 7, 1, 12), (3, 4, 7, 1, 12), (3, 5, 7, 1, 12), (3, 6, 7, 1, 12))
+STORES = ((0, 6, 0, 8), (0, 7, 0, 8), (0, 0, 0, 8), (0, 1, 0, 8), (0, 2, 0, 8), (0, 3, 0, 8), (0, 4, 0, 8), (0, 5, 0, 8), (1, 4, 0, 8), (1, 5, 0, 8), (1, 6, 0, 8), (1, 7, 0, 8), (1, 0, 0, 8), (1, 1, 0, 8), (1, 2, 0, 8), (1, 3, 0, 8), (2, 4, 0, 8), (2, 5, 0, 8), (2, 6, 0, 8), (2, 7, 0, 8), (2, 0, 0, 8), (2, 1, 0, 8), (2, 2, 0, 8), (2, 3, 0, 8), (3, 0, 0, 4), (3, 1, 0, 4), (3, 2, 0, 4), (3, 3, 0, 4), (3, 4, 0, 4), (3, 5, 0, 4), (3, 6, 0, 4), (3, 6, 4, 3), (3, 0, 4, 3), (3, 1, 4, 3), (3, 2, 4, 3), (3, 3, 4, 3), (3, 4, 4, 3), (3, 5, 4, 3), (3, 7, 0, 8), (3, 0, 7, 1), (3, 1, 7, 1), (3, 2, 7, 1), (3, 3, 7, 1), (3, 4, 7, 1), (3, 5, 7, 1), (3, 6, 7, 1))
+SCHEDULE = (
+    ("L", 0, 0, "DMA"), ("L", 1, 0, "DMA"), ("L", 2, 0, "DMA"), ("L", 3, 0, "DMA"), ("L", 4, 0, "DMA"), ("A", 0, 0, "V"),
+    ("A", 1, 0, "V"), ("SQ", 0, 0, "S"), ("L", 5, 0, "DMA"), ("RC", 0, 0, "V"), ("A", 2, 0, "V"), ("SQ", 1, 0, "S"),
+    ("RC", 1, 0, "V"), ("B", 0, 0, "V"), ("B", 1, 0, "V"), ("T", 0, 0, "PE"), ("A", 3, 0, "V"), ("T", 1, 0, "PE"),
+    ("D", 0, 0, "S"), ("L", 6, 0, "DMA"), ("A", 4, 0, "V"), ("NM", 2, 0, "G"), ("SQ", 2, 0, "S"), ("D", 1, 0, "S"),
+    ("RC", 2, 0, "V"), ("Q", 0, 0, "V"), ("B", 2, 0, "G"), ("Q", 0, 1, "V"), ("A", 5, 0, "V"), ("L", 7, 0, "DMA"),
+    ("M", 0, 0, "PE"), ("G", 0, 0, "S"), ("B", 3, 0, "G"), ("Q", 1, 0, "V"), ("T", 2, 0, "PE"), ("SQ", 3, 0, "S"),
+    ("Q", 1, 1, "V"), ("A", 6, 0, "V"), ("M", 1, 0, "PE"), ("D", 2, 0, "S"), ("M", 2, 0, "PE"), ("NM", 3, 0, "G"),
+    ("T", 3, 0, "PE"), ("L", 8, 0, "DMA"), ("RC", 3, 0, "V"), ("A", 7, 0, "V"), ("B", 4, 0, "G"), ("G", 1, 0, "S"),
+    ("D", 3, 0, "S"), ("A", 8, 0, "V"), ("NM", 4, 0, "G"), ("T", 4, 0, "PE"), ("SQ", 4, 0, "S"), ("B", 5, 0, "G"),
+    ("G", 2, 0, "S"), ("D", 4, 0, "S"), ("L", 9, 0, "DMA"), ("RC", 4, 0, "V"), ("Q", 2, 0, "V"), ("Q", 2, 1, "V"),
+    ("B", 6, 0, "G"), ("A", 9, 0, "V"), ("T", 5, 0, "PE"), ("M", 3, 0, "PE"), ("D", 5, 0, "S"), ("A", 10, 0, "V"),
+    ("M", 4, 0, "PE"), ("B", 7, 0, "G"), ("L", 10, 0, "DMA"), ("G", 3, 0, "S"), ("T", 6, 0, "PE"), ("G", 4, 0, "S"),
+    ("Q", 3, 0, "V"), ("T", 7, 0, "PE"), ("Q", 3, 1, "V"), ("D", 6, 0, "S"), ("A", 11, 0, "V"), ("M", 5, 0, "PE"),
+    ("M", 6, 0, "PE"), ("M", 7, 0, "PE"), ("D", 7, 0, "S"), ("A", 12, 0, "V"), ("NM", 5, 0, "G"), ("M", 8, 0, "PE"),
+    ("SQ", 5, 0, "S"), ("G", 5, 0, "S"), ("RC", 5, 0, "V"), ("Q", 4, 0, "V"), ("G", 6, 0, "S"), ("B", 8, 0, "G"),
+    ("M", 9, 0, "PE"), ("Q", 4, 1, "V"), ("G", 7, 0, "S"), ("A", 13, 0, "V"), ("M", 10, 0, "PE"), ("G", 8, 0, "S"),
+    ("M", 11, 0, "PE"), ("G", 9, 0, "S"), ("M", 12, 0, "PE"), ("B", 9, 0, "G"), ("G", 10, 0, "S"), ("A", 14, 0, "V"),
+    ("M", 13, 0, "PE"), ("G", 11, 0, "S"), ("M", 14, 0, "PE"), ("G", 12, 0, "S"), ("M", 15, 0, "PE"), ("G", 13, 0, "S"),
+    ("B", 10, 0, "G"), ("G", 14, 0, "S"), ("M", 16, 0, "PE"), ("A", 15, 0, "V"), ("G", 15, 0, "S"), ("M", 17, 0, "PE"),
+    ("G", 16, 0, "S"), ("B", 11, 0, "G"), ("M", 18, 0, "PE"), ("A", 16, 0, "V"), ("G", 17, 0, "S"), ("ST", 0, 0, "DMA"),
+    ("M", 19, 0, "PE"), ("SQ", 6, 0, "S"), ("M", 20, 0, "PE"), ("G", 18, 0, "S"), ("M", 21, 0, "PE"), ("NM", 6, 0, "G"),
+    ("RC", 6, 0, "V"), ("T", 8, 0, "PE"), ("A", 17, 0, "V"), ("G", 19, 0, "S"), ("ST", 1, 0, "DMA"), ("B", 12, 0, "G"),
+    ("G", 20, 0, "S"), ("T", 9, 0, "PE"), ("G", 21, 0, "S"), ("D", 8, 0, "S"), ("T", 10, 0, "PE"), ("A", 18, 0, "V"),
+    ("ST", 2, 0, "DMA"), ("B", 13, 0, "G"), ("T", 11, 0, "PE"), ("D", 9, 0, "S"), ("T", 12, 0, "PE"), ("A", 19, 0, "V"),
+    ("ST", 3, 0, "DMA"), ("M", 22, 0, "PE"), ("B", 14, 0, "G"), ("M", 23, 0, "PE"), ("D", 10, 0, "S"), ("M", 24, 0, "PE"),
+    ("ST", 4, 0, "DMA"), ("D", 11, 0, "V"), ("T", 13, 0, "PE"), ("NM", 7, 0, "G"), ("SQ", 7, 0, "S"), ("T", 14, 0, "PE"),
+    ("D", 12, 0, "S"), ("B", 15, 0, "G"), ("RC", 7, 0, "V"), ("Q", 5, 0, "V"), ("Q", 5, 1, "V"), ("D", 13, 0, "S"),
+    ("B", 16, 0, "G"), ("T", 15, 0, "PE"), ("D", 14, 0, "V"), ("M", 25, 0, "PE"), ("D", 15, 0, "S"), ("G", 22, 0, "V"),
+    ("B", 17, 0, "G"), ("G", 23, 0, "V"), ("M", 26, 0, "PE"), ("ST", 5, 0, "DMA"), ("A", 20, 0, "V"), ("G", 24, 0, "S"),
+    ("G", 25, 0, "S"), ("M", 27, 0, "PE"), ("B", 18, 0, "G"), ("G", 26, 0, "S"), ("M", 28, 0, "PE"), ("ST", 6, 0, "DMA"),
+    ("Q", 6, 0, "V"), ("G", 27, 0, "S"), ("T", 16, 0, "PE"), ("Q", 6, 1, "V"), ("G", 28, 0, "S"), ("ST", 7, 0, "DMA"),
+    ("B", 19, 0, "G"), ("T", 17, 0, "PE"), ("A", 21, 0, "V"), ("D", 16, 0, "S"), ("T", 18, 0, "PE"), ("T", 19, 0, "PE"),
+    ("A", 22, 0, "V"), ("D", 17, 0, "S"), ("M", 29, 0, "PE"), ("D", 18, 0, "S"), ("M", 30, 0, "PE"), ("A", 23, 0, "V"),
+    ("M", 31, 0, "PE"), ("D", 19, 0, "S"), ("M", 32, 0, "PE"), ("G", 29, 0, "V"), ("NM", 8, 0, "G"), ("G", 30, 0, "V"),
+    ("M", 33, 0, "PE"), ("SQ", 8, 0, "S"), ("G", 31, 0, "S"), ("Q", 7, 0, "V"), ("M", 34, 0, "PE"), ("ST", 8, 0, "DMA"),
+    ("G", 32, 0, "S"), ("RC", 8, 0, "V"), ("M", 35, 0, "PE"), ("Q", 7, 1, "V"), ("B", 20, 0, "G"), ("G", 33, 0, "S"),
+    ("M", 36, 0, "PE"), ("ST", 9, 0, "DMA"), ("A", 24, 0, "V"), ("G", 34, 0, "S"), ("M", 37, 0, "PE"), ("B", 21, 0, "G"),
+    ("G", 35, 0, "S"), ("M", 38, 0, "PE"), ("ST", 10, 0, "DMA"), ("A", 25, 0, "V"), ("G", 36, 0, "S"), ("M", 39, 0, "PE"),
+    ("G", 37, 0, "S"), ("B", 22, 0, "G"), ("M", 40, 0, "PE"), ("ST", 11, 0, "DMA"), ("A", 26, 0, "V"), ("G", 38, 0, "S"),
+    ("M", 41, 0, "PE"), ("G", 39, 0, "S"), ("M", 42, 0, "PE"), ("ST", 12, 0, "DMA"), ("B", 23, 0, "G"), ("A", 27, 0, "V"),
+    ("G", 40, 0, "S"), ("M", 43, 0, "PE"), ("G", 41, 0, "S"), ("M", 44, 0, "PE"), ("ST", 13, 0, "DMA"), ("A", 28, 0, "V"),
+    ("G", 42, 0, "S"), ("NM", 9, 0, "G"), ("T", 20, 0, "PE"), ("SQ", 9, 0, "S"), ("G", 43, 0, "S"), ("T", 21, 0, "PE"),
+    ("ST", 14, 0, "DMA"), ("RC", 9, 0, "V"), ("A", 29, 0, "V"), ("T", 22, 0, "PE"), ("D", 20, 0, "S"), ("B", 24, 0, "G"),
+    ("T", 23, 0, "PE"), ("ST", 15, 0, "DMA"), ("D", 21, 0, "S"), ("D", 22, 0, "V"), ("B", 25, 0, "G"), ("T", 24, 0, "PE"),
+    ("D", 23, 0, "S"), ("A", 30, 0, "V"), ("B", 26, 0, "G"), ("T", 25, 0, "PE"), ("D", 24, 0, "S"), ("Q", 8, 0, "V"),
+    ("B", 27, 0, "G"), ("Q", 8, 1, "V"), ("T", 26, 0, "PE"), ("D", 25, 0, "S"), ("A", 31, 0, "V"), ("M", 45, 0, "PE"),
+    ("D", 26, 0, "S"), ("T", 27, 0, "PE"), ("M", 46, 0, "PE"), ("D", 27, 0, "V"), ("SQ", 10, 0, "S"), ("G", 44, 0, "S"),
+    ("M", 47, 0, "PE"), ("G", 45, 0, "S"), ("RC", 10, 0, "V"), ("M", 48, 0, "PE"), ("Q", 9, 0, "V"), ("G", 46, 0, "S"),
+    ("M", 49, 0, "PE"), ("Q", 9, 1, "V"), ("G", 47, 0, "S"), ("ST", 16, 0, "DMA"), ("M", 50, 0, "PE"), ("B", 28, 0, "V"),
+    ("G", 48, 0, "S"), ("B", 29, 0, "V"), ("T", 28, 0, "PE"), ("B", 30, 0, "V"), ("G", 49, 0, "S"), ("ST", 17, 0, "DMA"),
+    ("B", 31, 0, "V"), ("T", 29, 0, "PE"), ("D", 28, 0, "S"), ("T", 30, 0, "PE"), ("T", 31, 0, "PE"), ("D", 29, 0, "V"),
+    ("D", 30, 0, "S"), ("M", 51, 0, "PE"), ("M", 52, 0, "PE"), ("Q", 10, 0, "V"), ("G", 50, 0, "S"), ("Q", 10, 1, "V"),
+    ("M", 53, 0, "PE"), ("Q", 11, 0, "V"), ("G", 51, 0, "S"), ("Q", 11, 1, "V"), ("ST", 18, 0, "DMA"), ("M", 54, 0, "PE"),
+    ("D", 31, 0, "V"), ("G", 52, 0, "S"), ("M", 55, 0, "PE"), ("G", 53, 0, "S"), ("ST", 19, 0, "DMA"), ("M", 56, 0, "PE"),
+    ("Q", 12, 0, "V"), ("G", 54, 0, "S"), ("Q", 12, 1, "V"), ("M", 57, 0, "PE"), ("G", 55, 0, "S"), ("ST", 20, 0, "DMA"),
+    ("M", 58, 0, "PE"), ("G", 56, 0, "S"), ("M", 59, 0, "PE"), ("G", 57, 0, "S"), ("ST", 21, 0, "DMA"), ("M", 60, 0, "PE"),
+    ("G", 58, 0, "S"), ("M", 61, 0, "PE"), ("G", 59, 0, "S"), ("ST", 22, 0, "DMA"), ("M", 62, 0, "PE"), ("G", 60, 0, "S"),
+    ("M", 63, 0, "PE"), ("G", 61, 0, "S"), ("M", 64, 0, "PE"), ("ST", 23, 0, "DMA"), ("G", 62, 0, "V"), ("G", 63, 0, "S"),
+    ("M", 65, 0, "PE"), ("M", 66, 0, "PE"), ("G", 64, 0, "S"), ("M", 67, 0, "PE"), ("ST", 24, 0, "DMA"), ("G", 65, 0, "S"),
+    ("M", 68, 0, "PE"), ("G", 66, 0, "S"), ("M", 69, 0, "PE"), ("ST", 25, 0, "DMA"), ("G", 67, 0, "S"), ("G", 68, 0, "S"),
+    ("M", 70, 0, "PE"), ("ST", 26, 0, "DMA"), ("G", 69, 0, "S"), ("M", 71, 0, "PE"), ("M", 72, 0, "PE"), ("G", 70, 0, "V"),
+    ("G", 71, 0, "S"), ("ST", 27, 0, "DMA"), ("M", 73, 0, "PE"), ("G", 72, 0, "S"), ("M", 75, 0, "PE"), ("G", 73, 0, "S"),
+    ("M", 74, 0, "PE"), ("G", 75, 0, "S"), ("M", 76, 0, "PE"), ("ST", 28, 0, "DMA"), ("G", 74, 0, "S"), ("M", 77, 0, "PE"),
+    ("G", 76, 0, "S"), ("M", 79, 0, "PE"), ("G", 77, 0, "S"), ("ST", 29, 0, "DMA"), ("M", 78, 0, "PE"), ("G", 79, 0, "S"),
+    ("ST", 30, 0, "DMA"), ("M", 80, 0, "PE"), ("G", 78, 0, "S"), ("M", 81, 0, "PE"), ("M", 83, 0, "PE"), ("ST", 31, 0, "DMA"),
+    ("G", 80, 0, "V"), ("G", 81, 0, "S"), ("M", 82, 0, "PE"), ("G", 83, 0, "S"), ("M", 84, 0, "PE"), ("ST", 32, 0, "DMA"),
+    ("G", 82, 0, "S"), ("M", 85, 0, "PE"), ("G", 84, 0, "S"), ("M", 86, 0, "PE"), ("G", 85, 0, "S"), ("G", 86, 0, "S"),
+    ("ST", 33, 0, "DMA"), ("ST", 34, 0, "DMA"), ("ST", 35, 0, "DMA"), ("ST", 36, 0, "DMA"), ("ST", 37, 0, "DMA"), ("ST", 38, 0, "DMA"),
+    ("ST", 39, 0, "DMA"), ("ST", 40, 0, "DMA"), ("ST", 41, 0, "DMA"), ("ST", 42, 0, "DMA"), ("ST", 43, 0, "DMA"), ("ST", 44, 0, "DMA"),
+    ("ST", 45, 0, "DMA"),
+)
+
+
+def tile_generator_pb_t_kernel(tc, feat_gated, out):
+    nc = tc.nc
+    with ExitStack() as ctx:
+        const = ctx.enter_context(tc.tile_pool(name="const", bufs=1))
+        xin = ctx.enter_context(tc.tile_pool(name="xin", bufs=1))
+        stat = ctx.enter_context(tc.tile_pool(name="stat", bufs=1))
+        work = ctx.enter_context(tc.tile_pool(name="work", bufs=1))
+        psum = ctx.enter_context(tc.psum_pool(name="psum", bufs=1))
+
+        ident = const.tile([P, P], BF16, name="ident")
+        make_identity(nc, ident[:])
+
+        xs = [xin.tile([P, 8, K], BF16, name="x%d" % c) for c in range(4)]
+        st = stat.tile([P, 32, 2, 6], F32, name="st")
+        mv = stat.tile([P, 32, 2], F32, name="mv")
+        sd = stat.tile([P, 32], F32, name="sd")
+        inv = stat.tile([P, 32], F32, name="inv")
+        nm = stat.tile([P, 32], F32, name="nm")
+
+        piece_of = {}
+        for pi in range(len(PIECES)):
+            for j in PIECES[pi]:
+                piece_of[j] = pi
+        fns = {}
+        pts = {}
+        grs = {}
+        cds = {}
+        pms = {}
+        ots = {}
+
+        def eng_of(e):
+            if e == "V":
+                return nc.vector
+            if e == "S":
+                return nc.scalar
+            return nc.gpsimd
+
+        def copy_on(e, dst, src):
+            if e == "V":
+                nc.vector.tensor_copy(out=dst, in_=src)
+            else:
+                nc.scalar.copy(out=dst, in_=src)
+
+        def do_load(li):
+            t = LOADS[li]
+            c, a0 = divmod(t[0], 8)
+            n = len(t)
+            src = feat_gated[c, P * a0 : P * (a0 + n), :].rearrange("(a p) k -> p a k", p=P)
+            nc.sync.dma_start(out=xs[c][:, a0 : a0 + n, :], in_=src)
+
+        def do_stats(j):
+            c, a = divmod(j, 8)
+            for h in range(2):
+                nc.vector.bn_stats(out=st[:, j, h, :], in_=xs[c][:, a, 512 * h : 512 * h + 512])
+            nc.vector.bn_aggr(out=mv[:, j, :], in_=st[:, j, :, :].rearrange("p a b -> p (a b)"))
+
+        def do_norm(j, e):
+            c, a = divmod(j, 8)
+            fn = work.tile([P, K], BF16, name="fn", tag="fn%d" % (j % NF))
+            fns[j] = fn
+            if e == "V":
+                nc.vector.tensor_scalar(
+                    out=fn[:], in0=xs[c][:, a, :], scalar1=mv[:, j, 0:1], scalar2=inv[:, j : j + 1],
+                    op0=ALU.subtract, op1=ALU.mult,
+                )
+            else:
+                nc.gpsimd.tensor_scalar(
+                    out=fn[:], in0=xs[c][:, a, :], scalar1=nm[:, j : j + 1], scalar2=inv[:, j : j + 1],
+                    op0=ALU.add, op1=ALU.mult,
+                )
+
+        def do_transposes(j):
+            pt = psum.tile([P, 8, P], BF16, name="pt", tag="pt%d" % (j % NPT))
+            pts[j] = pt
+            for b in range(8):
+                nc.tensor.transpose(pt[:, b, :], fns[j][:, P * b : P * b + P], ident[:])
+
+        def do_regroup(j, e):
+            pi = piece_of[j]
+            t = PIECES[pi]
+            if pi not in grs:
+                grs[pi] = work.tile([P, 2, P * len(t), 4], BF16, name="gr", tag="gr%d" % (pi % NG), align_bytes=64)
+            a = j - t[0]
+            copy_on(e, grs[pi][:, :, P * a : P * a + P, :], pts[j][:].rearrange("p (g t) r -> p g r t", g=2))
+
+        def do_quantise(pi, g):
+            t = PIECES[pi]
+            c, a0 = divmod(t[0], 8)
+            if c not in cds:
+                cds[c] = (
+                    work.tile([P, 2, ROWS], U32, name="codes", tag="codes%d" % (c % 2), align_bytes=64),
+                    work.tile([P, 2, ROWS], U8, name="scales", tag="scales%d" % (c % 2), align_bytes=64),
+                )
+            cols = slice(P * a0, P * (a0 + len(t)))
+            nc.vector.quantize_mx(
+                out=cds[c][0][:, g, cols].bitcast(FP8X4),
+                scales=cds[c][1][:, g, cols],
+                in_=grs[pi][:, g, :, :].rearrange("p r t -> p (r t)"),
+            )
+
+        def do_matmul(gi):
+            c, i, x0, w, pi = GROUPS[gi]
+            pm = psum.tile([P, 512], F32, name="pm", tag="pm%d" % (gi % NPM))
+            pms[gi] = pm
+            codes, scales = cds[c]
+            for g in range(2):
+                nc.tensor.matmul_mx(
+                    out=pm[:, 0 : P * w],
+                    lhsT=codes[:, g, P * i : P * i + P].bitcast(FP8X4),
+                    lhsT_scale=scales[:, g, P * i : P * i + P],
+                    rhs=codes[:, g, P * x0 : P * (x0 + w)].bitcast(FP8X4),
+                    rhs_scale=scales[:, g, P * x0 : P * (x0 + w)],
+                    start=(g == 0),
+                    stop=(g == 1),
+                )
+
+        def do_out(gi, e):
+            c, i, x0, w, pi = GROUPS[gi]
+            key = 8 * c + i
+            if key not in ots:
+                ots[key] = work.tile([P, ROWS], F32, name="ot", tag="ot%d" % (key % NO))
+            copy_on(e, ots[key][:, P * x0 : P * (x0 + w)], pms[gi][:, 0 : P * w])
+
+        def do_store(k):
+            c, i, x0, w = STORES[k]
+            nc.sync.dma_start(
+                out=out[c, P * i : P * i + P, P * x0 : P * (x0 + w)],
+                in_=ots[8 * c + i][:, P * x0 : P * (x0 + w)],
+            )
+
+        def run():
+            for kind, idx, sub, e in SCHEDULE:
+                if kind == "L":
+                    do_load(idx)
+                elif kind == "A":
+                    do_stats(idx)
+                elif kind == "SQ":
+                    b = BATCHES[idx]
+                    nc.scalar.activation(out=sd[:, b[0] : b[-1] + 1], in_=mv[:, b[0] : b[-1] + 1, 1], func=ACT.Sqrt, scale=float(K))
+                elif kind == "RC":
+                    b = BATCHES[idx]
+                    nc.vector.reciprocal(out=inv[:, b[0] : b[-1] + 1], in_=sd[:, b[0] : b[-1] + 1])
+                elif kind == "NM":
+                    b = BATCHES[idx]
+                    nc.gpsimd.tensor_scalar(
+                        out=nm[:, b[0] : b[-1] + 1], in0=mv[:, b[0] : b[-1] + 1, 0], scalar1=-1.0, scalar2=0.0,
+                        op0=ALU.mult, op1=ALU.add,
+                    )
+                elif kind == "B":
+                    do_norm(idx, e)
+                elif kind == "T":
+                    do_transposes(idx)
+                elif kind == "D":
+                    do_regroup(idx, e)
+                elif kind == "Q":
+                    do_quantise(idx, sub)
+                elif kind == "M":
+                    do_matmul(idx)
+                elif kind == "G":
+                    do_out(idx, e)
+                elif kind == "ST":
+                    do_store(idx)
+                else:
+                    raise ValueError(kind)
+
+        if PINNED:
+            with tc.manual_schedule():
+                run()
+        else:
+            run()

@@ -16,7 +16,7 @@ ACT = mybir.ActivationFunctionType
 P = 128
 K = 1024
 ROWS = 1024
-PINNED = False
+PINNED = True
 NF = 8
 NPT = 4
 NPM = 4

@@ -16,7 +16,7 @@ ACT = mybir.ActivationFunctionType
 P = 128
 K = 1024
 ROWS = 1024
-PINNED = True
+PINNED = False
 NF = 8
 NPT = 4
 NPM = 4
@@ -24,79 +24,83 @@ NG = 2
 NO = 16
 
 LOADS = ((0,), (1,), (2,), (3,), (4, 5, 6, 7), (8, 9, 10, 11), (12, 13, 14, 15), (16, 17, 18, 19), (20, 21, 22, 23), (24, 25, 26, 27), (28, 29, 30, 31))
-BATCHES = ((0,), (1,), (2, 3), (4, 5), (6, 7), (8, 9, 10, 11), (12, 13, 14, 15), (16, 17, 18, 19), (20, 21, 22, 23), (24, 25, 26, 27), (28, 29, 30, 31))
-PIECES = ((0,), (1,), (2, 3), (4, 5), (6, 7), (8, 9, 10, 11), (12, 13, 14, 15), (16, 17, 18, 19), (20, 21, 22, 23), (24, 25, 26, 27), (28, 29), (30,), (31,))
-GROUPS = ((0, 0, 0, 1, 0), (0, 1, 0, 2, 1), (0, 0, 1, 1, 1), (0, 2, 0, 4, 2), (0, 3, 0, 4, 2), (0, 0, 2, 2, 2), (0, 1, 2, 2, 2), (0, 4, 0, 4, 3), (0, 4, 4, 2, 3), (0, 5, 0, 4, 3), (0, 5, 4, 2, 3), (0, 0, 4, 2, 3), (0, 1, 4, 2, 3), (0, 2, 4, 2, 3), (0, 3, 4, 2, 3), (0, 6, 0, 4, 4), (0, 6, 4, 4, 4), (0, 7, 0, 4, 4), (0, 7, 4, 4, 4), (0, 0, 6, 2, 4), (0, 1, 6, 2, 4), (0, 2, 6, 2, 4), (0, 3, 6, 2, 4), (0, 4, 6, 2, 4), (0, 5, 6, 2, 4), (1, 0, 0, 4, 5), (1, 1, 0, 4, 5), (1, 2, 0, 4, 5), (1, 3, 0, 4, 5), (1, 4, 0, 4, 6), (1, 4, 4, 4, 6), (1, 5, 0, 4, 6), (1, 5, 4, 4, 6), (1, 6, 0, 4, 6), (1, 6, 4, 4, 6), (1, 7, 0, 4, 6), (1, 7, 4, 4, 6), (1, 0, 4, 4, 6), (1, 1, 4, 4, 6), (1, 2, 4, 4, 6), (1, 3, 4, 4, 6), (2, 0, 0, 4, 7), (2, 1, 0, 4, 7), (2, 2, 0, 4, 7), (2, 3, 0, 4, 7), (2, 4, 0, 4, 8), (2, 4, 4, 4, 8), (2, 5, 0, 4, 8), (2, 5, 4, 4, 8), (2, 6, 0, 4, 8), (2, 6, 4, 4, 8), (2, 7, 0, 4, 8), (2, 7, 4, 4, 8), (2, 0, 4, 4, 8), (2, 1, 4, 4, 8), (2, 2, 4, 4, 8), (2, 3, 4, 4, 8), (3, 0, 0, 4, 9), (3, 1, 0, 4, 9), (3, 2, 0, 4, 9), (3, 3, 0, 4, 9), (3, 4, 0, 4, 10), (3, 4, 4, 2, 10), (3, 5, 0, 4, 10), (3, 5, 4, 2, 10), (3, 0, 4, 2, 10), (3, 1, 4, 2, 10), (3, 2, 4, 2, 10), (3, 3, 4, 2, 10), (3, 6, 0, 4, 11), (3, 6, 4, 2, 11), (3, 6, 6, 1, 11), (3, 0, 6, 1, 11), (3, 1, 6, 1, 11), (3, 2, 6, 1, 11), (3, 3, 6, 1, 11), (3, 4, 6, 1, 11), (3, 5, 6, 1, 11), (3, 7, 0, 4, 12), (3, 7, 4, 4, 12), (3, 0, 7, 1, 12), (3, 1, 7, 1, 12), (3, 2, 7, 1, 12), (3, 3, 7, 1, 12), (3, 4, 7, 1, 12), (3, 5, 7, 1, 12), (3, 6, 7, 1, 12))
-STORES = ((0, 6, 0, 8), (0, 7, 0, 8), (0, 0, 0, 8), (0, 1, 0, 8), (0, 2, 0, 8), (0, 3, 0, 8), (0, 4, 0, 8), (0, 5, 0, 8), (1, 4, 0, 8), (1, 5, 0, 8), (1, 6, 0, 8), (1, 7, 0, 8), (1, 0, 0, 8), (1, 1, 0, 8), (1, 2, 0, 8), (1, 3, 0, 8), (2, 4, 0, 8), (2, 5, 0, 8), (2, 6, 0, 8), (2, 7, 0, 8), (2, 0, 0, 8), (2, 1, 0, 8), (2, 2, 0, 8), (2, 3, 0, 8), (3, 0, 0, 4), (3, 1, 0, 4), (3, 2, 0, 4), (3, 3, 0, 4), (3, 4, 0, 4), (3, 5, 0, 4), (3, 6, 0, 4), (3, 6, 4, 3), (3, 0, 4, 3), (3, 1, 4, 3), (3, 2, 4, 3), (3, 3, 4, 3), (3, 4, 4, 3), (3, 5, 4, 3), (3, 7, 0, 8), (3, 0, 7, 1), (3, 1, 7, 1), (3, 2, 7, 1), (3, 3, 7, 1), (3, 4, 7, 1), (3, 5, 7, 1), (3, 6, 7, 1))
+BATCHES = ((0, 1), (2, 3), (4, 5, 6, 7), (8, 9, 10, 11), (12, 13, 14, 15), (16, 17, 18, 19), (20, 21, 22, 23), (24, 25, 26, 27), (28, 29, 30, 31))
+PIECES = ((0, 1), (2, 3), (4, 5), (6, 7), (8, 9), (10, 11), (12, 13), (14, 15), (16, 17), (18, 19), (20, 21), (22, 23), (24, 25, 26, 27), (28, 29), (30,), (31,))
+GROUPS = ((0, 0, 0, 2, 0), (0, 1, 0, 2, 0), (0, 2, 0, 4, 1), (0, 3, 0, 4, 1), (0, 0, 2, 2, 1), (0, 1, 2, 2, 1), (0, 4, 0, 4, 2), (0, 4, 4, 2, 2), (0, 5, 0, 4, 2), (0, 5, 4, 2, 2), (0, 0, 4, 2, 2), (0, 1, 4, 2, 2), (0, 2, 4, 2, 2), (0, 3, 4, 2, 2), (0, 6, 0, 4, 3), (0, 6, 4, 4, 3), (0, 7, 0, 4, 3), (0, 7, 4, 4, 3), (0, 0, 6, 2, 3), (0, 1, 6, 2, 3), (0, 2, 6, 2, 3), (0, 3, 6, 2, 3), (0, 4, 6, 2, 3), (0, 5, 6, 2, 3), (1, 0, 0, 2, 4), (1, 1, 0, 2, 4), (1, 2, 0, 4, 5), (1, 3, 0, 4, 5), (1, 0, 2, 2, 5), (1, 1, 2, 2, 5), (1, 4, 0, 4, 6), (1, 4, 4, 2, 6), (1, 5, 0, 4, 6), (1, 5, 4, 2, 6), (1, 0, 4, 2, 6), (1, 1, 4, 2, 6), (1, 2, 4, 2, 6), (1, 3, 4, 2, 6), (1, 6, 0, 4, 7), (1, 6, 4, 4, 7), (1, 7, 0, 4, 7), (1, 7, 4, 4, 7), (1, 0, 6, 2, 7), (1, 1, 6, 2, 7), (1, 2, 6, 2, 7), (1, 3, 6, 2, 7), (1, 4, 6, 2, 7), (1, 5, 6, 2, 7), (2, 0, 0, 2, 8), (2, 1, 0, 2, 8), (2, 2, 0, 4, 9), (2, 3, 0, 4, 9), (2, 0, 2, 2, 9), (2, 1, 2, 2, 9), (2, 4, 0, 4, 10), (2, 4, 4, 2, 10), (2, 5, 0, 4, 10), (2, 5, 4, 2, 10), (2, 0, 4, 2, 10), (2, 1, 4, 2, 10), (2, 2, 4, 2, 10), (2, 3, 4, 2, 10), (2, 6, 0, 4, 11), (2, 6, 4, 4, 11), (2, 7, 0, 4, 11), (2, 7, 4, 4, 11), (2, 0, 6, 2, 11), (2, 1, 6, 2, 11), (2, 2, 6, 2, 11), (2, 3, 6, 2, 11), (2, 4, 6, 2, 11), (2, 5, 6, 2, 11), (3, 0, 0, 4, 12), (3, 1, 0, 4, 12), (3, 2, 0, 4, 12), (3, 3, 0, 4, 12), (3, 4, 0, 4, 13), (3, 4, 4, 2, 13), (3, 5, 0, 4, 13), (3, 5, 4, 2, 13), (3, 0, 4, 2, 13), (3, 1, 4, 2, 13), (3, 2, 4, 2, 13), (3, 3, 4, 2, 13), (3, 6, 0, 4, 14), (3, 6, 4, 2, 14), (3, 6, 6, 1, 14), (3, 0, 6, 1, 14), (3, 1, 6, 1, 14), (3, 2, 6, 1, 14), (3, 3, 6, 1, 14), (3, 4, 6, 1, 14), (3, 5, 6, 1, 14), (3, 7, 0, 4, 15), (3, 7, 4, 4, 15), (3, 0, 7, 1, 15), (3, 1, 7, 1, 15), (3, 2, 7, 1, 15), (3, 3, 7, 1, 15), (3, 4, 7, 1, 15), (3, 5, 7, 1, 15), (3, 6, 7, 1, 15))
+STORES = ((0, 6, 0, 8), (0, 7, 0, 8), (0, 0, 0, 8), (0, 1, 0, 8), (0, 2, 0, 8), (0, 3, 0, 8), (0, 4, 0, 8), (0, 5, 0, 8), (1, 6, 0, 8), (1, 7, 0, 8), (1, 0, 0, 8), (1, 1, 0, 8), (1, 2, 0, 8), (1, 3, 0, 8), (1, 4, 0, 8), (1, 5, 0, 8), (2, 6, 0, 8), (2, 7, 0, 8), (2, 0, 0, 8), (2, 1, 0, 8), (2, 2, 0, 8), (2, 3, 0, 8), (2, 4, 0, 8), (2, 5, 0, 8), (3, 0, 0, 4), (3, 1, 0, 4), (3, 2, 0, 4), (3, 3, 0, 4), (3, 4, 0, 4), (3, 5, 0, 4), (3, 6, 0, 4), (3, 6, 4, 3), (3, 0, 4, 3), (3, 1, 4, 3), (3, 2, 4, 3), (3, 3, 4, 3), (3, 4, 4, 3), (3, 5, 4, 3), (3, 7, 0, 8), (3, 0, 7, 1), (3, 1, 7, 1), (3, 2, 7, 1), (3, 3, 7, 1), (3, 4, 7, 1), (3, 5, 7, 1), (3, 6, 7, 1))
 SCHEDULE = (
     ("L", 0, 0, "DMA"), ("L", 1, 0, "DMA"), ("L", 2, 0, "DMA"), ("L", 3, 0, "DMA"), ("L", 4, 0, "DMA"), ("A", 0, 0, "V"),
-    ("A", 1, 0, "V"), ("SQ", 0, 0, "S"), ("L", 5, 0, "DMA"), ("RC", 0, 0, "V"), ("A", 2, 0, "V"), ("SQ", 1, 0, "S"),
-    ("RC", 1, 0, "V"), ("B", 0, 0, "V"), ("B", 1, 0, "V"), ("T", 0, 0, "PE"), ("A", 3, 0, "V"), ("T", 1, 0, "PE"),
-    ("D", 0, 0, "S"), ("L", 6, 0, "DMA"), ("A", 4, 0, "V"), ("NM", 2, 0, "G"), ("SQ", 2, 0, "S"), ("D", 1, 0, "S"),
-    ("RC", 2, 0, "V"), ("Q", 0, 0, "V"), ("B", 2, 0, "G"), ("Q", 0, 1, "V"), ("A", 5, 0, "V"), ("L", 7, 0, "DMA"),
-    ("M", 0, 0, "PE"), ("G", 0, 0, "S"), ("B", 3, 0, "G"), ("Q", 1, 0, "V"), ("T", 2, 0, "PE"), ("SQ", 3, 0, "S"),
-    ("Q", 1, 1, "V"), ("A", 6, 0, "V"), ("M", 1, 0, "PE"), ("D", 2, 0, "S"), ("M", 2, 0, "PE"), ("NM", 3, 0, "G"),
-    ("T", 3, 0, "PE"), ("L", 8, 0, "DMA"), ("RC", 3, 0, "V"), ("A", 7, 0, "V"), ("B", 4, 0, "G"), ("G", 1, 0, "S"),
-    ("D", 3, 0, "S"), ("A", 8, 0, "V"), ("NM", 4, 0, "G"), ("T", 4, 0, "PE"), ("SQ", 4, 0, "S"), ("B", 5, 0, "G"),
-    ("G", 2, 0, "S"), ("D", 4, 0, "S"), ("L", 9, 0, "DMA"), ("RC", 4, 0, "V"), ("Q", 2, 0, "V"), ("Q", 2, 1, "V"),
-    ("B", 6, 0, "G"), ("A", 9, 0, "V"), ("T", 5, 0, "PE"), ("M", 3, 0, "PE"), ("D", 5, 0, "S"), ("A", 10, 0, "V"),
-    ("M", 4, 0, "PE"), ("B", 7, 0, "G"), ("L", 10, 0, "DMA"), ("G", 3, 0, "S"), ("T", 6, 0, "PE"), ("G", 4, 0, "S"),
-    ("Q", 3, 0, "V"), ("T", 7, 0, "PE"), ("Q", 3, 1, "V"), ("D", 6, 0, "S"), ("A", 11, 0, "V"), ("M", 5, 0, "PE"),
-    ("M", 6, 0, "PE"), ("M", 7, 0, "PE"), ("D", 7, 0, "S"), ("A", 12, 0, "V"), ("NM", 5, 0, "G"), ("M", 8, 0, "PE"),
-    ("SQ", 5, 0, "S"), ("G", 5, 0, "S"), ("RC", 5, 0, "V"), ("Q", 4, 0, "V"), ("G", 6, 0, "S"), ("B", 8, 0, "G"),
-    ("M", 9, 0, "PE"), ("Q", 4, 1, "V"), ("G", 7, 0, "S"), ("A", 13, 0, "V"), ("M", 10, 0, "PE"), ("G", 8, 0, "S"),
-    ("M", 11, 0, "PE"), ("G", 9, 0, "S"), ("M", 12, 0, "PE"), ("B", 9, 0, "G"), ("G", 10, 0, "S"), ("A", 14, 0, "V"),
-    ("M", 13, 0, "PE"), ("G", 11, 0, "S"), ("M", 14, 0, "PE"), ("G", 12, 0, "S"), ("M", 15, 0, "PE"), ("G", 13, 0, "S"),
-    ("B", 10, 0, "G"), ("G", 14, 0, "S"), ("M", 16, 0, "PE"), ("A", 15, 0, "V"), ("G", 15, 0, "S"), ("M", 17, 0, "PE"),
-    ("G", 16, 0, "S"), ("B", 11, 0, "G"), ("M", 18, 0, "PE"), ("A", 16, 0, "V"), ("G", 17, 0, "S"), ("ST", 0, 0, "DMA"),
-    ("M", 19, 0, "PE"), ("SQ", 6, 0, "S"), ("M", 20, 0, "PE"), ("G", 18, 0, "S"), ("M", 21, 0, "PE"), ("NM", 6, 0, "G"),
-    ("RC", 6, 0, "V"), ("T", 8, 0, "PE"), ("A", 17, 0, "V"), ("G", 19, 0, "S"), ("ST", 1, 0, "DMA"), ("B", 12, 0, "G"),
-    ("G", 20, 0, "S"), ("T", 9, 0, "PE"), ("G", 21, 0, "S"), ("D", 8, 0, "S"), ("T", 10, 0, "PE"), ("A", 18, 0, "V"),
-    ("ST", 2, 0, "DMA"), ("B", 13, 0, "G"), ("T", 11, 0, "PE"), ("D", 9, 0, "S"), ("T", 12, 0, "PE"), ("A", 19, 0, "V"),
-    ("ST", 3, 0, "DMA"), ("M", 22, 0, "PE"), ("B", 14, 0, "G"), ("M", 23, 0, "PE"), ("D", 10, 0, "S"), ("M", 24, 0, "PE"),
-    ("ST", 4, 0, "DMA"), ("D", 11, 0, "V"), ("T", 13, 0, "PE"), ("NM", 7, 0, "G"), ("SQ", 7, 0, "S"), ("T", 14, 0, "PE"),
-    ("D", 12, 0, "S"), ("B", 15, 0, "G"), ("RC", 7, 0, "V"), ("Q", 5, 0, "V"), ("Q", 5, 1, "V"), ("D", 13, 0, "S"),
-    ("B", 16, 0, "G"), ("T", 15, 0, "PE"), ("D", 14, 0, "V"), ("M", 25, 0, "PE"), ("D", 15, 0, "S"), ("G", 22, 0, "V"),
-    ("B", 17, 0, "G"), ("G", 23, 0, "V"), ("M", 26, 0, "PE"), ("ST", 5, 0, "DMA"), ("A", 20, 0, "V"), ("G", 24, 0, "S"),
-    ("G", 25, 0, "S"), ("M", 27, 0, "PE"), ("B", 18, 0, "G"), ("G", 26, 0, "S"), ("M", 28, 0, "PE"), ("ST", 6, 0, "DMA"),
-    ("Q", 6, 0, "V"), ("G", 27, 0, "S"), ("T", 16, 0, "PE"), ("Q", 6, 1, "V"), ("G", 28, 0, "S"), ("ST", 7, 0, "DMA"),
-    ("B", 19, 0, "G"), ("T", 17, 0, "PE"), ("A", 21, 0, "V"), ("D", 16, 0, "S"), ("T", 18, 0, "PE"), ("T", 19, 0, "PE"),
-    ("A", 22, 0, "V"), ("D", 17, 0, "S"), ("M", 29, 0, "PE"), ("D", 18, 0, "S"), ("M", 30, 0, "PE"), ("A", 23, 0, "V"),
-    ("M", 31, 0, "PE"), ("D", 19, 0, "S"), ("M", 32, 0, "PE"), ("G", 29, 0, "V"), ("NM", 8, 0, "G"), ("G", 30, 0, "V"),
-    ("M", 33, 0, "PE"), ("SQ", 8, 0, "S"), ("G", 31, 0, "S"), ("Q", 7, 0, "V"), ("M", 34, 0, "PE"), ("ST", 8, 0, "DMA"),
-    ("G", 32, 0, "S"), ("RC", 8, 0, "V"), ("M", 35, 0, "PE"), ("Q", 7, 1, "V"), ("B", 20, 0, "G"), ("G", 33, 0, "S"),
-    ("M", 36, 0, "PE"), ("ST", 9, 0, "DMA"), ("A", 24, 0, "V"), ("G", 34, 0, "S"), ("M", 37, 0, "PE"), ("B", 21, 0, "G"),
-    ("G", 35, 0, "S"), ("M", 38, 0, "PE"), ("ST", 10, 0, "DMA"), ("A", 25, 0, "V"), ("G", 36, 0, "S"), ("M", 39, 0, "PE"),
-    ("G", 37, 0, "S"), ("B", 22, 0, "G"), ("M", 40, 0, "PE"), ("ST", 11, 0, "DMA"), ("A", 26, 0, "V"), ("G", 38, 0, "S"),
-    ("M", 41, 0, "PE"), ("G", 39, 0, "S"), ("M", 42, 0, "PE"), ("ST", 12, 0, "DMA"), ("B", 23, 0, "G"), ("A", 27, 0, "V"),
-    ("G", 40, 0, "S"), ("M", 43, 0, "PE"), ("G", 41, 0, "S"), ("M", 44, 0, "PE"), ("ST", 13, 0, "DMA"), ("A", 28, 0, "V"),
-    ("G", 42, 0, "S"), ("NM", 9, 0, "G"), ("T", 20, 0, "PE"), ("SQ", 9, 0, "S"), ("G", 43, 0, "S"), ("T", 21, 0, "PE"),
-    ("ST", 14, 0, "DMA"), ("RC", 9, 0, "V"), ("A", 29, 0, "V"), ("T", 22, 0, "PE"), ("D", 20, 0, "S"), ("B", 24, 0, "G"),
-    ("T", 23, 0, "PE"), ("ST", 15, 0, "DMA"), ("D", 21, 0, "S"), ("D", 22, 0, "V"), ("B", 25, 0, "G"), ("T", 24, 0, "PE"),
-    ("D", 23, 0, "S"), ("A", 30, 0, "V"), ("B", 26, 0, "G"), ("T", 25, 0, "PE"), ("D", 24, 0, "S"), ("Q", 8, 0, "V"),
-    ("B", 27, 0, "G"), ("Q", 8, 1, "V"), ("T", 26, 0, "PE"), ("D", 25, 0, "S"), ("A", 31, 0, "V"), ("M", 45, 0, "PE"),
-    ("D", 26, 0, "S"), ("T", 27, 0, "PE"), ("M", 46, 0, "PE"), ("D", 27, 0, "V"), ("SQ", 10, 0, "S"), ("G", 44, 0, "S"),
-    ("M", 47, 0, "PE"), ("G", 45, 0, "S"), ("RC", 10, 0, "V"), ("M", 48, 0, "PE"), ("Q", 9, 0, "V"), ("G", 46, 0, "S"),
-    ("M", 49, 0, "PE"), ("Q", 9, 1, "V"), ("G", 47, 0, "S"), ("ST", 16, 0, "DMA"), ("M", 50, 0, "PE"), ("B", 28, 0, "V"),
-    ("G", 48, 0, "S"), ("B", 29, 0, "V"), ("T", 28, 0, "PE"), ("B", 30, 0, "V"), ("G", 49, 0, "S"), ("ST", 17, 0, "DMA"),
-    ("B", 31, 0, "V"), ("T", 29, 0, "PE"), ("D", 28, 0, "S"), ("T", 30, 0, "PE"), ("T", 31, 0, "PE"), ("D", 29, 0, "V"),
-    ("D", 30, 0, "S"), ("M", 51, 0, "PE"), ("M", 52, 0, "PE"), ("Q", 10, 0, "V"), ("G", 50, 0, "S"), ("Q", 10, 1, "V"),
-    ("M", 53, 0, "PE"), ("Q", 11, 0, "V"), ("G", 51, 0, "S"), ("Q", 11, 1, "V"), ("ST", 18, 0, "DMA"), ("M", 54, 0, "PE"),
-    ("D", 31, 0, "V"), ("G", 52, 0, "S"), ("M", 55, 0, "PE"), ("G", 53, 0, "S"), ("ST", 19, 0, "DMA"), ("M", 56, 0, "PE"),
-    ("Q", 12, 0, "V"), ("G", 54, 0, "S"), ("Q", 12, 1, "V"), ("M", 57, 0, "PE"), ("G", 55, 0, "S"), ("ST", 20, 0, "DMA"),
-    ("M", 58, 0, "PE"), ("G", 56, 0, "S"), ("M", 59, 0, "PE"), ("G", 57, 0, "S"), ("ST", 21, 0, "DMA"), ("M", 60, 0, "PE"),
-    ("G", 58, 0, "S"), ("M", 61, 0, "PE"), ("G", 59, 0, "S"), ("ST", 22, 0, "DMA"), ("M", 62, 0, "PE"), ("G", 60, 0, "S"),
-    ("M", 63, 0, "PE"), ("G", 61, 0, "S"), ("M", 64, 0, "PE"), ("ST", 23, 0, "DMA"), ("G", 62, 0, "V"), ("G", 63, 0, "S"),
-    ("M", 65, 0, "PE"), ("M", 66, 0, "PE"), ("G", 64, 0, "S"), ("M", 67, 0, "PE"), ("ST", 24, 0, "DMA"), ("G", 65, 0, "S"),
-    ("M", 68, 0, "PE"), ("G", 66, 0, "S"), ("M", 69, 0, "PE"), ("ST", 25, 0, "DMA"), ("G", 67, 0, "S"), ("G", 68, 0, "S"),
-    ("M", 70, 0, "PE"), ("ST", 26, 0, "DMA"), ("G", 69, 0, "S"), ("M", 71, 0, "PE"), ("M", 72, 0, "PE"), ("G", 70, 0, "V"),
-    ("G", 71, 0, "S"), ("ST", 27, 0, "DMA"), ("M", 73, 0, "PE"), ("G", 72, 0, "S"), ("M", 75, 0, "PE"), ("G", 73, 0, "S"),
-    ("M", 74, 0, "PE"), ("G", 75, 0, "S"), ("M", 76, 0, "PE"), ("ST", 28, 0, "DMA"), ("G", 74, 0, "S"), ("M", 77, 0, "PE"),
-    ("G", 76, 0, "S"), ("M", 79, 0, "PE"), ("G", 77, 0, "S"), ("ST", 29, 0, "DMA"), ("M", 78, 0, "PE"), ("G", 79, 0, "S"),
-    ("ST", 30, 0, "DMA"), ("M", 80, 0, "PE"), ("G", 78, 0, "S"), ("M", 81, 0, "PE"), ("M", 83, 0, "PE"), ("ST", 31, 0, "DMA"),
-    ("G", 80, 0, "V"), ("G", 81, 0, "S"), ("M", 82, 0, "PE"), ("G", 83, 0, "S"), ("M", 84, 0, "PE"), ("ST", 32, 0, "DMA"),
-    ("G", 82, 0, "S"), ("M", 85, 0, "PE"), ("G", 84, 0, "S"), ("M", 86, 0, "PE"), ("G", 85, 0, "S"), ("G", 86, 0, "S"),
-    ("ST", 33, 0, "DMA"), ("ST", 34, 0, "DMA"), ("ST", 35, 0, "DMA"), ("ST", 36, 0, "DMA"), ("ST", 37, 0, "DMA"), ("ST", 38, 0, "DMA"),
+    ("A", 1, 0, "V"), ("L", 5, 0, "DMA"), ("A", 2, 0, "V"), ("SQ", 0, 0, "S"), ("RC", 0, 0, "V"), ("A", 3, 0, "V"),
+    ("L", 6, 0, "DMA"), ("B", 0, 0, "V"), ("SQ", 1, 0, "S"), ("B", 1, 0, "V"), ("T", 0, 0, "PE"), ("RC", 1, 0, "V"),
+    ("A", 4, 0, "V"), ("T", 1, 0, "PE"), ("D", 0, 0, "S"), ("B", 2, 0, "V"), ("D", 1, 0, "S"), ("B", 3, 0, "V"),
+    ("T", 2, 0, "PE"), ("L", 7, 0, "DMA"), ("A", 5, 0, "V"), ("T", 3, 0, "PE"), ("D", 2, 0, "S"), ("Q", 0, 0, "V"),
+    ("Q", 0, 1, "V"), ("D", 3, 0, "S"), ("A", 6, 0, "V"), ("M", 0, 0, "PE"), ("L", 8, 0, "DMA"), ("M", 1, 0, "PE"),
+    ("G", 0, 0, "S"), ("Q", 1, 0, "V"), ("G", 1, 0, "S"), ("Q", 1, 1, "V"), ("A", 7, 0, "V"), ("M", 2, 0, "PE"),
+    ("M", 3, 0, "PE"), ("G", 2, 0, "S"), ("A", 8, 0, "V"), ("L", 9, 0, "DMA"), ("M", 4, 0, "PE"), ("SQ", 2, 0, "S"),
+    ("M", 5, 0, "PE"), ("G", 3, 0, "S"), ("G", 4, 0, "S"), ("RC", 2, 0, "V"), ("A", 9, 0, "V"), ("G", 5, 0, "S"),
+    ("B", 4, 0, "V"), ("L", 10, 0, "DMA"), ("B", 5, 0, "V"), ("T", 4, 0, "PE"), ("B", 6, 0, "V"), ("B", 7, 0, "V"),
+    ("T", 5, 0, "PE"), ("D", 4, 0, "S"), ("A", 10, 0, "V"), ("T", 6, 0, "PE"), ("T", 7, 0, "PE"), ("D", 5, 0, "S"),
+    ("A", 11, 0, "V"), ("D", 6, 0, "S"), ("Q", 2, 0, "V"), ("Q", 2, 1, "V"), ("A", 12, 0, "V"), ("SQ", 3, 0, "S"),
+    ("M", 6, 0, "PE"), ("D", 7, 0, "S"), ("M", 7, 0, "PE"), ("RC", 3, 0, "V"), ("M", 8, 0, "PE"), ("A", 13, 0, "V"),
+    ("G", 6, 0, "S"), ("M", 9, 0, "PE"), ("G", 7, 0, "S"), ("M", 10, 0, "PE"), ("G", 8, 0, "S"), ("M", 11, 0, "PE"),
+    ("Q", 3, 0, "V"), ("Q", 3, 1, "V"), ("G", 9, 0, "S"), ("M", 12, 0, "PE"), ("B", 8, 0, "V"), ("G", 10, 0, "S"),
+    ("M", 13, 0, "PE"), ("B", 9, 0, "V"), ("G", 11, 0, "S"), ("M", 14, 0, "PE"), ("B", 10, 0, "V"), ("G", 12, 0, "S"),
+    ("B", 11, 0, "V"), ("G", 13, 0, "S"), ("M", 15, 0, "PE"), ("G", 14, 0, "S"), ("A", 14, 0, "V"), ("T", 8, 0, "PE"),
+    ("G", 15, 0, "S"), ("T", 9, 0, "PE"), ("D", 8, 0, "S"), ("ST", 0, 0, "DMA"), ("A", 15, 0, "V"), ("T", 10, 0, "PE"),
+    ("T", 11, 0, "PE"), ("D", 9, 0, "S"), ("A", 16, 0, "V"), ("M", 16, 0, "PE"), ("M", 17, 0, "PE"), ("SQ", 4, 0, "S"),
+    ("D", 10, 0, "S"), ("RC", 4, 0, "V"), ("D", 11, 0, "V"), ("M", 18, 0, "PE"), ("M", 19, 0, "PE"), ("G", 16, 0, "S"),
+    ("Q", 4, 0, "V"), ("Q", 4, 1, "V"), ("G", 17, 0, "S"), ("M", 20, 0, "PE"), ("Q", 5, 0, "V"), ("G", 18, 0, "S"),
+    ("Q", 5, 1, "V"), ("M", 21, 0, "PE"), ("ST", 1, 0, "DMA"), ("G", 19, 0, "S"), ("B", 12, 0, "V"), ("M", 22, 0, "PE"),
+    ("G", 20, 0, "S"), ("B", 13, 0, "V"), ("M", 23, 0, "PE"), ("G", 21, 0, "S"), ("B", 14, 0, "V"), ("M", 24, 0, "PE"),
+    ("G", 22, 0, "S"), ("ST", 2, 0, "DMA"), ("B", 15, 0, "V"), ("M", 25, 0, "PE"), ("G", 23, 0, "S"), ("T", 12, 0, "PE"),
+    ("A", 17, 0, "V"), ("G", 24, 0, "S"), ("G", 25, 0, "S"), ("T", 13, 0, "PE"), ("D", 12, 0, "S"), ("ST", 3, 0, "DMA"),
+    ("T", 14, 0, "PE"), ("A", 18, 0, "V"), ("T", 15, 0, "PE"), ("D", 13, 0, "S"), ("ST", 4, 0, "DMA"), ("M", 26, 0, "PE"),
+    ("D", 14, 0, "V"), ("M", 27, 0, "PE"), ("D", 15, 0, "S"), ("ST", 5, 0, "DMA"), ("M", 28, 0, "PE"), ("Q", 6, 0, "V"),
+    ("M", 29, 0, "PE"), ("Q", 6, 1, "V"), ("G", 26, 0, "S"), ("A", 19, 0, "V"), ("ST", 6, 0, "DMA"), ("G", 27, 0, "S"),
+    ("M", 30, 0, "PE"), ("G", 28, 0, "S"), ("M", 31, 0, "PE"), ("Q", 7, 0, "V"), ("ST", 7, 0, "DMA"), ("SQ", 5, 0, "S"),
+    ("M", 32, 0, "PE"), ("G", 29, 0, "S"), ("Q", 7, 1, "V"), ("G", 30, 0, "S"), ("RC", 5, 0, "V"), ("A", 20, 0, "V"),
+    ("M", 33, 0, "PE"), ("G", 31, 0, "S"), ("M", 34, 0, "PE"), ("G", 32, 0, "S"), ("M", 35, 0, "PE"), ("B", 16, 0, "V"),
+    ("G", 33, 0, "S"), ("M", 36, 0, "PE"), ("B", 17, 0, "V"), ("G", 34, 0, "S"), ("M", 37, 0, "PE"), ("B", 18, 0, "V"),
+    ("G", 35, 0, "S"), ("M", 38, 0, "PE"), ("B", 19, 0, "V"), ("G", 36, 0, "S"), ("A", 21, 0, "V"), ("G", 37, 0, "S"),
+    ("T", 16, 0, "PE"), ("G", 38, 0, "S"), ("T", 17, 0, "PE"), ("D", 16, 0, "S"), ("A", 22, 0, "V"), ("T", 18, 0, "PE"),
+    ("T", 19, 0, "PE"), ("D", 17, 0, "S"), ("M", 39, 0, "PE"), ("A", 23, 0, "V"), ("M", 40, 0, "PE"), ("D", 18, 0, "S"),
+    ("M", 41, 0, "PE"), ("D", 19, 0, "V"), ("M", 42, 0, "PE"), ("SQ", 6, 0, "S"), ("G", 39, 0, "S"), ("RC", 6, 0, "V"),
+    ("Q", 8, 0, "V"), ("G", 40, 0, "S"), ("M", 43, 0, "PE"), ("ST", 8, 0, "DMA"), ("Q", 8, 1, "V"), ("Q", 9, 0, "V"),
+    ("G", 41, 0, "S"), ("M", 44, 0, "PE"), ("Q", 9, 1, "V"), ("G", 42, 0, "S"), ("B", 20, 0, "V"), ("M", 45, 0, "PE"),
+    ("ST", 9, 0, "DMA"), ("G", 43, 0, "S"), ("B", 21, 0, "V"), ("M", 46, 0, "PE"), ("G", 44, 0, "S"), ("B", 22, 0, "V"),
+    ("M", 47, 0, "PE"), ("G", 45, 0, "S"), ("B", 23, 0, "V"), ("M", 48, 0, "PE"), ("G", 46, 0, "S"), ("T", 20, 0, "PE"),
+    ("A", 24, 0, "V"), ("ST", 10, 0, "DMA"), ("G", 47, 0, "S"), ("G", 48, 0, "S"), ("T", 21, 0, "PE"), ("D", 20, 0, "S"),
+    ("ST", 11, 0, "DMA"), ("T", 22, 0, "PE"), ("A", 25, 0, "V"), ("T", 23, 0, "PE"), ("D", 21, 0, "S"), ("M", 49, 0, "PE"),
+    ("ST", 12, 0, "DMA"), ("D", 22, 0, "V"), ("M", 50, 0, "PE"), ("D", 23, 0, "S"), ("M", 51, 0, "PE"), ("ST", 13, 0, "DMA"),
+    ("Q", 10, 0, "V"), ("M", 52, 0, "PE"), ("Q", 10, 1, "V"), ("G", 49, 0, "S"), ("A", 26, 0, "V"), ("G", 50, 0, "S"),
+    ("M", 53, 0, "PE"), ("ST", 14, 0, "DMA"), ("G", 51, 0, "S"), ("M", 54, 0, "PE"), ("Q", 11, 0, "V"), ("G", 52, 0, "S"),
+    ("M", 55, 0, "PE"), ("Q", 11, 1, "V"), ("ST", 15, 0, "DMA"), ("G", 53, 0, "S"), ("M", 56, 0, "PE"), ("A", 27, 0, "V"),
+    ("G", 54, 0, "S"), ("M", 57, 0, "PE"), ("G", 55, 0, "S"), ("M", 58, 0, "PE"), ("G", 56, 0, "S"), ("M", 59, 0, "PE"),
+    ("A", 28, 0, "V"), ("SQ", 7, 0, "S"), ("M", 60, 0, "PE"), ("G", 57, 0, "S"), ("G", 58, 0, "S"), ("M", 61, 0, "PE"),
+    ("G", 59, 0, "S"), ("M", 62, 0, "PE"), ("RC", 7, 0, "V"), ("A", 29, 0, "V"), ("G", 60, 0, "S"), ("G", 61, 0, "S"),
+    ("M", 63, 0, "PE"), ("G", 62, 0, "S"), ("M", 64, 0, "PE"), ("G", 63, 0, "S"), ("B", 24, 0, "V"), ("B", 25, 0, "V"),
+    ("M", 65, 0, "PE"), ("G", 64, 0, "S"), ("B", 26, 0, "V"), ("ST", 16, 0, "DMA"), ("M", 66, 0, "PE"), ("B", 27, 0, "V"),
+    ("G", 65, 0, "S"), ("T", 24, 0, "PE"), ("A", 30, 0, "V"), ("G", 66, 0, "S"), ("ST", 17, 0, "DMA"), ("T", 25, 0, "PE"),
+    ("D", 24, 0, "S"), ("T", 26, 0, "PE"), ("A", 31, 0, "V"), ("T", 27, 0, "PE"), ("ST", 18, 0, "DMA"), ("D", 25, 0, "S"),
+    ("M", 67, 0, "PE"), ("D", 26, 0, "V"), ("M", 68, 0, "PE"), ("M", 69, 0, "PE"), ("SQ", 8, 0, "S"), ("D", 27, 0, "S"),
+    ("M", 70, 0, "PE"), ("RC", 8, 0, "V"), ("G", 67, 0, "V"), ("B", 28, 0, "V"), ("M", 71, 0, "PE"), ("ST", 19, 0, "DMA"),
+    ("G", 68, 0, "S"), ("B", 29, 0, "V"), ("T", 28, 0, "PE"), ("G", 69, 0, "S"), ("Q", 12, 0, "V"), ("G", 70, 0, "S"),
+    ("T", 29, 0, "PE"), ("G", 71, 0, "S"), ("Q", 12, 1, "V"), ("ST", 20, 0, "DMA"), ("D", 28, 0, "S"), ("B", 30, 0, "V"),
+    ("B", 31, 0, "V"), ("T", 30, 0, "PE"), ("ST", 21, 0, "DMA"), ("D", 29, 0, "S"), ("T", 31, 0, "PE"), ("M", 72, 0, "PE"),
+    ("ST", 22, 0, "DMA"), ("D", 30, 0, "S"), ("Q", 13, 0, "V"), ("M", 73, 0, "PE"), ("Q", 13, 1, "V"), ("M", 74, 0, "PE"),
+    ("D", 31, 0, "V"), ("ST", 23, 0, "DMA"), ("G", 72, 0, "S"), ("M", 75, 0, "PE"), ("G", 73, 0, "S"), ("M", 76, 0, "PE"),
+    ("Q", 14, 0, "V"), ("ST", 24, 0, "DMA"), ("G", 74, 0, "S"), ("Q", 14, 1, "V"), ("Q", 15, 0, "V"), ("M", 77, 0, "PE"),
+    ("Q", 15, 1, "V"), ("G", 75, 0, "V"), ("ST", 25, 0, "DMA"), ("G", 76, 0, "S"), ("M", 78, 0, "PE"), ("G", 77, 0, "S"),
+    ("ST", 26, 0, "DMA"), ("M", 79, 0, "PE"), ("G", 78, 0, "S"), ("M", 80, 0, "PE"), ("ST", 27, 0, "DMA"), ("M", 81, 0, "PE"),
+    ("G", 79, 0, "V"), ("G", 80, 0, "S"), ("M", 82, 0, "PE"), ("G", 81, 0, "S"), ("M", 83, 0, "PE"), ("ST", 28, 0, "DMA"),
+    ("G", 82, 0, "S"), ("M", 84, 0, "PE"), ("G", 83, 0, "S"), ("ST", 29, 0, "DMA"), ("M", 85, 0, "PE"), ("G", 84, 0, "S"),
+    ("M", 86, 0, "PE"), ("M", 87, 0, "PE"), ("G", 85, 0, "V"), ("G", 86, 0, "S"), ("M", 88, 0, "PE"), ("ST", 30, 0, "DMA"),
+    ("G", 87, 0, "S"), ("M", 90, 0, "PE"), ("G", 88, 0, "S"), ("M", 89, 0, "PE"), ("G", 90, 0, "S"), ("M", 91, 0, "PE"),
+    ("G", 89, 0, "S"), ("ST", 31, 0, "DMA"), ("M", 92, 0, "PE"), ("G", 91, 0, "S"), ("M", 94, 0, "PE"), ("G", 92, 0, "S"),
+    ("ST", 32, 0, "DMA"), ("M", 93, 0, "PE"), ("G", 94, 0, "S"), ("ST", 33, 0, "DMA"), ("M", 95, 0, "PE"), ("G", 93, 0, "S"),
+    ("M", 96, 0, "PE"), ("M", 98, 0, "PE"), ("ST", 34, 0, "DMA"), ("G", 95, 0, "V"), ("G", 96, 0, "V"), ("G", 98, 0, "S"),
+    ("M", 99, 0, "PE"), ("M", 97, 0, "PE"), ("ST", 35, 0, "DMA"), ("G", 99, 0, "S"), ("M", 100, 0, "PE"), ("G", 97, 0, "S"),
+    ("G", 100, 0, "S"), ("M", 101, 0, "PE"), ("ST", 36, 0, "DMA"), ("G", 101, 0, "S"), ("ST", 37, 0, "DMA"), ("ST", 38, 0, "DMA"),
     ("ST", 39, 0, "DMA"), ("ST", 40, 0, "DMA"), ("ST", 41, 0, "DMA"), ("ST", 42, 0, "DMA"), ("ST", 43, 0, "DMA"), ("ST", 44, 0, "DMA"),
     ("ST", 45, 0, "DMA"),
 )

@@ -16,93 +16,86 @@ ACT = mybir.ActivationFunctionType
 P = 128
 K = 1024
 ROWS = 1024
-PINNED = False
+PINNED = True
 NF = 8
-NPT = 4
-NPM = 4
+NPT = 3
+NPM = 5
 NG = 2
 NO = 16
 
 LOADS = ((0,), (1,), (2,), (3,), (4, 5, 6, 7), (8, 9, 10, 11), (12, 13, 14, 15), (16, 17, 18, 19), (20, 21, 22, 23), (24, 25, 26, 27), (28, 29, 30, 31))
-BATCHES = ((0, 1), (2, 3), (4, 5, 6, 7), (8, 9, 10, 11), (12, 13, 14, 15), (16, 17, 18, 19), (20, 21, 22, 23), (24, 25, 26, 27), (28, 29, 30, 31))
-PIECES = ((0, 1), (2, 3), (4, 5), (6, 7), (8, 9), (10, 11), (12, 13), (14, 15), (16, 17), (18, 19), (20, 21), (22, 23), (24, 25, 26, 27), (28, 29), (30,), (31,))
-GROUPS = ((0, 0, 0, 2, 0), (0, 1, 0, 2, 0), (0, 2, 0, 4, 1), (0, 3, 0, 4, 1), (0, 0, 2, 2, 1), (0, 1, 2, 2, 1), (0, 4, 0, 4, 2), (0, 4, 4, 2, 2), (0, 5, 0, 4, 2), (0, 5, 4, 2, 2), (0, 0, 4, 2, 2), (0, 1, 4, 2, 2), (0, 2, 4, 2, 2), (0, 3, 4, 2, 2), (0, 6, 0, 4, 3), (0, 6, 4, 4, 3), (0, 7, 0, 4, 3), (0, 7, 4, 4, 3), (0, 0, 6, 2, 3), (0, 1, 6, 2, 3), (0, 2, 6, 2, 3), (0, 3, 6, 2, 3), (0, 4, 6, 2, 3), (0, 5, 6, 2, 3), (1, 0, 0, 2, 4), (1, 1, 0, 2, 4), (1, 2, 0, 4, 5), (1, 3, 0, 4, 5), (1, 0, 2, 2, 5), (1, 1, 2, 2, 5), (1, 4, 0, 4, 6), (1, 4, 4, 2, 6), (1, 5, 0, 4, 6), (1, 5, 4, 2, 6), (1, 0, 4, 2, 6), (1, 1, 4, 2, 6), (1, 2, 4, 2, 6), (1, 3, 4, 2, 6), (1, 6, 0, 4, 7), (1, 6, 4, 4, 7), (1, 7, 0, 4, 7), (1, 7, 4, 4, 7), (1, 0, 6, 2, 7), (1, 1, 6, 2, 7), (1, 2, 6, 2, 7), (1, 3, 6, 2, 7), (1, 4, 6, 2, 7), (1, 5, 6, 2, 7), (2, 0, 0, 2, 8), (2, 1, 0, 2, 8), (2, 2, 0, 4, 9), (2, 3, 0, 4, 9), (2, 0, 2, 2, 9), (2, 1, 2, 2, 9), (2, 4, 0, 4, 10), (2, 4, 4, 2, 10), (2, 5, 0, 4, 10), (2, 5, 4, 2, 10), (2, 0, 4, 2, 10), (2, 1, 4, 2, 10), (2, 2, 4, 2, 10), (2, 3, 4, 2, 10), (2, 6, 0, 4, 11), (2, 6, 4, 4, 11), (2, 7, 0, 4, 11), (2, 7, 4, 4, 11), (2, 0, 6, 2, 11), (2, 1, 6, 2, 11), (2, 2, 6, 2, 11), (2, 3, 6, 2, 11), (2, 4, 6, 2, 11), (2, 5, 6, 2, 11), (3, 0, 0, 4, 12), (3, 1, 0, 4, 12), (3, 2, 0, 4, 12), (3, 3, 0, 4, 12), (3, 4, 0, 4, 13), (3, 4, 4, 2, 13), (3, 5, 0, 4, 13), (3, 5, 4, 2, 13), (3, 0, 4, 2, 13), (3, 1, 4, 2, 13), (3, 2, 4, 2, 13), (3, 3, 4, 2, 13), (3, 6, 0, 4, 14), (3, 6, 4, 2, 14), (3, 6, 6, 1, 14), (3, 0, 6, 1, 14), (3, 1, 6, 1, 14), (3, 2, 6, 1, 14), (3, 3, 6, 1, 14), (3, 4, 6, 1, 14), (3, 5, 6, 1, 14), (3, 7, 0, 4, 15), (3, 7, 4, 4, 15), (3, 0, 7, 1, 15), (3, 1, 7, 1, 15), (3, 2, 7, 1, 15), (3, 3, 7, 1, 15), (3, 4, 7, 1, 15), (3, 5, 7, 1, 15), (3, 6, 7, 1, 15))
-STORES = ((0, 6, 0, 8), (0, 7, 0, 8), (0, 0, 0, 8), (0, 1, 0, 8), (0, 2, 0, 8), (0, 3, 0, 8), (0, 4, 0, 8), (0, 5, 0, 8), (1, 6, 0, 8), (1, 7, 0, 8), (1, 0, 0, 8), (1, 1, 0, 8), (1, 2, 0, 8), (1, 3, 0, 8), (1, 4, 0, 8), (1, 5, 0, 8), (2, 6, 0, 8), (2, 7, 0, 8), (2, 0, 0, 8), (2, 1, 0, 8), (2, 2, 0, 8), (2, 3, 0, 8), (2, 4, 0, 8), (2, 5, 0, 8), (3, 0, 0, 4), (3, 1, 0, 4), (3, 2, 0, 4), (3, 3, 0, 4), (3, 4, 0, 4), (3, 5, 0, 4), (3, 6, 0, 4), (3, 6, 4, 3), (3, 0, 4, 3), (3, 1, 4, 3), (3, 2, 4, 3), (3, 3, 4, 3), (3, 4, 4, 3), (3, 5, 4, 3), (3, 7, 0, 8), (3, 0, 7, 1), (3, 1, 7, 1), (3, 2, 7, 1), (3, 3, 7, 1), (3, 4, 7, 1), (3, 5, 7, 1), (3, 6, 7, 1))
+BATCHES = ((0,), (1,), (2, 3), (4, 5), (6, 7), (8, 9), (10, 11), (12, 13), (14, 15), (16, 17), (18, 19), (20, 21), (22, 23), (24, 25), (26, 27), (28, 29), (30, 31))
+PIECES = ((0, 1), (2, 3), (4, 5, 6, 7), (8, 9, 10, 11), (12, 13, 14, 15), (16, 17, 18, 19), (20, 21, 22, 23), (24, 25, 26, 27), (28, 29), (30,), (31,))
+GROUPS = ((0, 0, 0, 2, 0), (0, 1, 0, 2, 0), (0, 2, 0, 4, 1), (0, 3, 0, 4, 1), (0, 0, 2, 2, 1), (0, 1, 2, 2, 1), (0, 4, 0, 4, 2), (0, 4, 4, 4, 2), (0, 5, 0, 4, 2), (0, 5, 4, 4, 2), (0, 6, 0, 4, 2), (0, 6, 4, 4, 2), (0, 7, 0, 4, 2), (0, 7, 4, 4, 2), (0, 0, 4, 4, 2), (0, 1, 4, 4, 2), (0, 2, 4, 4, 2), (0, 3, 4, 4, 2), (1, 0, 0, 4, 3), (1, 1, 0, 4, 3), (1, 2, 0, 4, 3), (1, 3, 0, 4, 3), (1, 4, 0, 4, 4), (1, 4, 4, 4, 4), (1, 5, 0, 4, 4), (1, 5, 4, 4, 4), (1, 6, 0, 4, 4), (1, 6, 4, 4, 4), (1, 7, 0, 4, 4), (1, 7, 4, 4, 4), (1, 0, 4, 4, 4), (1, 1, 4, 4, 4), (1, 2, 4, 4, 4), (1, 3, 4, 4, 4), (2, 0, 0, 4, 5), (2, 1, 0, 4, 5), (2, 2, 0, 4, 5), (2, 3, 0, 4, 5), (2, 4, 0, 4, 6), (2, 4, 4, 4, 6), (2, 5, 0, 4, 6), (2, 5, 4, 4, 6), (2, 6, 0, 4, 6), (2, 6, 4, 4, 6), (2, 7, 0, 4, 6), (2, 7, 4, 4, 6), (2, 0, 4, 4, 6), (2, 1, 4, 4, 6), (2, 2, 4, 4, 6), (2, 3, 4, 4, 6), (3, 0, 0, 4, 7), (3, 1, 0, 4, 7), (3, 2, 0, 4, 7), (3, 3, 0, 4, 7), (3, 4, 0, 4, 8), (3, 4, 4, 2, 8), (3, 5, 0, 4, 8), (3, 5, 4, 2, 8), (3, 0, 4, 2, 8), (3, 1, 4, 2, 8), (3, 2, 4, 2, 8), (3, 3, 4, 2, 8), (3, 6, 0, 4, 9), (3, 6, 4, 2, 9), (3, 6, 6, 1, 9), (3, 0, 6, 1, 9), (3, 1, 6, 1, 9), (3, 2, 6, 1, 9), (3, 3, 6, 1, 9), (3, 4, 6, 1, 9), (3, 5, 6, 1, 9), (3, 7, 0, 4, 10), (3, 7, 4, 4, 10), (3, 0, 7, 1, 10), (3, 1, 7, 1, 10), (3, 2, 7, 1, 10), (3, 3, 7, 1, 10), (3, 4, 7, 1, 10), (3, 5, 7, 1, 10), (3, 6, 7, 1, 10))
+STORES = ((0, 4, 0, 8), (0, 5, 0, 8), (0, 6, 0, 8), (0, 7, 0, 8), (0, 0, 0, 8), (0, 1, 0, 8), (0, 2, 0, 8), (0, 3, 0, 8), (1, 4, 0, 8), (1, 5, 0, 8), (1, 6, 0, 8), (1, 7, 0, 8), (1, 0, 0, 8), (1, 1, 0, 8), (1, 2, 0, 8), (1, 3, 0, 8), (2, 4, 0, 8), (2, 5, 0, 8), (2, 6, 0, 8), (2, 7, 0, 8), (2, 0, 0, 8), (2, 1, 0, 8), (2, 2, 0, 8), (2, 3, 0, 8), (3, 0, 0, 4), (3, 1, 0, 4), (3, 2, 0, 4), (3, 3, 0, 4), (3, 4, 0, 4), (3, 5, 0, 4), (3, 6, 0, 4), (3, 6, 4, 3), (3, 0, 4, 3), (3, 1, 4, 3), (3, 2, 4, 3), (3, 3, 4, 3), (3, 4, 4, 3), (3, 5, 4, 3), (3, 7, 0, 8), (3, 0, 7, 1), (3, 1, 7, 1), (3, 2, 7, 1), (3, 3, 7, 1), (3, 4, 7, 1), (3, 5, 7, 1), (3, 6, 7, 1))
 SCHEDULE = (
     ("L", 0, 0, "DMA"), ("L", 1, 0, "DMA"), ("L", 2, 0, "DMA"), ("L", 3, 0, "DMA"), ("L", 4, 0, "DMA"), ("A", 0, 0, "V"),
-    ("A", 1, 0, "V"), ("L", 5, 0, "DMA"), ("A", 2, 0, "V"), ("SQ", 0, 0, "S"), ("RC", 0, 0, "V"), ("A", 3, 0, "V"),
-    ("L", 6, 0, "DMA"), ("B", 0, 0, "V"), ("SQ", 1, 0, "S"), ("B", 1, 0, "V"), ("T", 0, 0, "PE"), ("RC", 1, 0, "V"),
-    ("A", 4, 0, "V"), ("T", 1, 0, "PE"), ("D", 0, 0, "S"), ("B", 2, 0, "V"), ("D", 1, 0, "S"), ("B", 3, 0, "V"),
-    ("T", 2, 0, "PE"), ("L", 7, 0, "DMA"), ("A", 5, 0, "V"), ("T", 3, 0, "PE"), ("D", 2, 0, "S"), ("Q", 0, 0, "V"),
-    ("Q", 0, 1, "V"), ("D", 3, 0, "S"), ("A", 6, 0, "V"), ("M", 0, 0, "PE"), ("L", 8, 0, "DMA"), ("M", 1, 0, "PE"),
-    ("G", 0, 0, "S"), ("Q", 1, 0, "V"), ("G", 1, 0, "S"), ("Q", 1, 1, "V"), ("A", 7, 0, "V"), ("M", 2, 0, "PE"),
-    ("M", 3, 0, "PE"), ("G", 2, 0, "S"), ("A", 8, 0, "V"), ("L", 9, 0, "DMA"), ("M", 4, 0, "PE"), ("SQ", 2, 0, "S"),
-    ("M", 5, 0, "PE"), ("G", 3, 0, "S"), ("G", 4, 0, "S"), ("RC", 2, 0, "V"), ("A", 9, 0, "V"), ("G", 5, 0, "S"),
-    ("B", 4, 0, "V"), ("L", 10, 0, "DMA"), ("B", 5, 0, "V"), ("T", 4, 0, "PE"), ("B", 6, 0, "V"), ("B", 7, 0, "V"),
-    ("T", 5, 0, "PE"), ("D", 4, 0, "S"), ("A", 10, 0, "V"), ("T", 6, 0, "PE"), ("T", 7, 0, "PE"), ("D", 5, 0, "S"),
-    ("A", 11, 0, "V"), ("D", 6, 0, "S"), ("Q", 2, 0, "V"), ("Q", 2, 1, "V"), ("A", 12, 0, "V"), ("SQ", 3, 0, "S"),
-    ("M", 6, 0, "PE"), ("D", 7, 0, "S"), ("M", 7, 0, "PE"), ("RC", 3, 0, "V"), ("M", 8, 0, "PE"), ("A", 13, 0, "V"),
-    ("G", 6, 0, "S"), ("M", 9, 0, "PE"), ("G", 7, 0, "S"), ("M", 10, 0, "PE"), ("G", 8, 0, "S"), ("M", 11, 0, "PE"),
-    ("Q", 3, 0, "V"), ("Q", 3, 1, "V"), ("G", 9, 0, "S"), ("M", 12, 0, "PE"), ("B", 8, 0, "V"), ("G", 10, 0, "S"),
-    ("M", 13, 0, "PE"), ("B", 9, 0, "V"), ("G", 11, 0, "S"), ("M", 14, 0, "PE"), ("B", 10, 0, "V"), ("G", 12, 0, "S"),
-    ("B", 11, 0, "V"), ("G", 13, 0, "S"), ("M", 15, 0, "PE"), ("G", 14, 0, "S"), ("A", 14, 0, "V"), ("T", 8, 0, "PE"),
-    ("G", 15, 0, "S"), ("T", 9, 0, "PE"), ("D", 8, 0, "S"), ("ST", 0, 0, "DMA"), ("A", 15, 0, "V"), ("T", 10, 0, "PE"),
-    ("T", 11, 0, "PE"), ("D", 9, 0, "S"), ("A", 16, 0, "V"), ("M", 16, 0, "PE"), ("M", 17, 0, "PE"), ("SQ", 4, 0, "S"),
-    ("D", 10, 0, "S"), ("RC", 4, 0, "V"), ("D", 11, 0, "V"), ("M", 18, 0, "PE"), ("M", 19, 0, "PE"), ("G", 16, 0, "S"),
-    ("Q", 4, 0, "V"), ("Q", 4, 1, "V"), ("G", 17, 0, "S"), ("M", 20, 0, "PE"), ("Q", 5, 0, "V"), ("G", 18, 0, "S"),
-    ("Q", 5, 1, "V"), ("M", 21, 0, "PE"), ("ST", 1, 0, "DMA"), ("G", 19, 0, "S"), ("B", 12, 0, "V"), ("M", 22, 0, "PE"),
-    ("G", 20, 0, "S"), ("B", 13, 0, "V"), ("M", 23, 0, "PE"), ("G", 21, 0, "S"), ("B", 14, 0, "V"), ("M", 24, 0, "PE"),
-    ("G", 22, 0, "S"), ("ST", 2, 0, "DMA"), ("B", 15, 0, "V"), ("M", 25, 0, "PE"), ("G", 23, 0, "S"), ("T", 12, 0, "PE"),
-    ("A", 17, 0, "V"), ("G", 24, 0, "S"), ("G", 25, 0, "S"), ("T", 13, 0, "PE"), ("D", 12, 0, "S"), ("ST", 3, 0, "DMA"),
-    ("T", 14, 0, "PE"), ("A", 18, 0, "V"), ("T", 15, 0, "PE"), ("D", 13, 0, "S"), ("ST", 4, 0, "DMA"), ("M", 26, 0, "PE"),
-    ("D", 14, 0, "V"), ("M", 27, 0, "PE"), ("D", 15, 0, "S"), ("ST", 5, 0, "DMA"), ("M", 28, 0, "PE"), ("Q", 6, 0, "V"),
-    ("M", 29, 0, "PE"), ("Q", 6, 1, "V"), ("G", 26, 0, "S"), ("A", 19, 0, "V"), ("ST", 6, 0, "DMA"), ("G", 27, 0, "S"),
-    ("M", 30, 0, "PE"), ("G", 28, 0, "S"), ("M", 31, 0, "PE"), ("Q", 7, 0, "V"), ("ST", 7, 0, "DMA"), ("SQ", 5, 0, "S"),
-    ("M", 32, 0, "PE"), ("G", 29, 0, "S"), ("Q", 7, 1, "V"), ("G", 30, 0, "S"), ("RC", 5, 0, "V"), ("A", 20, 0, "V"),
-    ("M", 33, 0, "PE"), ("G", 31, 0, "S"), ("M", 34, 0, "PE"), ("G", 32, 0, "S"), ("M", 35, 0, "PE"), ("B", 16, 0, "V"),
-    ("G", 33, 0, "S"), ("M", 36, 0, "PE"), ("B", 17, 0, "V"), ("G", 34, 0, "S"), ("M", 37, 0, "PE"), ("B", 18, 0, "V"),
-    ("G", 35, 0, "S"), ("M", 38, 0, "PE"), ("B", 19, 0, "V"), ("G", 36, 0, "S"), ("A", 21, 0, "V"), ("G", 37, 0, "S"),
-    ("T", 16, 0, "PE"), ("G", 38, 0, "S"), ("T", 17, 0, "PE"), ("D", 16, 0, "S"), ("A", 22, 0, "V"), ("T", 18, 0, "PE"),
-    ("T", 19, 0, "PE"), ("D", 17, 0, "S"), ("M", 39, 0, "PE"), ("A", 23, 0, "V"), ("M", 40, 0, "PE"), ("D", 18, 0, "S"),
-    ("M", 41, 0, "PE"), ("D", 19, 0, "V"), ("M", 42, 0, "PE"), ("SQ", 6, 0, "S"), ("G", 39, 0, "S"), ("RC", 6, 0, "V"),
-    ("Q", 8, 0, "V"), ("G", 40, 0, "S"), ("M", 43, 0, "PE"), ("ST", 8, 0, "DMA"), ("Q", 8, 1, "V"), ("Q", 9, 0, "V"),
-    ("G", 41, 0, "S"), ("M", 44, 0, "PE"), ("Q", 9, 1, "V"), ("G", 42, 0, "S"), ("B", 20, 0, "V"), ("M", 45, 0, "PE"),
-    ("ST", 9, 0, "DMA"), ("G", 43, 0, "S"), ("B", 21, 0, "V"), ("M", 46, 0, "PE"), ("G", 44, 0, "S"), ("B", 22, 0, "V"),
-    ("M", 47, 0, "PE"), ("G", 45, 0, "S"), ("B", 23, 0, "V"), ("M", 48, 0, "PE"), ("G", 46, 0, "S"), ("T", 20, 0, "PE"),
-    ("A", 24, 0, "V"), ("ST", 10, 0, "DMA"), ("G", 47, 0, "S"), ("G", 48, 0, "S"), ("T", 21, 0, "PE"), ("D", 20, 0, "S"),
-    ("ST", 11, 0, "DMA"), ("T", 22, 0, "PE"), ("A", 25, 0, "V"), ("T", 23, 0, "PE"), ("D", 21, 0, "S"), ("M", 49, 0, "PE"),
-    ("ST", 12, 0, "DMA"), ("D", 22, 0, "V"), ("M", 50, 0, "PE"), ("D", 23, 0, "S"), ("M", 51, 0, "PE"), ("ST", 13, 0, "DMA"),
-    ("Q", 10, 0, "V"), ("M", 52, 0, "PE"), ("Q", 10, 1, "V"), ("G", 49, 0, "S"), ("A", 26, 0, "V"), ("G", 50, 0, "S"),
-    ("M", 53, 0, "PE"), ("ST", 14, 0, "DMA"), ("G", 51, 0, "S"), ("M", 54, 0, "PE"), ("Q", 11, 0, "V"), ("G", 52, 0, "S"),
-    ("M", 55, 0, "PE"), ("Q", 11, 1, "V"), ("ST", 15, 0, "DMA"), ("G", 53, 0, "S"), ("M", 56, 0, "PE"), ("A", 27, 0, "V"),
-    ("G", 54, 0, "S"), ("M", 57, 0, "PE"), ("G", 55, 0, "S"), ("M", 58, 0, "PE"), ("G", 56, 0, "S"), ("M", 59, 0, "PE"),
-    ("A", 28, 0, "V"), ("SQ", 7, 0, "S"), ("M", 60, 0, "PE"), ("G", 57, 0, "S"), ("G", 58, 0, "S"), ("M", 61, 0, "PE"),
-    ("G", 59, 0, "S"), ("M", 62, 0, "PE"), ("RC", 7, 0, "V"), ("A", 29, 0, "V"), ("G", 60, 0, "S"), ("G", 61, 0, "S"),
-    ("M", 63, 0, "PE"), ("G", 62, 0, "S"), ("M", 64, 0, "PE"), ("G", 63, 0, "S"), ("B", 24, 0, "V"), ("B", 25, 0, "V"),
-    ("M", 65, 0, "PE"), ("G", 64, 0, "S"), ("B", 26, 0, "V"), ("ST", 16, 0, "DMA"), ("M", 66, 0, "PE"), ("B", 27, 0, "V"),
-    ("G", 65, 0, "S"), ("T", 24, 0, "PE"), ("A", 30, 0, "V"), ("G", 66, 0, "S"), ("ST", 17, 0, "DMA"), ("T", 25, 0, "PE"),
-    ("D", 24, 0, "S"), ("T", 26, 0, "PE"), ("A", 31, 0, "V"), ("T", 27, 0, "PE"), ("ST", 18, 0, "DMA"), ("D", 25, 0, "S"),
-    ("M", 67, 0, "PE"), ("D", 26, 0, "V"), ("M", 68, 0, "PE"), ("M", 69, 0, "PE"), ("SQ", 8, 0, "S"), ("D", 27, 0, "S"),
-    ("M", 70, 0, "PE"), ("RC", 8, 0, "V"), ("G", 67, 0, "V"), ("B", 28, 0, "V"), ("M", 71, 0, "PE"), ("ST", 19, 0, "DMA"),
-    ("G", 68, 0, "S"), ("B", 29, 0, "V"), ("T", 28, 0, "PE"), ("G", 69, 0, "S"), ("Q", 12, 0, "V"), ("G", 70, 0, "S"),
-    ("T", 29, 0, "PE"), ("G", 71, 0, "S"), ("Q", 12, 1, "V"), ("ST", 20, 0, "DMA"), ("D", 28, 0, "S"), ("B", 30, 0, "V"),
-    ("B", 31, 0, "V"), ("T", 30, 0, "PE"), ("ST", 21, 0, "DMA"), ("D", 29, 0, "S"), ("T", 31, 0, "PE"), ("M", 72, 0, "PE"),
-    ("ST", 22, 0, "DMA"), ("D", 30, 0, "S"), ("Q", 13, 0, "V"), ("M", 73, 0, "PE"), ("Q", 13, 1, "V"), ("M", 74, 0, "PE"),
-    ("D", 31, 0, "V"), ("ST", 23, 0, "DMA"), ("G", 72, 0, "S"), ("M", 75, 0, "PE"), ("G", 73, 0, "S"), ("M", 76, 0, "PE"),
-    ("Q", 14, 0, "V"), ("ST", 24, 0, "DMA"), ("G", 74, 0, "S"), ("Q", 14, 1, "V"), ("Q", 15, 0, "V"), ("M", 77, 0, "PE"),
-    ("Q", 15, 1, "V"), ("G", 75, 0, "V"), ("ST", 25, 0, "DMA"), ("G", 76, 0, "S"), ("M", 78, 0, "PE"), ("G", 77, 0, "S"),
-    ("ST", 26, 0, "DMA"), ("M", 79, 0, "PE"), ("G", 78, 0, "S"), ("M", 80, 0, "PE"), ("ST", 27, 0, "DMA"), ("M", 81, 0, "PE"),
-    ("G", 79, 0, "V"), ("G", 80, 0, "S"), ("M", 82, 0, "PE"), ("G", 81, 0, "S"), ("M", 83, 0, "PE"), ("ST", 28, 0, "DMA"),
-    ("G", 82, 0, "S"), ("M", 84, 0, "PE"), ("G", 83, 0, "S"), ("ST", 29, 0, "DMA"), ("M", 85, 0, "PE"), ("G", 84, 0, "S"),
-    ("M", 86, 0, "PE"), ("M", 87, 0, "PE"), ("G", 85, 0, "V"), ("G", 86, 0, "S"), ("M", 88, 0, "PE"), ("ST", 30, 0, "DMA"),
-    ("G", 87, 0, "S"), ("M", 90, 0, "PE"), ("G", 88, 0, "S"), ("M", 89, 0, "PE"), ("G", 90, 0, "S"), ("M", 91, 0, "PE"),
-    ("G", 89, 0, "S"), ("ST", 31, 0, "DMA"), ("M", 92, 0, "PE"), ("G", 91, 0, "S"), ("M", 94, 0, "PE"), ("G", 92, 0, "S"),
-    ("ST", 32, 0, "DMA"), ("M", 93, 0, "PE"), ("G", 94, 0, "S"), ("ST", 33, 0, "DMA"), ("M", 95, 0, "PE"), ("G", 93, 0, "S"),
-    ("M", 96, 0, "PE"), ("M", 98, 0, "PE"), ("ST", 34, 0, "DMA"), ("G", 95, 0, "V"), ("G", 96, 0, "V"), ("G", 98, 0, "S"),
-    ("M", 99, 0, "PE"), ("M", 97, 0, "PE"), ("ST", 35, 0, "DMA"), ("G", 99, 0, "S"), ("M", 100, 0, "PE"), ("G", 97, 0, "S"),
-    ("G", 100, 0, "S"), ("M", 101, 0, "PE"), ("ST", 36, 0, "DMA"), ("G", 101, 0, "S"), ("ST", 37, 0, "DMA"), ("ST", 38, 0, "DMA"),
-    ("ST", 39, 0, "DMA"), ("ST", 40, 0, "DMA"), ("ST", 41, 0, "DMA"), ("ST", 42, 0, "DMA"), ("ST", 43, 0, "DMA"), ("ST", 44, 0, "DMA"),
-    ("ST", 45, 0, "DMA"),
+    ("A", 1, 0, "V"), ("SQ", 0, 0, "S"), ("L", 5, 0, "DMA"), ("A", 2, 0, "V"), ("SQ", 1, 0, "S"), ("RC", 0, 0, "V"),
+    ("A", 3, 0, "V"), ("L", 6, 0, "DMA"), ("RC", 1, 0, "V"), ("B", 0, 0, "V"), ("B", 1, 0, "V"), ("SQ", 2, 0, "S"),
+    ("A", 4, 0, "V"), ("T", 0, 0, "PE"), ("T", 1, 0, "PE"), ("RC", 2, 0, "V"), ("A", 5, 0, "V"), ("L", 7, 0, "DMA"),
+    ("D", 0, 0, "S"), ("D", 1, 0, "S"), ("B", 2, 0, "V"), ("B", 3, 0, "V"), ("A", 6, 0, "V"), ("T", 2, 0, "PE"),
+    ("SQ", 3, 0, "S"), ("L", 8, 0, "DMA"), ("T", 3, 0, "PE"), ("RC", 3, 0, "V"), ("Q", 0, 0, "V"), ("D", 2, 0, "S"),
+    ("Q", 0, 1, "V"), ("B", 4, 0, "V"), ("B", 5, 0, "V"), ("D", 3, 0, "S"), ("A", 7, 0, "V"), ("T", 4, 0, "PE"),
+    ("L", 9, 0, "DMA"), ("T", 5, 0, "PE"), ("A", 8, 0, "V"), ("M", 0, 0, "PE"), ("D", 4, 0, "S"), ("M", 1, 0, "PE"),
+    ("Q", 1, 0, "V"), ("SQ", 4, 0, "S"), ("D", 5, 0, "S"), ("Q", 1, 1, "V"), ("G", 0, 0, "V"), ("L", 10, 0, "DMA"),
+    ("RC", 4, 0, "V"), ("A", 9, 0, "V"), ("G", 1, 0, "S"), ("M", 2, 0, "PE"), ("M", 3, 0, "PE"), ("B", 6, 0, "V"),
+    ("M", 4, 0, "PE"), ("G", 2, 0, "S"), ("B", 7, 0, "V"), ("M", 5, 0, "PE"), ("A", 10, 0, "V"), ("SQ", 5, 0, "S"),
+    ("T", 6, 0, "PE"), ("G", 3, 0, "S"), ("T", 7, 0, "PE"), ("G", 4, 0, "S"), ("RC", 5, 0, "V"), ("G", 5, 0, "S"),
+    ("A", 11, 0, "V"), ("D", 6, 0, "S"), ("B", 8, 0, "V"), ("D", 7, 0, "S"), ("B", 9, 0, "V"), ("A", 12, 0, "V"),
+    ("T", 8, 0, "PE"), ("SQ", 6, 0, "S"), ("T", 9, 0, "PE"), ("Q", 2, 0, "V"), ("D", 8, 0, "S"), ("RC", 6, 0, "V"),
+    ("Q", 2, 1, "V"), ("D", 9, 0, "S"), ("B", 10, 0, "V"), ("B", 11, 0, "V"), ("A", 13, 0, "V"), ("T", 10, 0, "PE"),
+    ("T", 11, 0, "PE"), ("A", 14, 0, "V"), ("M", 6, 0, "PE"), ("D", 10, 0, "S"), ("M", 7, 0, "PE"), ("A", 15, 0, "V"),
+    ("SQ", 7, 0, "S"), ("M", 8, 0, "PE"), ("D", 11, 0, "S"), ("M", 9, 0, "PE"), ("RC", 7, 0, "V"), ("M", 10, 0, "PE"),
+    ("G", 6, 0, "V"), ("G", 7, 0, "S"), ("B", 12, 0, "V"), ("SQ", 8, 0, "S"), ("G", 8, 0, "S"), ("Q", 3, 0, "V"),
+    ("M", 11, 0, "PE"), ("ST", 0, 0, "DMA"), ("G", 9, 0, "S"), ("RC", 8, 0, "V"), ("Q", 3, 1, "V"), ("T", 12, 0, "PE"),
+    ("G", 10, 0, "S"), ("B", 13, 0, "V"), ("M", 12, 0, "PE"), ("G", 11, 0, "S"), ("B", 14, 0, "V"), ("ST", 1, 0, "DMA"),
+    ("B", 15, 0, "V"), ("D", 12, 0, "S"), ("T", 13, 0, "PE"), ("A", 16, 0, "V"), ("ST", 2, 0, "DMA"), ("T", 14, 0, "PE"),
+    ("G", 12, 0, "S"), ("M", 13, 0, "PE"), ("A", 17, 0, "V"), ("D", 13, 0, "S"), ("T", 15, 0, "PE"), ("D", 14, 0, "V"),
+    ("M", 14, 0, "PE"), ("G", 13, 0, "S"), ("M", 15, 0, "PE"), ("SQ", 9, 0, "S"), ("D", 15, 0, "S"), ("A", 18, 0, "V"),
+    ("M", 16, 0, "PE"), ("ST", 3, 0, "DMA"), ("M", 17, 0, "PE"), ("G", 14, 0, "S"), ("RC", 9, 0, "V"), ("A", 19, 0, "V"),
+    ("M", 18, 0, "PE"), ("G", 15, 0, "S"), ("G", 16, 0, "S"), ("M", 19, 0, "PE"), ("ST", 4, 0, "DMA"), ("Q", 4, 0, "V"),
+    ("G", 17, 0, "S"), ("M", 20, 0, "PE"), ("Q", 4, 1, "V"), ("SQ", 10, 0, "S"), ("M", 21, 0, "PE"), ("ST", 5, 0, "DMA"),
+    ("G", 18, 0, "S"), ("B", 16, 0, "V"), ("B", 17, 0, "V"), ("G", 19, 0, "S"), ("RC", 10, 0, "V"), ("G", 20, 0, "V"),
+    ("ST", 6, 0, "DMA"), ("M", 22, 0, "PE"), ("G", 21, 0, "S"), ("B", 18, 0, "V"), ("T", 16, 0, "PE"), ("B", 19, 0, "V"),
+    ("ST", 7, 0, "DMA"), ("G", 22, 0, "S"), ("A", 20, 0, "V"), ("T", 17, 0, "PE"), ("T", 18, 0, "PE"), ("D", 16, 0, "S"),
+    ("M", 23, 0, "PE"), ("A", 21, 0, "V"), ("D", 17, 0, "S"), ("M", 24, 0, "PE"), ("T", 19, 0, "PE"), ("D", 18, 0, "V"),
+    ("G", 23, 0, "S"), ("M", 25, 0, "PE"), ("SQ", 11, 0, "S"), ("A", 22, 0, "V"), ("G", 24, 0, "S"), ("M", 26, 0, "PE"),
+    ("ST", 8, 0, "DMA"), ("D", 19, 0, "S"), ("M", 27, 0, "PE"), ("RC", 11, 0, "V"), ("M", 28, 0, "PE"), ("A", 23, 0, "V"),
+    ("G", 25, 0, "S"), ("M", 29, 0, "PE"), ("G", 26, 0, "S"), ("Q", 5, 0, "V"), ("G", 27, 0, "S"), ("M", 30, 0, "PE"),
+    ("ST", 9, 0, "DMA"), ("Q", 5, 1, "V"), ("SQ", 12, 0, "S"), ("M", 31, 0, "PE"), ("G", 28, 0, "S"), ("B", 20, 0, "V"),
+    ("M", 32, 0, "PE"), ("ST", 10, 0, "DMA"), ("B", 21, 0, "V"), ("G", 29, 0, "S"), ("RC", 12, 0, "V"), ("A", 24, 0, "V"),
+    ("T", 20, 0, "PE"), ("G", 30, 0, "S"), ("T", 21, 0, "PE"), ("G", 31, 0, "S"), ("ST", 11, 0, "DMA"), ("B", 22, 0, "V"),
+    ("M", 33, 0, "PE"), ("D", 20, 0, "S"), ("B", 23, 0, "V"), ("A", 25, 0, "V"), ("ST", 12, 0, "DMA"), ("M", 34, 0, "PE"),
+    ("D", 21, 0, "S"), ("T", 22, 0, "PE"), ("G", 32, 0, "V"), ("ST", 13, 0, "DMA"), ("T", 23, 0, "PE"), ("G", 33, 0, "V"),
+    ("SQ", 13, 0, "S"), ("M", 35, 0, "PE"), ("G", 34, 0, "S"), ("A", 26, 0, "V"), ("ST", 14, 0, "DMA"), ("D", 22, 0, "S"),
+    ("M", 36, 0, "PE"), ("M", 37, 0, "PE"), ("RC", 13, 0, "V"), ("ST", 15, 0, "DMA"), ("D", 23, 0, "S"), ("A", 27, 0, "V"),
+    ("G", 35, 0, "S"), ("B", 24, 0, "V"), ("B", 25, 0, "V"), ("G", 36, 0, "S"), ("Q", 6, 0, "V"), ("T", 24, 0, "PE"),
+    ("SQ", 14, 0, "S"), ("G", 37, 0, "S"), ("Q", 6, 1, "V"), ("T", 25, 0, "PE"), ("RC", 14, 0, "V"), ("A", 28, 0, "V"),
+    ("D", 24, 0, "S"), ("M", 38, 0, "PE"), ("B", 26, 0, "V"), ("D", 25, 0, "S"), ("M", 39, 0, "PE"), ("B", 27, 0, "V"),
+    ("A", 29, 0, "V"), ("M", 40, 0, "PE"), ("G", 38, 0, "S"), ("T", 26, 0, "PE"), ("G", 39, 0, "S"), ("A", 30, 0, "V"),
+    ("T", 27, 0, "PE"), ("G", 40, 0, "S"), ("M", 41, 0, "PE"), ("SQ", 15, 0, "S"), ("ST", 16, 0, "DMA"), ("D", 26, 0, "V"),
+    ("D", 27, 0, "S"), ("M", 42, 0, "PE"), ("M", 43, 0, "PE"), ("RC", 15, 0, "V"), ("G", 41, 0, "S"), ("A", 31, 0, "V"),
+    ("M", 44, 0, "PE"), ("G", 42, 0, "S"), ("M", 45, 0, "PE"), ("G", 43, 0, "S"), ("ST", 17, 0, "DMA"), ("M", 46, 0, "PE"),
+    ("Q", 7, 0, "V"), ("G", 44, 0, "S"), ("M", 47, 0, "PE"), ("Q", 7, 1, "V"), ("SQ", 16, 0, "S"), ("ST", 18, 0, "DMA"),
+    ("M", 48, 0, "PE"), ("G", 45, 0, "S"), ("B", 28, 0, "V"), ("B", 29, 0, "V"), ("M", 49, 0, "PE"), ("G", 46, 0, "S"),
+    ("RC", 16, 0, "V"), ("B", 30, 0, "V"), ("T", 28, 0, "PE"), ("G", 47, 0, "S"), ("ST", 19, 0, "DMA"), ("B", 31, 0, "V"),
+    ("G", 48, 0, "V"), ("T", 29, 0, "PE"), ("G", 49, 0, "S"), ("T", 30, 0, "PE"), ("D", 28, 0, "S"), ("ST", 20, 0, "DMA"),
+    ("M", 50, 0, "PE"), ("D", 29, 0, "V"), ("D", 30, 0, "S"), ("M", 51, 0, "PE"), ("ST", 21, 0, "DMA"), ("T", 31, 0, "PE"),
+    ("G", 50, 0, "S"), ("Q", 8, 0, "V"), ("ST", 22, 0, "DMA"), ("M", 52, 0, "PE"), ("Q", 8, 1, "V"), ("G", 51, 0, "S"),
+    ("Q", 9, 0, "V"), ("M", 53, 0, "PE"), ("Q", 9, 1, "V"), ("ST", 23, 0, "DMA"), ("G", 52, 0, "S"), ("M", 54, 0, "PE"),
+    ("D", 31, 0, "V"), ("G", 53, 0, "S"), ("M", 55, 0, "PE"), ("M", 56, 0, "PE"), ("ST", 24, 0, "DMA"), ("G", 54, 0, "S"),
+    ("M", 57, 0, "PE"), ("ST", 25, 0, "DMA"), ("M", 58, 0, "PE"), ("G", 55, 0, "S"), ("Q", 10, 0, "V"), ("Q", 10, 1, "V"),
+    ("G", 56, 0, "S"), ("ST", 26, 0, "DMA"), ("M", 59, 0, "PE"), ("G", 57, 0, "V"), ("G", 58, 0, "S"), ("M", 60, 0, "PE"),
+    ("ST", 27, 0, "DMA"), ("M", 61, 0, "PE"), ("G", 59, 0, "S"), ("ST", 28, 0, "DMA"), ("M", 63, 0, "PE"), ("G", 60, 0, "S"),
+    ("M", 62, 0, "PE"), ("G", 61, 0, "S"), ("ST", 29, 0, "DMA"), ("M", 64, 0, "PE"), ("G", 63, 0, "S"), ("M", 65, 0, "PE"),
+    ("G", 62, 0, "S"), ("M", 66, 0, "PE"), ("M", 68, 0, "PE"), ("G", 64, 0, "V"), ("G", 65, 0, "S"), ("G", 66, 0, "S"),
+    ("G", 68, 0, "S"), ("M", 69, 0, "PE"), ("ST", 30, 0, "DMA"), ("M", 67, 0, "PE"), ("M", 70, 0, "PE"), ("M", 71, 0, "PE"),
+    ("ST", 31, 0, "DMA"), ("G", 69, 0, "S"), ("G", 67, 0, "S"), ("M", 73, 0, "PE"), ("G", 70, 0, "S"), ("ST", 32, 0, "DMA"),
+    ("M", 74, 0, "PE"), ("G", 71, 0, "S"), ("M", 72, 0, "PE"), ("ST", 33, 0, "DMA"), ("G", 73, 0, "S"), ("M", 75, 0, "PE"),
+    ("ST", 34, 0, "DMA"), ("G", 74, 0, "S"), ("M", 76, 0, "PE"), ("G", 72, 0, "S"), ("ST", 35, 0, "DMA"), ("M", 78, 0, "PE"),
+    ("M", 79, 0, "PE"), ("G", 75, 0, "S"), ("ST", 36, 0, "DMA"), ("G", 76, 0, "S"), ("G", 78, 0, "S"), ("G", 79, 0, "S"),
+    ("M", 77, 0, "PE"), ("ST", 37, 0, "DMA"), ("ST", 38, 0, "DMA"), ("G", 77, 0, "S"), ("ST", 39, 0, "DMA"), ("ST", 40, 0, "DMA"),
+    ("ST", 41, 0, "DMA"), ("ST", 42, 0, "DMA"), ("ST", 43, 0, "DMA"), ("ST", 44, 0, "DMA"), ("ST", 45, 0, "DMA"),
 )
 
 

@@ -16,87 +16,31 @@ ACT = mybir.ActivationFunctionType
 P = 128
 K = 1024
 ROWS = 1024
-PINNED = True
-NF = 8
-NPT = 3
-NPM = 5
-NG = 2
-NO = 16
+COMMUNITIES = 4
+TILES = 8
+PINNED = False
+T_BANKS = 3
+MX_BANKS = 8 - T_BANKS
+FN_BUFS = 8
+GR_BUFS = 3
+OT_BUFS = 16
+MID_PIECES = ((0, 2), (2, 2), (4, 2), (6, 2))
+LAST_PIECES = ((0, 2), (2, 2), (4, 2), (6, 1), (7, 1))
+MID_CUTS = (8,)
+LAST_CUTS = (4, 7, 8)
+LAG_F2 = 2
+LAG_BE = 3
+SECTIONS = ("products", "quantise", "stats")
 
-LOADS = ((0,), (1,), (2,), (3,), (4, 5, 6, 7), (8, 9, 10, 11), (12, 13, 14, 15), (16, 17, 18, 19), (20, 21, 22, 23), (24, 25, 26, 27), (28, 29, 30, 31))
-BATCHES = ((0,), (1,), (2, 3), (4, 5), (6, 7), (8, 9), (10, 11), (12, 13), (14, 15), (16, 17), (18, 19), (20, 21), (22, 23), (24, 25), (26, 27), (28, 29), (30, 31))
-PIECES = ((0, 1), (2, 3), (4, 5, 6, 7), (8, 9, 10, 11), (12, 13, 14, 15), (16, 17, 18, 19), (20, 21, 22, 23), (24, 25, 26, 27), (28, 29), (30,), (31,))
-GROUPS = ((0, 0, 0, 2, 0), (0, 1, 0, 2, 0), (0, 2, 0, 4, 1), (0, 3, 0, 4, 1), (0, 0, 2, 2, 1), (0, 1, 2, 2, 1), (0, 4, 0, 4, 2), (0, 4, 4, 4, 2), (0, 5, 0, 4, 2), (0, 5, 4, 4, 2), (0, 6, 0, 4, 2), (0, 6, 4, 4, 2), (0, 7, 0, 4, 2), (0, 7, 4, 4, 2), (0, 0, 4, 4, 2), (0, 1, 4, 4, 2), (0, 2, 4, 4, 2), (0, 3, 4, 4, 2), (1, 0, 0, 4, 3), (1, 1, 0, 4, 3), (1, 2, 0, 4, 3), (1, 3, 0, 4, 3), (1, 4, 0, 4, 4), (1, 4, 4, 4, 4), (1, 5, 0, 4, 4), (1, 5, 4, 4, 4), (1, 6, 0, 4, 4), (1, 6, 4, 4, 4), (1, 7, 0, 4, 4), (1, 7, 4, 4, 4), (1, 0, 4, 4, 4), (1, 1, 4, 4, 4), (1, 2, 4, 4, 4), (1, 3, 4, 4, 4), (2, 0, 0, 4, 5), (2, 1, 0, 4, 5), (2, 2, 0, 4, 5), (2, 3, 0, 4, 5), (2, 4, 0, 4, 6), (2, 4, 4, 4, 6), (2, 5, 0, 4, 6), (2, 5, 4, 4, 6), (2, 6, 0, 4, 6), (2, 6, 4, 4, 6), (2, 7, 0, 4, 6), (2, 7, 4, 4, 6), (2, 0, 4, 4, 6), (2, 1, 4, 4, 6), (2, 2, 4, 4, 6), (2, 3, 4, 4, 6), (3, 0, 0, 4, 7), (3, 1, 0, 4, 7), (3, 2, 0, 4, 7), (3, 3, 0, 4, 7), (3, 4, 0, 4, 8), (3, 4, 4, 2, 8), (3, 5, 0, 4, 8), (3, 5, 4, 2, 8), (3, 0, 4, 2, 8), (3, 1, 4, 2, 8), (3, 2, 4, 2, 8), (3, 3, 4, 2, 8), (3, 6, 0, 4, 9), (3, 6, 4, 2, 9), (3, 6, 6, 1, 9), (3, 0, 6, 1, 9), (3, 1, 6, 1, 9), (3, 2, 6, 1, 9), (3, 3, 6, 1, 9), (3, 4, 6, 1, 9), (3, 5, 6, 1, 9), (3, 7, 0, 4, 10), (3, 7, 4, 4, 10), (3, 0, 7, 1, 10), (3, 1, 7, 1, 10), (3, 2, 7, 1, 10), (3, 3, 7, 1, 10), (3, 4, 7, 1, 10), (3, 5, 7, 1, 10), (3, 6, 7, 1, 10))
-STORES = ((0, 4, 0, 8), (0, 5, 0, 8), (0, 6, 0, 8), (0, 7, 0, 8), (0, 0, 0, 8), (0, 1, 0, 8), (0, 2, 0, 8), (0, 3, 0, 8), (1, 4, 0, 8), (1, 5, 0, 8), (1, 6, 0, 8), (1, 7, 0, 8), (1, 0, 0, 8), (1, 1, 0, 8), (1, 2, 0, 8), (1, 3, 0, 8), (2, 4, 0, 8), (2, 5, 0, 8), (2, 6, 0, 8), (2, 7, 0, 8), (2, 0, 0, 8), (2, 1, 0, 8), (2, 2, 0, 8), (2, 3, 0, 8), (3, 0, 0, 4), (3, 1, 0, 4), (3, 2, 0, 4), (3, 3, 0, 4), (3, 4, 0, 4), (3, 5, 0, 4), (3, 6, 0, 4), (3, 6, 4, 3), (3, 0, 4, 3), (3, 1, 4, 3), (3, 2, 4, 3), (3, 3, 4, 3), (3, 4, 4, 3), (3, 5, 4, 3), (3, 7, 0, 8), (3, 0, 7, 1), (3, 1, 7, 1), (3, 2, 7, 1), (3, 3, 7, 1), (3, 4, 7, 1), (3, 5, 7, 1), (3, 6, 7, 1))
-SCHEDULE = (
-    ("L", 0, 0, "DMA"), ("L", 1, 0, "DMA"), ("L", 2, 0, "DMA"), ("L", 3, 0, "DMA"), ("L", 4, 0, "DMA"), ("A", 0, 0, "V"),
-    ("A", 1, 0, "V"), ("SQ", 0, 0, "S"), ("L", 5, 0, "DMA"), ("A", 2, 0, "V"), ("SQ", 1, 0, "S"), ("RC", 0, 0, "V"),
-    ("A", 3, 0, "V"), ("L", 6, 0, "DMA"), ("RC", 1, 0, "V"), ("B", 0, 0, "V"), ("B", 1, 0, "V"), ("SQ", 2, 0, "S"),
-    ("A", 4, 0, "V"), ("T", 0, 0, "PE"), ("T", 1, 0, "PE"), ("RC", 2, 0, "V"), ("A", 5, 0, "V"), ("L", 7, 0, "DMA"),
-    ("D", 0, 0, "S"), ("D", 1, 0, "S"), ("B", 2, 0, "V"), ("B", 3, 0, "V"), ("A", 6, 0, "V"), ("T", 2, 0, "PE"),
-    ("SQ", 3, 0, "S"), ("L", 8, 0, "DMA"), ("T", 3, 0, "PE"), ("RC", 3, 0, "V"), ("Q", 0, 0, "V"), ("D", 2, 0, "S"),
-    ("Q", 0, 1, "V"), ("B", 4, 0, "V"), ("B", 5, 0, "V"), ("D", 3, 0, "S"), ("A", 7, 0, "V"), ("T", 4, 0, "PE"),
-    ("L", 9, 0, "DMA"), ("T", 5, 0, "PE"), ("A", 8, 0, "V"), ("M", 0, 0, "PE"), ("D", 4, 0, "S"), ("M", 1, 0, "PE"),
-    ("Q", 1, 0, "V"), ("SQ", 4, 0, "S"), ("D", 5, 0, "S"), ("Q", 1, 1, "V"), ("G", 0, 0, "V"), ("L", 10, 0, "DMA"),
-    ("RC", 4, 0, "V"), ("A", 9, 0, "V"), ("G", 1, 0, "S"), ("M", 2, 0, "PE"), ("M", 3, 0, "PE"), ("B", 6, 0, "V"),
-    ("M", 4, 0, "PE"), ("G", 2, 0, "S"), ("B", 7, 0, "V"), ("M", 5, 0, "PE"), ("A", 10, 0, "V"), ("SQ", 5, 0, "S"),
-    ("T", 6, 0, "PE"), ("G", 3, 0, "S"), ("T", 7, 0, "PE"), ("G", 4, 0, "S"), ("RC", 5, 0, "V"), ("G", 5, 0, "S"),
-    ("A", 11, 0, "V"), ("D", 6, 0, "S"), ("B", 8, 0, "V"), ("D", 7, 0, "S"), ("B", 9, 0, "V"), ("A", 12, 0, "V"),
-    ("T", 8, 0, "PE"), ("SQ", 6, 0, "S"), ("T", 9, 0, "PE"), ("Q", 2, 0, "V"), ("D", 8, 0, "S"), ("RC", 6, 0, "V"),
-    ("Q", 2, 1, "V"), ("D", 9, 0, "S"), ("B", 10, 0, "V"), ("B", 11, 0, "V"), ("A", 13, 0, "V"), ("T", 10, 0, "PE"),
-    ("T", 11, 0, "PE"), ("A", 14, 0, "V"), ("M", 6, 0, "PE"), ("D", 10, 0, "S"), ("M", 7, 0, "PE"), ("A", 15, 0, "V"),
-    ("SQ", 7, 0, "S"), ("M", 8, 0, "PE"), ("D", 11, 0, "S"), ("M", 9, 0, "PE"), ("RC", 7, 0, "V"), ("M", 10, 0, "PE"),
-    ("G", 6, 0, "V"), ("G", 7, 0, "S"), ("B", 12, 0, "V"), ("SQ", 8, 0, "S"), ("G", 8, 0, "S"), ("Q", 3, 0, "V"),
-    ("M", 11, 0, "PE"), ("ST", 0, 0, "DMA"), ("G", 9, 0, "S"), ("RC", 8, 0, "V"), ("Q", 3, 1, "V"), ("T", 12, 0, "PE"),
-    ("G", 10, 0, "S"), ("B", 13, 0, "V"), ("M", 12, 0, "PE"), ("G", 11, 0, "S"), ("B", 14, 0, "V"), ("ST", 1, 0, "DMA"),
-    ("B", 15, 0, "V"), ("D", 12, 0, "S"), ("T", 13, 0, "PE"), ("A", 16, 0, "V"), ("ST", 2, 0, "DMA"), ("T", 14, 0, "PE"),
-    ("G", 12, 0, "S"), ("M", 13, 0, "PE"), ("A", 17, 0, "V"), ("D", 13, 0, "S"), ("T", 15, 0, "PE"), ("D", 14, 0, "V"),
-    ("M", 14, 0, "PE"), ("G", 13, 0, "S"), ("M", 15, 0, "PE"), ("SQ", 9, 0, "S"), ("D", 15, 0, "S"), ("A", 18, 0, "V"),
-    ("M", 16, 0, "PE"), ("ST", 3, 0, "DMA"), ("M", 17, 0, "PE"), ("G", 14, 0, "S"), ("RC", 9, 0, "V"), ("A", 19, 0, "V"),
-    ("M", 18, 0, "PE"), ("G", 15, 0, "S"), ("G", 16, 0, "S"), ("M", 19, 0, "PE"), ("ST", 4, 0, "DMA"), ("Q", 4, 0, "V"),
-    ("G", 17, 0, "S"), ("M", 20, 0, "PE"), ("Q", 4, 1, "V"), ("SQ", 10, 0, "S"), ("M", 21, 0, "PE"), ("ST", 5, 0, "DMA"),
-    ("G", 18, 0, "S"), ("B", 16, 0, "V"), ("B", 17, 0, "V"), ("G", 19, 0, "S"), ("RC", 10, 0, "V"), ("G", 20, 0, "V"),
-    ("ST", 6, 0, "DMA"), ("M", 22, 0, "PE"), ("G", 21, 0, "S"), ("B", 18, 0, "V"), ("T", 16, 0, "PE"), ("B", 19, 0, "V"),
-    ("ST", 7, 0, "DMA"), ("G", 22, 0, "S"), ("A", 20, 0, "V"), ("T", 17, 0, "PE"), ("T", 18, 0, "PE"), ("D", 16, 0, "S"),
-    ("M", 23, 0, "PE"), ("A", 21, 0, "V"), ("D", 17, 0, "S"), ("M", 24, 0, "PE"), ("T", 19, 0, "PE"), ("D", 18, 0, "V"),
-    ("G", 23, 0, "S"), ("M", 25, 0, "PE"), ("SQ", 11, 0, "S"), ("A", 22, 0, "V"), ("G", 24, 0, "S"), ("M", 26, 0, "PE"),
-    ("ST", 8, 0, "DMA"), ("D", 19, 0, "S"), ("M", 27, 0, "PE"), ("RC", 11, 0, "V"), ("M", 28, 0, "PE"), ("A", 23, 0, "V"),
-    ("G", 25, 0, "S"), ("M", 29, 0, "PE"), ("G", 26, 0, "S"), ("Q", 5, 0, "V"), ("G", 27, 0, "S"), ("M", 30, 0, "PE"),
-    ("ST", 9, 0, "DMA"), ("Q", 5, 1, "V"), ("SQ", 12, 0, "S"), ("M", 31, 0, "PE"), ("G", 28, 0, "S"), ("B", 20, 0, "V"),
-    ("M", 32, 0, "PE"), ("ST", 10, 0, "DMA"), ("B", 21, 0, "V"), ("G", 29, 0, "S"), ("RC", 12, 0, "V"), ("A", 24, 0, "V"),
-    ("T", 20, 0, "PE"), ("G", 30, 0, "S"), ("T", 21, 0, "PE"), ("G", 31, 0, "S"), ("ST", 11, 0, "DMA"), ("B", 22, 0, "V"),
-    ("M", 33, 0, "PE"), ("D", 20, 0, "S"), ("B", 23, 0, "V"), ("A", 25, 0, "V"), ("ST", 12, 0, "DMA"), ("M", 34, 0, "PE"),
-    ("D", 21, 0, "S"), ("T", 22, 0, "PE"), ("G", 32, 0, "V"), ("ST", 13, 0, "DMA"), ("T", 23, 0, "PE"), ("G", 33, 0, "V"),
-    ("SQ", 13, 0, "S"), ("M", 35, 0, "PE"), ("G", 34, 0, "S"), ("A", 26, 0, "V"), ("ST", 14, 0, "DMA"), ("D", 22, 0, "S"),
-    ("M", 36, 0, "PE"), ("M", 37, 0, "PE"), ("RC", 13, 0, "V"), ("ST", 15, 0, "DMA"), ("D", 23, 0, "S"), ("A", 27, 0, "V"),
-    ("G", 35, 0, "S"), ("B", 24, 0, "V"), ("B", 25, 0, "V"), ("G", 36, 0, "S"), ("Q", 6, 0, "V"), ("T", 24, 0, "PE"),
-    ("SQ", 14, 0, "S"), ("G", 37, 0, "S"), ("Q", 6, 1, "V"), ("T", 25, 0, "PE"), ("RC", 14, 0, "V"), ("A", 28, 0, "V"),
-    ("D", 24, 0, "S"), ("M", 38, 0, "PE"), ("B", 26, 0, "V"), ("D", 25, 0, "S"), ("M", 39, 0, "PE"), ("B", 27, 0, "V"),
-    ("A", 29, 0, "V"), ("M", 40, 0, "PE"), ("G", 38, 0, "S"), ("T", 26, 0, "PE"), ("G", 39, 0, "S"), ("A", 30, 0, "V"),
-    ("T", 27, 0, "PE"), ("G", 40, 0, "S"), ("M", 41, 0, "PE"), ("SQ", 15, 0, "S"), ("ST", 16, 0, "DMA"), ("D", 26, 0, "V"),
-    ("D", 27, 0, "S"), ("M", 42, 0, "PE"), ("M", 43, 0, "PE"), ("RC", 15, 0, "V"), ("G", 41, 0, "S"), ("A", 31, 0, "V"),
-    ("M", 44, 0, "PE"), ("G", 42, 0, "S"), ("M", 45, 0, "PE"), ("G", 43, 0, "S"), ("ST", 17, 0, "DMA"), ("M", 46, 0, "PE"),
-    ("Q", 7, 0, "V"), ("G", 44, 0, "S"), ("M", 47, 0, "PE"), ("Q", 7, 1, "V"), ("SQ", 16, 0, "S"), ("ST", 18, 0, "DMA"),
-    ("M", 48, 0, "PE"), ("G", 45, 0, "S"), ("B", 28, 0, "V"), ("B", 29, 0, "V"), ("M", 49, 0, "PE"), ("G", 46, 0, "S"),
-    ("RC", 16, 0, "V"), ("B", 30, 0, "V"), ("T", 28, 0, "PE"), ("G", 47, 0, "S"), ("ST", 19, 0, "DMA"), ("B", 31, 0, "V"),
-    ("G", 48, 0, "V"), ("T", 29, 0, "PE"), ("G", 49, 0, "S"), ("T", 30, 0, "PE"), ("D", 28, 0, "S"), ("ST", 20, 0, "DMA"),
-    ("M", 50, 0, "PE"), ("D", 29, 0, "V"), ("D", 30, 0, "S"), ("M", 51, 0, "PE"), ("ST", 21, 0, "DMA"), ("T", 31, 0, "PE"),
-    ("G", 50, 0, "S"), ("Q", 8, 0, "V"), ("ST", 22, 0, "DMA"), ("M", 52, 0, "PE"), ("Q", 8, 1, "V"), ("G", 51, 0, "S"),
-    ("Q", 9, 0, "V"), ("M", 53, 0, "PE"), ("Q", 9, 1, "V"), ("ST", 23, 0, "DMA"), ("G", 52, 0, "S"), ("M", 54, 0, "PE"),
-    ("D", 31, 0, "V"), ("G", 53, 0, "S"), ("M", 55, 0, "PE"), ("M", 56, 0, "PE"), ("ST", 24, 0, "DMA"), ("G", 54, 0, "S"),
-    ("M", 57, 0, "PE"), ("ST", 25, 0, "DMA"), ("M", 58, 0, "PE"), ("G", 55, 0, "S"), ("Q", 10, 0, "V"), ("Q", 10, 1, "V"),
-    ("G", 56, 0, "S"), ("ST", 26, 0, "DMA"), ("M", 59, 0, "PE"), ("G", 57, 0, "V"), ("G", 58, 0, "S"), ("M", 60, 0, "PE"),
-    ("ST", 27, 0, "DMA"), ("M", 61, 0, "PE"), ("G", 59, 0, "S"), ("ST", 28, 0, "DMA"), ("M", 63, 0, "PE"), ("G", 60, 0, "S"),
-    ("M", 62, 0, "PE"), ("G", 61, 0, "S"), ("ST", 29, 0, "DMA"), ("M", 64, 0, "PE"), ("G", 63, 0, "S"), ("M", 65, 0, "PE"),
-    ("G", 62, 0, "S"), ("M", 66, 0, "PE"), ("M", 68, 0, "PE"), ("G", 64, 0, "V"), ("G", 65, 0, "S"), ("G", 66, 0, "S"),
-    ("G", 68, 0, "S"), ("M", 69, 0, "PE"), ("ST", 30, 0, "DMA"), ("M", 67, 0, "PE"), ("M", 70, 0, "PE"), ("M", 71, 0, "PE"),
-    ("ST", 31, 0, "DMA"), ("G", 69, 0, "S"), ("G", 67, 0, "S"), ("M", 73, 0, "PE"), ("G", 70, 0, "S"), ("ST", 32, 0, "DMA"),
-    ("M", 74, 0, "PE"), ("G", 71, 0, "S"), ("M", 72, 0, "PE"), ("ST", 33, 0, "DMA"), ("G", 73, 0, "S"), ("M", 75, 0, "PE"),
-    ("ST", 34, 0, "DMA"), ("G", 74, 0, "S"), ("M", 76, 0, "PE"), ("G", 72, 0, "S"), ("ST", 35, 0, "DMA"), ("M", 78, 0, "PE"),
-    ("M", 79, 0, "PE"), ("G", 75, 0, "S"), ("ST", 36, 0, "DMA"), ("G", 76, 0, "S"), ("G", 78, 0, "S"), ("G", 79, 0, "S"),
-    ("M", 77, 0, "PE"), ("ST", 37, 0, "DMA"), ("ST", 38, 0, "DMA"), ("G", 77, 0, "S"), ("ST", 39, 0, "DMA"), ("ST", 40, 0, "DMA"),
-    ("ST", 41, 0, "DMA"), ("ST", 42, 0, "DMA"), ("ST", 43, 0, "DMA"), ("ST", 44, 0, "DMA"), ("ST", 45, 0, "DMA"),
-)
+
+def column_chunks(first, end):
+    chunks = []
+    x = first
+    while x < end:
+        w = 4 if end - x >= 4 else (2 if end - x >= 2 else 1)
+        chunks.append((x, w))
+        x += w
+    return chunks
 
 
 def tile_generator_pb_t_kernel(tc, feat_gated, out):
@@ -108,161 +52,129 @@ def tile_generator_pb_t_kernel(tc, feat_gated, out):
         work = ctx.enter_context(tc.tile_pool(name="work", bufs=1))
         psum = ctx.enter_context(tc.psum_pool(name="psum", bufs=1))
 
+        xs = [xin.tile([P, TILES, K], BF16, name="x%d" % c) for c in range(COMMUNITIES)]
+        for c in range(COMMUNITIES):
+            for a0, n in (((0, 1), (1, 1), (2, 2), (4, 4)) if c == 0 else ((0, 4), (4, 4))):
+                src = feat_gated[c, P * a0 : P * (a0 + n), :].rearrange("(a p) k -> p a k", p=P)
+                nc.sync.dma_start(out=xs[c][:, a0 : a0 + n, :], in_=src)
+
         ident = const.tile([P, P], BF16, name="ident")
         make_identity(nc, ident[:])
 
-        xs = [xin.tile([P, 8, K], BF16, name="x%d" % c) for c in range(4)]
-        st = stat.tile([P, 32, 2, 6], F32, name="st")
-        mv = stat.tile([P, 32, 2], F32, name="mv")
-        sd = stat.tile([P, 32], F32, name="sd")
-        inv = stat.tile([P, 32], F32, name="inv")
-        nm = stat.tile([P, 32], F32, name="nm")
+        st = stat.tile([P, COMMUNITIES * TILES, 2, 6], F32, name="st")
+        mv = stat.tile([P, COMMUNITIES * TILES, 2], F32, name="mv")
+        sd = stat.tile([P, COMMUNITIES * TILES], F32, name="sd")
+        inv = stat.tile([P, COMMUNITIES * TILES], F32, name="inv")
 
-        piece_of = {}
-        for pi in range(len(PIECES)):
-            for j in PIECES[pi]:
-                piece_of[j] = pi
+        pieces = []
+        for c in range(COMMUNITIES):
+            for a0, n in (LAST_PIECES if c == COMMUNITIES - 1 else MID_PIECES):
+                pieces.append((c, a0, n))
+
         fns = {}
         pts = {}
-        grs = {}
         cds = {}
-        pms = {}
         ots = {}
+        count = {"group": 0}
+        done_cols = {}
 
-        def eng_of(e):
-            if e == "V":
-                return nc.vector
-            if e == "S":
-                return nc.scalar
-            return nc.gpsimd
-
-        def copy_on(e, dst, src):
-            if e == "V":
+        def copy_on(on_vector, dst, src):
+            if on_vector:
                 nc.vector.tensor_copy(out=dst, in_=src)
             else:
                 nc.scalar.copy(out=dst, in_=src)
 
-        def do_load(li):
-            t = LOADS[li]
-            c, a0 = divmod(t[0], 8)
-            n = len(t)
-            src = feat_gated[c, P * a0 : P * (a0 + n), :].rearrange("(a p) k -> p a k", p=P)
-            nc.sync.dma_start(out=xs[c][:, a0 : a0 + n, :], in_=src)
+        def statistics(pi):
+            c, a0, n = pieces[pi]
+            j0 = TILES * c + a0
+            for a in range(a0, a0 + n):
+                j = TILES * c + a
+                for h in range(2):
+                    nc.vector.bn_stats(out=st[:, j, h, :], in_=xs[c][:, a, 512 * h : 512 * h + 512])
+                nc.vector.bn_aggr(out=mv[:, j, :], in_=st[:, j, :, :].rearrange("p a b -> p (a b)"))
+            nc.scalar.activation(out=sd[:, j0 : j0 + n], in_=mv[:, j0 : j0 + n, 1], func=ACT.Sqrt, scale=float(K))
+            nc.vector.reciprocal(out=inv[:, j0 : j0 + n], in_=sd[:, j0 : j0 + n])
 
-        def do_stats(j):
-            c, a = divmod(j, 8)
-            for h in range(2):
-                nc.vector.bn_stats(out=st[:, j, h, :], in_=xs[c][:, a, 512 * h : 512 * h + 512])
-            nc.vector.bn_aggr(out=mv[:, j, :], in_=st[:, j, :, :].rearrange("p a b -> p (a b)"))
-
-        def do_norm(j, e):
-            c, a = divmod(j, 8)
-            fn = work.tile([P, K], BF16, name="fn", tag="fn%d" % (j % NF))
-            fns[j] = fn
-            if e == "V":
+        def quantised_piece(pi):
+            c, a0, n = pieces[pi]
+            for a in range(a0, a0 + n):
+                j = TILES * c + a
+                fns[j] = work.tile([P, K], BF16, name="fn", tag="fn%d" % (j % FN_BUFS))
                 nc.vector.tensor_scalar(
-                    out=fn[:], in0=xs[c][:, a, :], scalar1=mv[:, j, 0:1], scalar2=inv[:, j : j + 1],
+                    out=fns[j][:], in0=xs[c][:, a, :], scalar1=mv[:, j, 0:1], scalar2=inv[:, j : j + 1],
                     op0=ALU.subtract, op1=ALU.mult,
                 )
-            else:
-                nc.gpsimd.tensor_scalar(
-                    out=fn[:], in0=xs[c][:, a, :], scalar1=nm[:, j : j + 1], scalar2=inv[:, j : j + 1],
-                    op0=ALU.add, op1=ALU.mult,
+            for a in range(a0, a0 + n):
+                j = TILES * c + a
+                pts[j] = psum.tile([P, 8, P], BF16, name="pt", tag="pt%d" % (j % T_BANKS))
+                for b in range(8):
+                    nc.tensor.transpose(pts[j][:, b, :], fns[j][:, P * b : P * b + P], ident[:])
+            gr = work.tile([P, 2, P * n, 4], BF16, name="gr", tag="gr%d" % (pi % GR_BUFS), align_bytes=64)
+            for a in range(a0, a0 + n):
+                j = TILES * c + a
+                copy_on(
+                    (j >= 24 and j % 2 == 1) or (8 <= j < 24 and j % 4 == 3),
+                    gr[:, :, P * (a - a0) : P * (a - a0 + 1), :],
+                    pts[j][:].rearrange("p (g t) r -> p g r t", g=2),
                 )
-
-        def do_transposes(j):
-            pt = psum.tile([P, 8, P], BF16, name="pt", tag="pt%d" % (j % NPT))
-            pts[j] = pt
-            for b in range(8):
-                nc.tensor.transpose(pt[:, b, :], fns[j][:, P * b : P * b + P], ident[:])
-
-        def do_regroup(j, e):
-            pi = piece_of[j]
-            t = PIECES[pi]
-            if pi not in grs:
-                grs[pi] = work.tile([P, 2, P * len(t), 4], BF16, name="gr", tag="gr%d" % (pi % NG), align_bytes=64)
-            a = j - t[0]
-            copy_on(e, grs[pi][:, :, P * a : P * a + P, :], pts[j][:].rearrange("p (g t) r -> p g r t", g=2))
-
-        def do_quantise(pi, g):
-            t = PIECES[pi]
-            c, a0 = divmod(t[0], 8)
-            if c not in cds:
+            if a0 == 0:
                 cds[c] = (
                     work.tile([P, 2, ROWS], U32, name="codes", tag="codes%d" % (c % 2), align_bytes=64),
                     work.tile([P, 2, ROWS], U8, name="scales", tag="scales%d" % (c % 2), align_bytes=64),
                 )
-            cols = slice(P * a0, P * (a0 + len(t)))
-            nc.vector.quantize_mx(
-                out=cds[c][0][:, g, cols].bitcast(FP8X4),
-                scales=cds[c][1][:, g, cols],
-                in_=grs[pi][:, g, :, :].rearrange("p r t -> p (r t)"),
-            )
-
-        def do_matmul(gi):
-            c, i, x0, w, pi = GROUPS[gi]
-            pm = psum.tile([P, 512], F32, name="pm", tag="pm%d" % (gi % NPM))
-            pms[gi] = pm
-            codes, scales = cds[c]
+            cols = slice(P * a0, P * (a0 + n))
             for g in range(2):
-                nc.tensor.matmul_mx(
-                    out=pm[:, 0 : P * w],
-                    lhsT=codes[:, g, P * i : P * i + P].bitcast(FP8X4),
-                    lhsT_scale=scales[:, g, P * i : P * i + P],
-                    rhs=codes[:, g, P * x0 : P * (x0 + w)].bitcast(FP8X4),
-                    rhs_scale=scales[:, g, P * x0 : P * (x0 + w)],
-                    start=(g == 0),
-                    stop=(g == 1),
+                nc.vector.quantize_mx(
+                    out=cds[c][0][:, g, cols].bitcast(FP8X4),
+                    scales=cds[c][1][:, g, cols],
+                    in_=gr[:, g, :, :].rearrange("p r t -> p (r t)"),
                 )
 
-        def do_out(gi, e):
-            c, i, x0, w, pi = GROUPS[gi]
-            key = 8 * c + i
-            if key not in ots:
-                ots[key] = work.tile([P, ROWS], F32, name="ot", tag="ot%d" % (key % NO))
-            copy_on(e, ots[key][:, P * x0 : P * (x0 + w)], pms[gi][:, 0 : P * w])
-
-        def do_store(k):
-            c, i, x0, w = STORES[k]
-            nc.sync.dma_start(
-                out=out[c, P * i : P * i + P, P * x0 : P * (x0 + w)],
-                in_=ots[8 * c + i][:, P * x0 : P * (x0 + w)],
-            )
+        def products(pi):
+            c, a0, n = pieces[pi]
+            codes, scales = cds[c]
+            cuts = LAST_CUTS if c == COMMUNITIES - 1 else MID_CUTS
+            blocks = []
+            for i in range(a0, a0 + n):
+                blocks.extend([(i, x, w) for x, w in column_chunks(0, a0 + n)])
+            for i in range(a0):
+                blocks.extend([(i, x, w) for x, w in column_chunks(a0, a0 + n)])
+            for i, x, w in blocks:
+                gi = count["group"]
+                count["group"] = gi + 1
+                pm = psum.tile([P, 512], F32, name="pm", tag="pm%d" % (gi % MX_BANKS))
+                for g in range(2):
+                    nc.tensor.matmul_mx(
+                        out=pm[:, 0 : P * w],
+                        lhsT=codes[:, g, P * i : P * i + P].bitcast(FP8X4),
+                        lhsT_scale=scales[:, g, P * i : P * i + P],
+                        rhs=codes[:, g, P * x : P * (x + w)].bitcast(FP8X4),
+                        rhs_scale=scales[:, g, P * x : P * (x + w)],
+                        start=(g == 0),
+                        stop=(g == 1),
+                    )
+                key = TILES * c + i
+                if key not in ots:
+                    ots[key] = work.tile([P, ROWS], F32, name="ot", tag="ot%d" % (key % OT_BUFS))
+                    done_cols[key] = 0
+                copy_on((c == 3 and gi % 2 == 1) or (c == 2 and a0 >= 4 and gi % 3 == 2), ots[key][:, P * x : P * (x + w)], pm[:, 0 : P * w])
+                if (x + w) in cuts:
+                    x0 = done_cols[key]
+                    nc.sync.dma_start(
+                        out=out[c, P * i : P * i + P, P * x0 : P * (x + w)],
+                        in_=ots[key][:, P * x0 : P * (x + w)],
+                    )
+                    done_cols[key] = x + w
 
         def run():
-            for kind, idx, sub, e in SCHEDULE:
-                if kind == "L":
-                    do_load(idx)
-                elif kind == "A":
-                    do_stats(idx)
-                elif kind == "SQ":
-                    b = BATCHES[idx]
-                    nc.scalar.activation(out=sd[:, b[0] : b[-1] + 1], in_=mv[:, b[0] : b[-1] + 1, 1], func=ACT.Sqrt, scale=float(K))
-                elif kind == "RC":
-                    b = BATCHES[idx]
-                    nc.vector.reciprocal(out=inv[:, b[0] : b[-1] + 1], in_=sd[:, b[0] : b[-1] + 1])
-                elif kind == "NM":
-                    b = BATCHES[idx]
-                    nc.gpsimd.tensor_scalar(
-                        out=nm[:, b[0] : b[-1] + 1], in0=mv[:, b[0] : b[-1] + 1, 0], scalar1=-1.0, scalar2=0.0,
-                        op0=ALU.mult, op1=ALU.add,
-                    )
-                elif kind == "B":
-                    do_norm(idx, e)
-                elif kind == "T":
-                    do_transposes(idx)
-                elif kind == "D":
-                    do_regroup(idx, e)
-                elif kind == "Q":
-                    do_quantise(idx, sub)
-                elif kind == "M":
-                    do_matmul(idx)
-                elif kind == "G":
-                    do_out(idx, e)
-                elif kind == "ST":
-                    do_store(idx)
-                else:
-                    raise ValueError(kind)
+            for s in range(len(pieces) + LAG_BE):
+                for section in SECTIONS:
+                    if section == "stats" and s < len(pieces):
+                        statistics(s)
+                    if section == "quantise" and 0 <= s - LAG_F2 < len(pieces):
+                        quantised_piece(s - LAG_F2)
+                    if section == "products" and 0 <= s - LAG_BE < len(pieces):
+                        products(s - LAG_BE)
 
         if PINNED:
             with tc.manual_schedule():

@@ -15,22 +15,31 @@ ACT = mybir.ActivationFunctionType
 
 P = 128
 K = 1024
+K_PASS = 512
+PASSES = K // K_PASS
+PACK = 4
 ROWS = 1024
 COMMUNITIES = 4
-TILES = 8
-PINNED = False
+TILES = ROWS // P
+ALL_TILES = COMMUNITIES * TILES
+BN_CHUNK = 512
+BN_STATS_DIM = 6
+
 T_BANKS = 3
 MX_BANKS = 8 - T_BANKS
 FN_BUFS = 8
 GR_BUFS = 3
-OT_BUFS = 16
-MID_PIECES = ((0, 2), (2, 2), (4, 2), (6, 2))
-LAST_PIECES = ((0, 2), (2, 2), (4, 2), (6, 1), (7, 1))
-MID_CUTS = (8,)
-LAST_CUTS = (4, 7, 8)
-LAG_F2 = 2
-LAG_BE = 3
-SECTIONS = ("products", "quantise", "stats")
+OT_BUFS = 2 * TILES
+
+STEPS = ((2,), (2,), (2, 2), (2, 2), (2, 2), (2, 2), (2, 2), (4,), (2, 1, 1))
+BATCHES = (2, 2, 4, 4, 4, 4, 4, 4, 4)
+FIRST_STATS = 4
+FIRST_LEAD = 3
+STATS_LEAD = 6
+WHOLE_ROW_CUTS = (8,)
+LAST_COMMUNITY_CUTS = (4, 7, 8)
+FIRST_LOADS = ((0, 1), (1, 1), (2, 1), (3, 1), (4, 4))
+LOADS = ((0, 4), (4, 4))
 
 
 def column_chunks(first, end):
@@ -41,6 +50,15 @@ def column_chunks(first, end):
         chunks.append((x, w))
         x += w
     return chunks
+
+
+def regroups_on_vector(j):
+    u = j // 4
+    return u >= 2 and j == 4 * u + 3 - u % 2
+
+
+def result_copy_on_vector(c, first_tile, group):
+    return c == COMMUNITIES - 1 and first_tile >= TILES // 2 and group % 5 == 0
 
 
 def tile_generator_pb_t_kernel(tc, feat_gated, out):
@@ -54,130 +72,149 @@ def tile_generator_pb_t_kernel(tc, feat_gated, out):
 
         xs = [xin.tile([P, TILES, K], BF16, name="x%d" % c) for c in range(COMMUNITIES)]
         for c in range(COMMUNITIES):
-            for a0, n in (((0, 1), (1, 1), (2, 2), (4, 4)) if c == 0 else ((0, 4), (4, 4))):
+            for a0, n in FIRST_LOADS if c == 0 else LOADS:
                 src = feat_gated[c, P * a0 : P * (a0 + n), :].rearrange("(a p) k -> p a k", p=P)
                 nc.sync.dma_start(out=xs[c][:, a0 : a0 + n, :], in_=src)
 
         ident = const.tile([P, P], BF16, name="ident")
         make_identity(nc, ident[:])
 
-        st = stat.tile([P, COMMUNITIES * TILES, 2, 6], F32, name="st")
-        mv = stat.tile([P, COMMUNITIES * TILES, 2], F32, name="mv")
-        sd = stat.tile([P, COMMUNITIES * TILES], F32, name="sd")
-        inv = stat.tile([P, COMMUNITIES * TILES], F32, name="inv")
+        st = stat.tile([P, ALL_TILES, K // BN_CHUNK, BN_STATS_DIM], F32, name="st")
+        mv = stat.tile([P, ALL_TILES, 2], F32, name="mv")
+        sd = stat.tile([P, ALL_TILES], F32, name="sd")
+        inv = stat.tile([P, ALL_TILES], F32, name="inv")
 
-        pieces = []
-        for c in range(COMMUNITIES):
-            for a0, n in (LAST_PIECES if c == COMMUNITIES - 1 else MID_PIECES):
-                pieces.append((c, a0, n))
+        batch_size_at_end = {}
+        j = 0
+        for n in BATCHES:
+            batch_size_at_end[j + n - 1] = n
+            j += n
 
-        fns = {}
-        pts = {}
-        cds = {}
-        ots = {}
-        count = {"group": 0}
-        done_cols = {}
+        normalised = {}
+        transposed = {}
+        quantised = {}
+        results = {}
+        stored_up_to = {}
+        count = {"statistics": 0, "piece": 0, "group": 0}
 
-        def copy_on(on_vector, dst, src):
+        def copy_out_of_psum(on_vector, dst, src):
             if on_vector:
                 nc.vector.tensor_copy(out=dst, in_=src)
             else:
                 nc.scalar.copy(out=dst, in_=src)
 
-        def statistics(pi):
-            c, a0, n = pieces[pi]
-            j0 = TILES * c + a0
-            for a in range(a0, a0 + n):
-                j = TILES * c + a
-                for h in range(2):
-                    nc.vector.bn_stats(out=st[:, j, h, :], in_=xs[c][:, a, 512 * h : 512 * h + 512])
-                nc.vector.bn_aggr(out=mv[:, j, :], in_=st[:, j, :, :].rearrange("p a b -> p (a b)"))
-            nc.scalar.activation(out=sd[:, j0 : j0 + n], in_=mv[:, j0 : j0 + n, 1], func=ACT.Sqrt, scale=float(K))
-            nc.vector.reciprocal(out=inv[:, j0 : j0 + n], in_=sd[:, j0 : j0 + n])
+        def statistics(j):
+            c, a = divmod(j, TILES)
+            for h in range(K // BN_CHUNK):
+                nc.vector.bn_stats(out=st[:, j, h, :], in_=xs[c][:, a, BN_CHUNK * h : BN_CHUNK * (h + 1)])
+            nc.vector.bn_aggr(out=mv[:, j, :], in_=st[:, j, :, :].rearrange("p a b -> p (a b)"))
+            if j in batch_size_at_end:
+                j0 = j + 1 - batch_size_at_end[j]
+                nc.scalar.activation(out=sd[:, j0 : j + 1], in_=mv[:, j0 : j + 1, 1], func=ACT.Sqrt, scale=float(K))
+                nc.vector.reciprocal(out=inv[:, j0 : j + 1], in_=sd[:, j0 : j + 1])
 
-        def quantised_piece(pi):
-            c, a0, n = pieces[pi]
-            for a in range(a0, a0 + n):
-                j = TILES * c + a
-                fns[j] = work.tile([P, K], BF16, name="fn", tag="fn%d" % (j % FN_BUFS))
-                nc.vector.tensor_scalar(
-                    out=fns[j][:], in0=xs[c][:, a, :], scalar1=mv[:, j, 0:1], scalar2=inv[:, j : j + 1],
-                    op0=ALU.subtract, op1=ALU.mult,
+        def statistics_up_to(end):
+            while count["statistics"] < min(end, ALL_TILES):
+                statistics(count["statistics"])
+                count["statistics"] += 1
+
+        def normalise(j):
+            c, a = divmod(j, TILES)
+            normalised[j] = work.tile([P, K], BF16, name="fn", tag="fn%d" % (j % FN_BUFS))
+            nc.vector.tensor_scalar(
+                out=normalised[j][:], in0=xs[c][:, a, :], scalar1=mv[:, j, 0:1], scalar2=inv[:, j : j + 1],
+                op0=ALU.subtract, op1=ALU.mult,
+            )
+
+        def transposes(j):
+            transposed[j] = psum.tile([P, K // P, P], BF16, name="pt", tag="pt%d" % (j % T_BANKS))
+            for b in range(K // P):
+                nc.tensor.transpose(transposed[j][:, b, :], normalised[j][:, P * b : P * b + P], ident[:])
+
+        def regroup(j0, n):
+            pi = count["piece"]
+            count["piece"] = pi + 1
+            grouped = work.tile([P, PASSES, P * n, PACK], BF16, name="gr", tag="gr%d" % (pi % GR_BUFS), align_bytes=64)
+            for j in range(j0, j0 + n):
+                copy_out_of_psum(
+                    regroups_on_vector(j),
+                    grouped[:, :, P * (j - j0) : P * (j - j0 + 1), :],
+                    transposed[j][:].rearrange("p (g t) r -> p g r t", g=PASSES),
                 )
-            for a in range(a0, a0 + n):
-                j = TILES * c + a
-                pts[j] = psum.tile([P, 8, P], BF16, name="pt", tag="pt%d" % (j % T_BANKS))
-                for b in range(8):
-                    nc.tensor.transpose(pts[j][:, b, :], fns[j][:, P * b : P * b + P], ident[:])
-            gr = work.tile([P, 2, P * n, 4], BF16, name="gr", tag="gr%d" % (pi % GR_BUFS), align_bytes=64)
-            for a in range(a0, a0 + n):
-                j = TILES * c + a
-                copy_on(
-                    (j >= 24 and j % 2 == 1) or (8 <= j < 24 and j % 4 == 3),
-                    gr[:, :, P * (a - a0) : P * (a - a0 + 1), :],
-                    pts[j][:].rearrange("p (g t) r -> p g r t", g=2),
-                )
+            return grouped
+
+        def quantise(j0, n, grouped):
+            c, a0 = divmod(j0, TILES)
             if a0 == 0:
-                cds[c] = (
-                    work.tile([P, 2, ROWS], U32, name="codes", tag="codes%d" % (c % 2), align_bytes=64),
-                    work.tile([P, 2, ROWS], U8, name="scales", tag="scales%d" % (c % 2), align_bytes=64),
+                quantised[c] = (
+                    work.tile([P, PASSES, ROWS], U32, name="codes", tag="codes%d" % (c % 2), align_bytes=64),
+                    work.tile([P, PASSES, ROWS], U8, name="scales", tag="scales%d" % (c % 2), align_bytes=64),
                 )
             cols = slice(P * a0, P * (a0 + n))
-            for g in range(2):
+            for g in range(PASSES):
                 nc.vector.quantize_mx(
-                    out=cds[c][0][:, g, cols].bitcast(FP8X4),
-                    scales=cds[c][1][:, g, cols],
-                    in_=gr[:, g, :, :].rearrange("p r t -> p (r t)"),
+                    out=quantised[c][0][:, g, cols].bitcast(FP8X4),
+                    scales=quantised[c][1][:, g, cols],
+                    in_=grouped[:, g, :, :].rearrange("p r t -> p (r t)"),
                 )
 
-        def products(pi):
-            c, a0, n = pieces[pi]
-            codes, scales = cds[c]
-            cuts = LAST_CUTS if c == COMMUNITIES - 1 else MID_CUTS
+        def products(j0, n):
+            c, a0 = divmod(j0, TILES)
+            codes, scales = quantised[c]
+            cuts = LAST_COMMUNITY_CUTS if c == COMMUNITIES - 1 else WHOLE_ROW_CUTS
             blocks = []
             for i in range(a0, a0 + n):
                 blocks.extend([(i, x, w) for x, w in column_chunks(0, a0 + n)])
             for i in range(a0):
                 blocks.extend([(i, x, w) for x, w in column_chunks(a0, a0 + n)])
             for i, x, w in blocks:
-                gi = count["group"]
-                count["group"] = gi + 1
-                pm = psum.tile([P, 512], F32, name="pm", tag="pm%d" % (gi % MX_BANKS))
-                for g in range(2):
+                group = count["group"]
+                count["group"] = group + 1
+                acc = psum.tile([P, 512], F32, name="pm", tag="pm%d" % (group % MX_BANKS))
+                for g in range(PASSES):
                     nc.tensor.matmul_mx(
-                        out=pm[:, 0 : P * w],
+                        out=acc[:, 0 : P * w],
                         lhsT=codes[:, g, P * i : P * i + P].bitcast(FP8X4),
                         lhsT_scale=scales[:, g, P * i : P * i + P],
                         rhs=codes[:, g, P * x : P * (x + w)].bitcast(FP8X4),
                         rhs_scale=scales[:, g, P * x : P * (x + w)],
                         start=(g == 0),
-                        stop=(g == 1),
+                        stop=(g == PASSES - 1),
                     )
                 key = TILES * c + i
-                if key not in ots:
-                    ots[key] = work.tile([P, ROWS], F32, name="ot", tag="ot%d" % (key % OT_BUFS))
-                    done_cols[key] = 0
-                copy_on((c == 3 and gi % 2 == 1) or (c == 2 and a0 >= 4 and gi % 3 == 2), ots[key][:, P * x : P * (x + w)], pm[:, 0 : P * w])
+                if key not in results:
+                    results[key] = work.tile([P, ROWS], F32, name="ot", tag="ot%d" % (key % OT_BUFS))
+                    stored_up_to[key] = 0
+                copy_out_of_psum(
+                    result_copy_on_vector(c, a0, group), results[key][:, P * x : P * (x + w)], acc[:, 0 : P * w]
+                )
                 if (x + w) in cuts:
-                    x0 = done_cols[key]
+                    x0 = stored_up_to[key]
                     nc.sync.dma_start(
                         out=out[c, P * i : P * i + P, P * x0 : P * (x + w)],
-                        in_=ots[key][:, P * x0 : P * (x + w)],
+                        in_=results[key][:, P * x0 : P * (x + w)],
                     )
-                    done_cols[key] = x + w
+                    stored_up_to[key] = x + w
 
-        def run():
-            for s in range(len(pieces) + LAG_BE):
-                for section in SECTIONS:
-                    if section == "stats" and s < len(pieces):
-                        statistics(s)
-                    if section == "quantise" and 0 <= s - LAG_F2 < len(pieces):
-                        quantised_piece(s - LAG_F2)
-                    if section == "products" and 0 <= s - LAG_BE < len(pieces):
-                        products(s - LAG_BE)
-
-        if PINNED:
-            with tc.manual_schedule():
-                run()
-        else:
-            run()
+        statistics_up_to(FIRST_STATS)
+        first = 0
+        for pieces_of_step in STEPS:
+            size = sum(pieces_of_step)
+            target = first + size + (STATS_LEAD if first > 0 else FIRST_LEAD)
+            for j in range(first, first + size):
+                normalise(j)
+            for j in range(first, first + size):
+                transposes(j)
+            statistics_up_to(count["statistics"] + (target - count["statistics"]) // 2)
+            spans = []
+            j = first
+            for n in pieces_of_step:
+                spans.append((j, n, regroup(j, n)))
+                j += n
+            for j0, n, grouped in spans:
+                quantise(j0, n, grouped)
+                statistics_up_to(count["statistics"] + 1)
+            statistics_up_to(target)
+            for j0, n, grouped in spans:
+                products(j0, n)
+            first += size

@@ -25,21 +25,89 @@ ALL_TILES = COMMUNITIES * TILES
 BN_CHUNK = 512
 BN_STATS_DIM = 6
 
-T_BANKS = 3
+T_BANKS = 4
 MX_BANKS = 8 - T_BANKS
 FN_BUFS = 8
-GR_BUFS = 3
+GR_BUFS = 2
 OT_BUFS = 2 * TILES
 
-STEPS = ((2,), (2,), (2, 2), (2, 2), (2, 2), (2, 2), (2, 2), (4,), (2, 1, 1))
-BATCHES = (2, 2, 4, 4, 4, 4, 4, 4, 4)
-FIRST_STATS = 4
-FIRST_LEAD = 3
-STATS_LEAD = 6
+LOAD_SIZES = (1, 1, 1, 1, 4, 4, 4, 4, 4, 4, 4)
+BATCH_SIZES = (2, 2, 4, 4, 4, 4, 4, 4, 4)
+PIECE_SIZES = (2, 2, 2, 2, 2, 2, 2, 2, 2, 2, 2, 2, 4, 2, 1, 1)
 WHOLE_ROW_CUTS = (8,)
 LAST_COMMUNITY_CUTS = (4, 7, 8)
-FIRST_LOADS = ((0, 1), (1, 1), (2, 1), (3, 1), (4, 4))
-LOADS = ((0, 4), (4, 4))
+REGROUPED_BY_VECTOR = (11, 14, 19, 22, 26, 31)
+RESULTS_COPIED_BY_VECTOR = (67, 75, 79, 85, 95, 96)
+
+ORDER = (
+    ("load", 0), ("load", 1), ("load", 2), ("load", 3), ("load", 4), ("stats", 0), ("stats", 1), ("load", 5),
+    ("stats", 2), ("sqrt", 0), ("recip", 0), ("stats", 3), ("load", 6), ("norm", 0), ("sqrt", 1), ("norm", 1),
+    ("transp", 0), ("recip", 1), ("stats", 4), ("transp", 1), ("regroup", 0), ("norm", 2), ("regroup", 1),
+    ("norm", 3), ("transp", 2), ("load", 7), ("stats", 5), ("transp", 3), ("regroup", 2), ("quant", 0), ("quant", 1),
+    ("regroup", 3), ("stats", 6), ("mx", 0), ("load", 8), ("mx", 1), ("result", 0), ("quant", 2), ("result", 1),
+    ("quant", 3), ("stats", 7), ("mx", 2), ("mx", 3), ("result", 2), ("stats", 8), ("load", 9), ("mx", 4),
+    ("sqrt", 2), ("mx", 5), ("result", 3), ("result", 4), ("recip", 2), ("stats", 9), ("result", 5), ("norm", 4),
+    ("load", 10), ("norm", 5), ("transp", 4), ("norm", 6), ("norm", 7), ("transp", 5), ("regroup", 4), ("stats", 10),
+    ("transp", 6), ("transp", 7), ("regroup", 5), ("stats", 11), ("regroup", 6), ("quant", 4), ("quant", 5),
+    ("stats", 12), ("sqrt", 3), ("mx", 6), ("regroup", 7), ("mx", 7), ("recip", 3), ("mx", 8), ("stats", 13),
+    ("result", 6), ("mx", 9), ("result", 7), ("mx", 10), ("result", 8), ("mx", 11), ("quant", 6), ("quant", 7),
+    ("result", 9), ("mx", 12), ("norm", 8), ("result", 10), ("mx", 13), ("norm", 9), ("result", 11), ("mx", 14),
+    ("norm", 10), ("result", 12), ("norm", 11), ("result", 13), ("mx", 15), ("result", 14), ("stats", 14),
+    ("transp", 8), ("result", 15), ("transp", 9), ("regroup", 8), ("store", 0), ("stats", 15), ("transp", 10),
+    ("transp", 11), ("regroup", 9), ("stats", 16), ("mx", 16), ("mx", 17), ("sqrt", 4), ("regroup", 10), ("recip", 4),
+    ("regroup", 11), ("mx", 18), ("mx", 19), ("result", 16), ("quant", 8), ("quant", 9), ("result", 17), ("mx", 20),
+    ("quant", 10), ("result", 18), ("quant", 11), ("mx", 21), ("store", 1), ("result", 19), ("norm", 12), ("mx", 22),
+    ("result", 20), ("norm", 13), ("mx", 23), ("result", 21), ("norm", 14), ("mx", 24), ("result", 22), ("store", 2),
+    ("norm", 15), ("mx", 25), ("result", 23), ("transp", 12), ("stats", 17), ("result", 24), ("result", 25),
+    ("transp", 13), ("regroup", 12), ("store", 3), ("transp", 14), ("stats", 18), ("transp", 15), ("regroup", 13),
+    ("store", 4), ("mx", 26), ("regroup", 14), ("mx", 27), ("regroup", 15), ("store", 5), ("mx", 28), ("quant", 12),
+    ("mx", 29), ("quant", 13), ("result", 26), ("stats", 19), ("store", 6), ("result", 27), ("mx", 30),
+    ("result", 28), ("mx", 31), ("quant", 14), ("store", 7), ("sqrt", 5), ("mx", 32), ("result", 29), ("quant", 15),
+    ("result", 30), ("recip", 5), ("stats", 20), ("mx", 33), ("result", 31), ("mx", 34), ("result", 32), ("mx", 35),
+    ("norm", 16), ("result", 33), ("mx", 36), ("norm", 17), ("result", 34), ("mx", 37), ("norm", 18), ("result", 35),
+    ("mx", 38), ("norm", 19), ("result", 36), ("stats", 21), ("result", 37), ("transp", 16), ("result", 38),
+    ("transp", 17), ("regroup", 16), ("stats", 22), ("transp", 18), ("transp", 19), ("regroup", 17), ("mx", 39),
+    ("stats", 23), ("mx", 40), ("regroup", 18), ("mx", 41), ("regroup", 19), ("mx", 42), ("sqrt", 6), ("result", 39),
+    ("recip", 6), ("quant", 16), ("result", 40), ("mx", 43), ("store", 8), ("quant", 17), ("quant", 18),
+    ("result", 41), ("mx", 44), ("quant", 19), ("result", 42), ("norm", 20), ("mx", 45), ("store", 9), ("result", 43),
+    ("norm", 21), ("mx", 46), ("result", 44), ("norm", 22), ("mx", 47), ("result", 45), ("norm", 23), ("mx", 48),
+    ("result", 46), ("transp", 20), ("stats", 24), ("store", 10), ("result", 47), ("result", 48), ("transp", 21),
+    ("regroup", 20), ("store", 11), ("transp", 22), ("stats", 25), ("transp", 23), ("regroup", 21), ("mx", 49),
+    ("store", 12), ("regroup", 22), ("mx", 50), ("regroup", 23), ("mx", 51), ("store", 13), ("quant", 20), ("mx", 52),
+    ("quant", 21), ("result", 49), ("stats", 26), ("result", 50), ("mx", 53), ("store", 14), ("result", 51),
+    ("mx", 54), ("quant", 22), ("result", 52), ("mx", 55), ("quant", 23), ("store", 15), ("result", 53), ("mx", 56),
+    ("stats", 27), ("result", 54), ("mx", 57), ("result", 55), ("mx", 58), ("result", 56), ("mx", 59), ("stats", 28),
+    ("sqrt", 7), ("mx", 60), ("result", 57), ("result", 58), ("mx", 61), ("result", 59), ("mx", 62), ("recip", 7),
+    ("stats", 29), ("result", 60), ("result", 61), ("mx", 63), ("result", 62), ("mx", 64), ("result", 63),
+    ("norm", 24), ("norm", 25), ("mx", 65), ("result", 64), ("norm", 26), ("store", 16), ("mx", 66), ("norm", 27),
+    ("result", 65), ("transp", 24), ("stats", 30), ("result", 66), ("store", 17), ("transp", 25), ("regroup", 24),
+    ("transp", 26), ("stats", 31), ("transp", 27), ("store", 18), ("regroup", 25), ("mx", 67), ("regroup", 26),
+    ("mx", 68), ("mx", 69), ("sqrt", 8), ("regroup", 27), ("mx", 70), ("recip", 8), ("result", 67), ("norm", 28),
+    ("mx", 71), ("store", 19), ("result", 68), ("norm", 29), ("transp", 28), ("result", 69), ("quant", 24),
+    ("result", 70), ("transp", 29), ("result", 71), ("quant", 25), ("store", 20), ("regroup", 28), ("norm", 30),
+    ("norm", 31), ("transp", 30), ("store", 21), ("regroup", 29), ("transp", 31), ("mx", 72), ("store", 22),
+    ("regroup", 30), ("quant", 26), ("mx", 73), ("quant", 27), ("mx", 74), ("regroup", 31), ("store", 23),
+    ("result", 72), ("mx", 75), ("result", 73), ("mx", 76), ("quant", 28), ("store", 24), ("result", 74),
+    ("quant", 29), ("quant", 30), ("mx", 77), ("quant", 31), ("result", 75), ("store", 25), ("result", 76),
+    ("mx", 78), ("result", 77), ("store", 26), ("mx", 79), ("result", 78), ("mx", 80), ("store", 27), ("mx", 81),
+    ("result", 79), ("result", 80), ("mx", 82), ("result", 81), ("mx", 83), ("store", 28), ("result", 82), ("mx", 84),
+    ("result", 83), ("store", 29), ("mx", 85), ("result", 84), ("mx", 86), ("mx", 87), ("result", 85), ("result", 86),
+    ("mx", 88), ("store", 30), ("result", 87), ("mx", 90), ("result", 88), ("mx", 89), ("result", 90), ("mx", 91),
+    ("result", 89), ("store", 31), ("mx", 92), ("result", 91), ("mx", 94), ("result", 92), ("store", 32), ("mx", 93),
+    ("result", 94), ("store", 33), ("mx", 95), ("result", 93), ("mx", 96), ("mx", 98), ("store", 34), ("result", 95),
+    ("result", 96), ("result", 98), ("mx", 99), ("mx", 97), ("store", 35), ("result", 99), ("mx", 100),
+    ("result", 97), ("result", 100), ("mx", 101), ("store", 36), ("result", 101), ("store", 37), ("store", 38),
+    ("store", 39), ("store", 40), ("store", 41), ("store", 42), ("store", 43), ("store", 44), ("store", 45),
+)
+
+
+def spans(sizes):
+    pairs = []
+    first = 0
+    for n in sizes:
+        pairs.append((first, n))
+        first += n
+    return pairs
 
 
 def column_chunks(first, end):
@@ -52,17 +120,38 @@ def column_chunks(first, end):
     return chunks
 
 
-def regroups_on_vector(j):
-    u = j // 4
-    return u >= 2 and j == 4 * u + 3 - u % 2
-
-
-def result_copy_on_vector(c, first_tile, group):
-    return c == COMMUNITIES - 1 and first_tile >= TILES // 2 and group % 5 == 0
+def groups_and_stores(pieces):
+    groups = []
+    stores = []
+    stored_up_to = {}
+    for j0, n in pieces:
+        c, a0 = divmod(j0, TILES)
+        blocks = []
+        for i in range(a0, a0 + n):
+            blocks.extend([(i, x, w) for x, w in column_chunks(0, a0 + n)])
+        for i in range(a0):
+            blocks.extend([(i, x, w) for x, w in column_chunks(a0, a0 + n)])
+        for i, x, w in blocks:
+            groups.append((c, i, x, w))
+            waits = c == COMMUNITIES - 1 and i < TILES - 1
+            if (x + w) in (LAST_COMMUNITY_CUTS if waits else WHOLE_ROW_CUTS):
+                x0 = stored_up_to.get((c, i), 0)
+                stores.append((c, i, x0, x + w - x0))
+                stored_up_to[(c, i)] = x + w
+    return groups, stores
 
 
 def tile_generator_pb_t_kernel(tc, feat_gated, out):
     nc = tc.nc
+    loads = spans(LOAD_SIZES)
+    batches = spans(BATCH_SIZES)
+    pieces = spans(PIECE_SIZES)
+    groups, stores = groups_and_stores(pieces)
+    piece_of = {}
+    for pi in range(len(pieces)):
+        for j in range(pieces[pi][0], pieces[pi][0] + pieces[pi][1]):
+            piece_of[j] = pi
+
     with ExitStack() as ctx:
         const = ctx.enter_context(tc.tile_pool(name="const", bufs=1))
         xin = ctx.enter_context(tc.tile_pool(name="xin", bufs=1))
@@ -70,32 +159,21 @@ def tile_generator_pb_t_kernel(tc, feat_gated, out):
         work = ctx.enter_context(tc.tile_pool(name="work", bufs=1))
         psum = ctx.enter_context(tc.psum_pool(name="psum", bufs=1))
 
-        xs = [xin.tile([P, TILES, K], BF16, name="x%d" % c) for c in range(COMMUNITIES)]
-        for c in range(COMMUNITIES):
-            for a0, n in FIRST_LOADS if c == 0 else LOADS:
-                src = feat_gated[c, P * a0 : P * (a0 + n), :].rearrange("(a p) k -> p a k", p=P)
-                nc.sync.dma_start(out=xs[c][:, a0 : a0 + n, :], in_=src)
-
         ident = const.tile([P, P], BF16, name="ident")
         make_identity(nc, ident[:])
 
+        xs = [xin.tile([P, TILES, K], BF16, name="x%d" % c) for c in range(COMMUNITIES)]
         st = stat.tile([P, ALL_TILES, K // BN_CHUNK, BN_STATS_DIM], F32, name="st")
         mv = stat.tile([P, ALL_TILES, 2], F32, name="mv")
         sd = stat.tile([P, ALL_TILES], F32, name="sd")
         inv = stat.tile([P, ALL_TILES], F32, name="inv")
 
-        batch_size_at_end = {}
-        j = 0
-        for n in BATCHES:
-            batch_size_at_end[j + n - 1] = n
-            j += n
-
         normalised = {}
         transposed = {}
+        grouped = {}
         quantised = {}
+        sums = {}
         results = {}
-        stored_up_to = {}
-        count = {"statistics": 0, "piece": 0, "group": 0}
 
         def copy_out_of_psum(on_vector, dst, src):
             if on_vector:
@@ -103,22 +181,27 @@ def tile_generator_pb_t_kernel(tc, feat_gated, out):
             else:
                 nc.scalar.copy(out=dst, in_=src)
 
-        def statistics(j):
+        def load(k):
+            c, a0 = divmod(loads[k][0], TILES)
+            n = loads[k][1]
+            src = feat_gated[c, P * a0 : P * (a0 + n), :].rearrange("(a p) k -> p a k", p=P)
+            nc.sync.dma_start(out=xs[c][:, a0 : a0 + n, :], in_=src)
+
+        def stats(j):
             c, a = divmod(j, TILES)
             for h in range(K // BN_CHUNK):
-                nc.vector.bn_stats(out=st[:, j, h, :], in_=xs[c][:, a, BN_CHUNK * h : BN_CHUNK * (h + 1)])
+                nc.vector.bn_stats(out=st[:, j, h, :], in_=xs[c][:, a, BN_CHUNK * h : BN_CHUNK * h + BN_CHUNK])
             nc.vector.bn_aggr(out=mv[:, j, :], in_=st[:, j, :, :].rearrange("p a b -> p (a b)"))
-            if j in batch_size_at_end:
-                j0 = j + 1 - batch_size_at_end[j]
-                nc.scalar.activation(out=sd[:, j0 : j + 1], in_=mv[:, j0 : j + 1, 1], func=ACT.Sqrt, scale=float(K))
-                nc.vector.reciprocal(out=inv[:, j0 : j + 1], in_=sd[:, j0 : j + 1])
 
-        def statistics_up_to(end):
-            while count["statistics"] < min(end, ALL_TILES):
-                statistics(count["statistics"])
-                count["statistics"] += 1
+        def sqrt(b):
+            j0, n = batches[b]
+            nc.scalar.activation(out=sd[:, j0 : j0 + n], in_=mv[:, j0 : j0 + n, 1], func=ACT.Sqrt, scale=float(K))
 
-        def normalise(j):
+        def recip(b):
+            j0, n = batches[b]
+            nc.vector.reciprocal(out=inv[:, j0 : j0 + n], in_=sd[:, j0 : j0 + n])
+
+        def norm(j):
             c, a = divmod(j, TILES)
             normalised[j] = work.tile([P, K], BF16, name="fn", tag="fn%d" % (j % FN_BUFS))
             nc.vector.tensor_scalar(
@@ -126,95 +209,74 @@ def tile_generator_pb_t_kernel(tc, feat_gated, out):
                 op0=ALU.subtract, op1=ALU.mult,
             )
 
-        def transposes(j):
+        def transp(j):
             transposed[j] = psum.tile([P, K // P, P], BF16, name="pt", tag="pt%d" % (j % T_BANKS))
             for b in range(K // P):
                 nc.tensor.transpose(transposed[j][:, b, :], normalised[j][:, P * b : P * b + P], ident[:])
 
-        def regroup(j0, n):
-            pi = count["piece"]
-            count["piece"] = pi + 1
-            grouped = work.tile([P, PASSES, P * n, PACK], BF16, name="gr", tag="gr%d" % (pi % GR_BUFS), align_bytes=64)
-            for j in range(j0, j0 + n):
-                copy_out_of_psum(
-                    regroups_on_vector(j),
-                    grouped[:, :, P * (j - j0) : P * (j - j0 + 1), :],
-                    transposed[j][:].rearrange("p (g t) r -> p g r t", g=PASSES),
+        def regroup(j):
+            pi = piece_of[j]
+            j0, n = pieces[pi]
+            if pi not in grouped:
+                grouped[pi] = work.tile(
+                    [P, PASSES, P * n, PACK], BF16, name="gr", tag="gr%d" % (pi % GR_BUFS), align_bytes=64
                 )
-            return grouped
+            copy_out_of_psum(
+                j in REGROUPED_BY_VECTOR,
+                grouped[pi][:, :, P * (j - j0) : P * (j - j0) + P, :],
+                transposed[j][:].rearrange("p (g t) r -> p g r t", g=PASSES),
+            )
 
-        def quantise(j0, n, grouped):
+        def quant(piece_and_pass):
+            pi, g = divmod(piece_and_pass, PASSES)
+            j0, n = pieces[pi]
             c, a0 = divmod(j0, TILES)
-            if a0 == 0:
+            if c not in quantised:
                 quantised[c] = (
                     work.tile([P, PASSES, ROWS], U32, name="codes", tag="codes%d" % (c % 2), align_bytes=64),
                     work.tile([P, PASSES, ROWS], U8, name="scales", tag="scales%d" % (c % 2), align_bytes=64),
                 )
             cols = slice(P * a0, P * (a0 + n))
-            for g in range(PASSES):
-                nc.vector.quantize_mx(
-                    out=quantised[c][0][:, g, cols].bitcast(FP8X4),
-                    scales=quantised[c][1][:, g, cols],
-                    in_=grouped[:, g, :, :].rearrange("p r t -> p (r t)"),
-                )
+            nc.vector.quantize_mx(
+                out=quantised[c][0][:, g, cols].bitcast(FP8X4),
+                scales=quantised[c][1][:, g, cols],
+                in_=grouped[pi][:, g, :, :].rearrange("p r t -> p (r t)"),
+            )
 
-        def products(j0, n):
-            c, a0 = divmod(j0, TILES)
+        def mx(gi):
+            c, i, x, w = groups[gi]
+            sums[gi] = psum.tile([P, 512], F32, name="pm", tag="pm%d" % (gi % MX_BANKS))
             codes, scales = quantised[c]
-            cuts = LAST_COMMUNITY_CUTS if c == COMMUNITIES - 1 else WHOLE_ROW_CUTS
-            blocks = []
-            for i in range(a0, a0 + n):
-                blocks.extend([(i, x, w) for x, w in column_chunks(0, a0 + n)])
-            for i in range(a0):
-                blocks.extend([(i, x, w) for x, w in column_chunks(a0, a0 + n)])
-            for i, x, w in blocks:
-                group = count["group"]
-                count["group"] = group + 1
-                acc = psum.tile([P, 512], F32, name="pm", tag="pm%d" % (group % MX_BANKS))
-                for g in range(PASSES):
-                    nc.tensor.matmul_mx(
-                        out=acc[:, 0 : P * w],
-                        lhsT=codes[:, g, P * i : P * i + P].bitcast(FP8X4),
-                        lhsT_scale=scales[:, g, P * i : P * i + P],
-                        rhs=codes[:, g, P * x : P * (x + w)].bitcast(FP8X4),
-                        rhs_scale=scales[:, g, P * x : P * (x + w)],
-                        start=(g == 0),
-                        stop=(g == PASSES - 1),
-                    )
-                key = TILES * c + i
-                if key not in results:
-                    results[key] = work.tile([P, ROWS], F32, name="ot", tag="ot%d" % (key % OT_BUFS))
-                    stored_up_to[key] = 0
-                copy_out_of_psum(
-                    result_copy_on_vector(c, a0, group), results[key][:, P * x : P * (x + w)], acc[:, 0 : P * w]
+            for g in range(PASSES):
+                nc.tensor.matmul_mx(
+                    out=sums[gi][:, 0 : P * w],
+                    lhsT=codes[:, g, P * i : P * i + P].bitcast(FP8X4),
+                    lhsT_scale=scales[:, g, P * i : P * i + P],
+                    rhs=codes[:, g, P * x : P * (x + w)].bitcast(FP8X4),
+                    rhs_scale=scales[:, g, P * x : P * (x + w)],
+                    start=(g == 0),
+                    stop=(g == PASSES - 1),
                 )
-                if (x + w) in cuts:
-                    x0 = stored_up_to[key]
-                    nc.sync.dma_start(
-                        out=out[c, P * i : P * i + P, P * x0 : P * (x + w)],
-                        in_=results[key][:, P * x0 : P * (x + w)],
-                    )
-                    stored_up_to[key] = x + w
 
-        statistics_up_to(FIRST_STATS)
-        first = 0
-        for pieces_of_step in STEPS:
-            size = sum(pieces_of_step)
-            target = first + size + (STATS_LEAD if first > 0 else FIRST_LEAD)
-            for j in range(first, first + size):
-                normalise(j)
-            for j in range(first, first + size):
-                transposes(j)
-            statistics_up_to(count["statistics"] + (target - count["statistics"]) // 2)
-            spans = []
-            j = first
-            for n in pieces_of_step:
-                spans.append((j, n, regroup(j, n)))
-                j += n
-            for j0, n, grouped in spans:
-                quantise(j0, n, grouped)
-                statistics_up_to(count["statistics"] + 1)
-            statistics_up_to(target)
-            for j0, n, grouped in spans:
-                products(j0, n)
-            first += size
+        def result(gi):
+            c, i, x, w = groups[gi]
+            key = TILES * c + i
+            if key not in results:
+                results[key] = work.tile([P, ROWS], F32, name="ot", tag="ot%d" % (key % OT_BUFS))
+            copy_out_of_psum(
+                gi in RESULTS_COPIED_BY_VECTOR, results[key][:, P * x : P * (x + w)], sums[gi][:, 0 : P * w]
+            )
+
+        def store(k):
+            c, i, x, w = stores[k]
+            nc.sync.dma_start(
+                out=out[c, P * i : P * i + P, P * x : P * (x + w)],
+                in_=results[TILES * c + i][:, P * x : P * (x + w)],
+            )
+
+        actions = {
+            "load": load, "stats": stats, "sqrt": sqrt, "recip": recip, "norm": norm, "transp": transp,
+            "regroup": regroup, "quant": quant, "mx": mx, "result": result, "store": store,
+        }
+        for kind, index in ORDER:
+            actions[kind](index)

@@ -159,7 +159,7 @@ def tile_generator_pb_t_kernel(tc, feat_gated, out):
         work = ctx.enter_context(tc.tile_pool(name="work", bufs=1))
         psum = ctx.enter_context(tc.psum_pool(name="psum", bufs=1))
 
-        ident = const.tile([P, P], BF16, name="ident")
+        ident = const.tile([P, P], F32, name="ident")
         make_identity(nc, ident[:])
 
         xs = [xin.tile([P, TILES, K], BF16, name="x%d" % c) for c in range(COMMUNITIES)]
@@ -210,21 +210,22 @@ def tile_generator_pb_t_kernel(tc, feat_gated, out):
             )
 
         def transp(j):
-            transposed[j] = psum.tile([P, K // P, P], BF16, name="pt", tag="pt%d" % (j % T_BANKS))
-            for b in range(K // P):
-                nc.tensor.transpose(transposed[j][:, b, :], normalised[j][:, P * b : P * b + P], ident[:])
+            transposed[j] = psum.tile([P, K // 2 // P, P], F32, name="pt", tag="pt%d" % (j % T_BANKS))
+            words = normalised[j][:].bitcast(F32)
+            for b in range(K // 2 // P):
+                nc.tensor.transpose(transposed[j][:, b, :], words[:, P * b : P * b + P], ident[:])
 
         def regroup(j):
             pi = piece_of[j]
             j0, n = pieces[pi]
             if pi not in grouped:
                 grouped[pi] = work.tile(
-                    [P, PASSES, P * n, PACK], BF16, name="gr", tag="gr%d" % (pi % GR_BUFS), align_bytes=64
+                    [P, PASSES, P * n, PACK // 2], F32, name="gr", tag="gr%d" % (pi % GR_BUFS), align_bytes=64
                 )
             copy_out_of_psum(
                 j in REGROUPED_BY_VECTOR,
                 grouped[pi][:, :, P * (j - j0) : P * (j - j0) + P, :],
-                transposed[j][:].rearrange("p (g t) r -> p g r t", g=PASSES),
+                transposed[j][:].rearrange("p (g u) r -> p g r u", g=PASSES),
             )
 
         def quant(piece_and_pass):
@@ -240,7 +241,7 @@ def tile_generator_pb_t_kernel(tc, feat_gated, out):
             nc.vector.quantize_mx(
                 out=quantised[c][0][:, g, cols].bitcast(FP8X4),
                 scales=quantised[c][1][:, g, cols],
-                in_=grouped[pi][:, g, :, :].rearrange("p r t -> p (r t)"),
+                in_=grouped[pi][:, g, :, :].rearrange("p r u -> p (r u)").bitcast(BF16),
             )
 
         def mx(gi):

@@ -17,88 +17,24 @@ P = 128
 K = 1024
 K_PASS = 512
 PASSES = K // K_PASS
-PACK = 4
 ROWS = 1024
 COMMUNITIES = 4
 TILES = ROWS // P
 ALL_TILES = COMMUNITIES * TILES
 BN_CHUNK = 512
 BN_STATS_DIM = 6
+BANK = 512
+WORDS = K // 2
 
-T_BANKS = 4
+T_BANKS = 2
 MX_BANKS = 8 - T_BANKS
-FN_BUFS = 8
-GR_BUFS = 2
-OT_BUFS = 2 * TILES
 
-LOAD_SIZES = (1, 1, 1, 1, 4, 4, 4, 4, 4, 4, 4)
-BATCH_SIZES = (2, 2, 4, 4, 4, 4, 4, 4, 4)
-PIECE_SIZES = (2, 2, 2, 2, 2, 2, 2, 2, 2, 2, 2, 2, 4, 2, 1, 1)
-WHOLE_ROW_CUTS = (8,)
-LAST_COMMUNITY_CUTS = (4, 7, 8)
-REGROUPED_BY_VECTOR = (11, 14, 19, 22, 26, 31)
-RESULTS_COPIED_BY_VECTOR = (67, 75, 79, 85, 95, 96)
-
-ORDER = (
-    ("load", 0), ("load", 1), ("load", 2), ("load", 3), ("load", 4), ("stats", 0), ("stats", 1), ("load", 5),
-    ("stats", 2), ("sqrt", 0), ("recip", 0), ("stats", 3), ("load", 6), ("norm", 0), ("sqrt", 1), ("norm", 1),
-    ("transp", 0), ("recip", 1), ("stats", 4), ("transp", 1), ("regroup", 0), ("norm", 2), ("regroup", 1),
-    ("norm", 3), ("transp", 2), ("load", 7), ("stats", 5), ("transp", 3), ("regroup", 2), ("quant", 0), ("quant", 1),
-    ("regroup", 3), ("stats", 6), ("mx", 0), ("load", 8), ("mx", 1), ("result", 0), ("quant", 2), ("result", 1),
-    ("quant", 3), ("stats", 7), ("mx", 2), ("mx", 3), ("result", 2), ("stats", 8), ("load", 9), ("mx", 4),
-    ("sqrt", 2), ("mx", 5), ("result", 3), ("result", 4), ("recip", 2), ("stats", 9), ("result", 5), ("norm", 4),
-    ("load", 10), ("norm", 5), ("transp", 4), ("norm", 6), ("norm", 7), ("transp", 5), ("regroup", 4), ("stats", 10),
-    ("transp", 6), ("transp", 7), ("regroup", 5), ("stats", 11), ("regroup", 6), ("quant", 4), ("quant", 5),
-    ("stats", 12), ("sqrt", 3), ("mx", 6), ("regroup", 7), ("mx", 7), ("recip", 3), ("mx", 8), ("stats", 13),
-    ("result", 6), ("mx", 9), ("result", 7), ("mx", 10), ("result", 8), ("mx", 11), ("quant", 6), ("quant", 7),
-    ("result", 9), ("mx", 12), ("norm", 8), ("result", 10), ("mx", 13), ("norm", 9), ("result", 11), ("mx", 14),
-    ("norm", 10), ("result", 12), ("norm", 11), ("result", 13), ("mx", 15), ("result", 14), ("stats", 14),
-    ("transp", 8), ("result", 15), ("transp", 9), ("regroup", 8), ("store", 0), ("stats", 15), ("transp", 10),
-    ("transp", 11), ("regroup", 9), ("stats", 16), ("mx", 16), ("mx", 17), ("sqrt", 4), ("regroup", 10), ("recip", 4),
-    ("regroup", 11), ("mx", 18), ("mx", 19), ("result", 16), ("quant", 8), ("quant", 9), ("result", 17), ("mx", 20),
-    ("quant", 10), ("result", 18), ("quant", 11), ("mx", 21), ("store", 1), ("result", 19), ("norm", 12), ("mx", 22),
-    ("result", 20), ("norm", 13), ("mx", 23), ("result", 21), ("norm", 14), ("mx", 24), ("result", 22), ("store", 2),
-    ("norm", 15), ("mx", 25), ("result", 23), ("transp", 12), ("stats", 17), ("result", 24), ("result", 25),
-    ("transp", 13), ("regroup", 12), ("store", 3), ("transp", 14), ("stats", 18), ("transp", 15), ("regroup", 13),
-    ("store", 4), ("mx", 26), ("regroup", 14), ("mx", 27), ("regroup", 15), ("store", 5), ("mx", 28), ("quant", 12),
-    ("mx", 29), ("quant", 13), ("result", 26), ("stats", 19), ("store", 6), ("result", 27), ("mx", 30),
-    ("result", 28), ("mx", 31), ("quant", 14), ("store", 7), ("sqrt", 5), ("mx", 32), ("result", 29), ("quant", 15),
-    ("result", 30), ("recip", 5), ("stats", 20), ("mx", 33), ("result", 31), ("mx", 34), ("result", 32), ("mx", 35),
-    ("norm", 16), ("result", 33), ("mx", 36), ("norm", 17), ("result", 34), ("mx", 37), ("norm", 18), ("result", 35),
-    ("mx", 38), ("norm", 19), ("result", 36), ("stats", 21), ("result", 37), ("transp", 16), ("result", 38),
-    ("transp", 17), ("regroup", 16), ("stats", 22), ("transp", 18), ("transp", 19), ("regroup", 17), ("mx", 39),
-    ("stats", 23), ("mx", 40), ("regroup", 18), ("mx", 41), ("regroup", 19), ("mx", 42), ("sqrt", 6), ("result", 39),
-    ("recip", 6), ("quant", 16), ("result", 40), ("mx", 43), ("store", 8), ("quant", 17), ("quant", 18),
-    ("result", 41), ("mx", 44), ("quant", 19), ("result", 42), ("norm", 20), ("mx", 45), ("store", 9), ("result", 43),
-    ("norm", 21), ("mx", 46), ("result", 44), ("norm", 22), ("mx", 47), ("result", 45), ("norm", 23), ("mx", 48),
-    ("result", 46), ("transp", 20), ("stats", 24), ("store", 10), ("result", 47), ("result", 48), ("transp", 21),
-    ("regroup", 20), ("store", 11), ("transp", 22), ("stats", 25), ("transp", 23), ("regroup", 21), ("mx", 49),
-    ("store", 12), ("regroup", 22), ("mx", 50), ("regroup", 23), ("mx", 51), ("store", 13), ("quant", 20), ("mx", 52),
-    ("quant", 21), ("result", 49), ("stats", 26), ("result", 50), ("mx", 53), ("store", 14), ("result", 51),
-    ("mx", 54), ("quant", 22), ("result", 52), ("mx", 55), ("quant", 23), ("store", 15), ("result", 53), ("mx", 56),
-    ("stats", 27), ("result", 54), ("mx", 57), ("result", 55), ("mx", 58), ("result", 56), ("mx", 59), ("stats", 28),
-    ("sqrt", 7), ("mx", 60), ("result", 57), ("result", 58), ("mx", 61), ("result", 59), ("mx", 62), ("recip", 7),
-    ("stats", 29), ("result", 60), ("result", 61), ("mx", 63), ("result", 62), ("mx", 64), ("result", 63),
-    ("norm", 24), ("norm", 25), ("mx", 65), ("result", 64), ("norm", 26), ("store", 16), ("mx", 66), ("norm", 27),
-    ("result", 65), ("transp", 24), ("stats", 30), ("result", 66), ("store", 17), ("transp", 25), ("regroup", 24),
-    ("transp", 26), ("stats", 31), ("transp", 27), ("store", 18), ("regroup", 25), ("mx", 67), ("regroup", 26),
-    ("mx", 68), ("mx", 69), ("sqrt", 8), ("regroup", 27), ("mx", 70), ("recip", 8), ("result", 67), ("norm", 28),
-    ("mx", 71), ("store", 19), ("result", 68), ("norm", 29), ("transp", 28), ("result", 69), ("quant", 24),
-    ("result", 70), ("transp", 29), ("result", 71), ("quant", 25), ("store", 20), ("regroup", 28), ("norm", 30),
-    ("norm", 31), ("transp", 30), ("store", 21), ("regroup", 29), ("transp", 31), ("mx", 72), ("store", 22),
-    ("regroup", 30), ("quant", 26), ("mx", 73), ("quant", 27), ("mx", 74), ("regroup", 31), ("store", 23),
-    ("result", 72), ("mx", 75), ("result", 73), ("mx", 76), ("quant", 28), ("store", 24), ("result", 74),
-    ("quant", 29), ("quant", 30), ("mx", 77), ("quant", 31), ("result", 75), ("store", 25), ("result", 76),
-    ("mx", 78), ("result", 77), ("store", 26), ("mx", 79), ("result", 78), ("mx", 80), ("store", 27), ("mx", 81),
-    ("result", 79), ("result", 80), ("mx", 82), ("result", 81), ("mx", 83), ("store", 28), ("result", 82), ("mx", 84),
-    ("result", 83), ("store", 29), ("mx", 85), ("result", 84), ("mx", 86), ("mx", 87), ("result", 85), ("result", 86),
-    ("mx", 88), ("store", 30), ("result", 87), ("mx", 90), ("result", 88), ("mx", 89), ("result", 90), ("mx", 91),
-    ("result", 89), ("store", 31), ("mx", 92), ("result", 91), ("mx", 94), ("result", 92), ("store", 32), ("mx", 93),
-    ("result", 94), ("store", 33), ("mx", 95), ("result", 93), ("mx", 96), ("mx", 98), ("store", 34), ("result", 95),
-    ("result", 96), ("result", 98), ("mx", 99), ("mx", 97), ("store", 35), ("result", 99), ("mx", 100),
-    ("result", 97), ("result", 100), ("mx", 101), ("store", 36), ("result", 101), ("store", 37), ("store", 38),
-    ("store", 39), ("store", 40), ("store", 41), ("store", 42), ("store", 43), ("store", 44), ("store", 45),
-)
+LOAD_SIZES = (1, 1, 2, 2, 2, 4, 4, 4, 4, 4, 4)
+PIECE_SIZES = (2,) * 16
+COLUMN_TILES_A_STEP = 16
+LAST_STEPS = 2
+FINE_STORES = 3
+STATS_ON_SCALAR = ()
 
 
 def spans(sizes):
@@ -110,127 +46,117 @@ def spans(sizes):
     return pairs
 
 
-def column_chunks(first, end):
-    chunks = []
-    x = first
-    while x < end:
-        w = 4 if end - x >= 4 else (2 if end - x >= 2 else 1)
-        chunks.append((x, w))
+def bank_fills(c, i0, i1, x0, x1):
+    fills = []
+    x = x0
+    while x < x1:
+        w = 4 if x1 - x >= 4 else (2 if x1 - x >= 2 else 1)
+        i = i0
+        while i < i1:
+            h = min(4 // w, i1 - i)
+            fills.append((c, i, h, x, w))
+            i += h
         x += w
-    return chunks
+    return fills
 
 
-def groups_and_stores(pieces):
-    groups = []
-    stores = []
-    stored_up_to = {}
-    for j0, n in pieces:
-        c, a0 = divmod(j0, TILES)
-        blocks = []
-        for i in range(a0, a0 + n):
-            blocks.extend([(i, x, w) for x, w in column_chunks(0, a0 + n)])
-        for i in range(a0):
-            blocks.extend([(i, x, w) for x, w in column_chunks(a0, a0 + n)])
-        for i, x, w in blocks:
-            groups.append((c, i, x, w))
-            waits = c == COMMUNITIES - 1 and i < TILES - 1
-            if (x + w) in (LAST_COMMUNITY_CUTS if waits else WHOLE_ROW_CUTS):
-                x0 = stored_up_to.get((c, i), 0)
-                stores.append((c, i, x0, x + w - x0))
-                stored_up_to[(c, i)] = x + w
-    return groups, stores
+def fills_of(piece, fine):
+    j0, n = piece
+    c, a0 = divmod(j0, TILES)
+    items = []
+    for i0, i1, x0, x1 in ((0, a0, a0, a0 + n), (a0, a0 + n, 0, a0 + n)):
+        fills = bank_fills(c, i0, i1, x0, x1)
+        if fine:
+            items.extend([(f, (c, f[1], f[1] + f[2], f[3], f[3] + f[4])) for f in fills])
+        elif fills:
+            items.extend([(f,) for f in fills[:-1]])
+            items.append((fills[-1], (c, i0, i1, x0, x1)))
+    return items
 
 
 def tile_generator_pb_t_kernel(tc, feat_gated, out):
     nc = tc.nc
-    loads = spans(LOAD_SIZES)
-    batches = spans(BATCH_SIZES)
     pieces = spans(PIECE_SIZES)
-    groups, stores = groups_and_stores(pieces)
-    piece_of = {}
-    for pi in range(len(pieces)):
-        for j in range(pieces[pi][0], pieces[pi][0] + pieces[pi][1]):
-            piece_of[j] = pi
 
     with ExitStack() as ctx:
         const = ctx.enter_context(tc.tile_pool(name="const", bufs=1))
-        xin = ctx.enter_context(tc.tile_pool(name="xin", bufs=1))
-        stat = ctx.enter_context(tc.tile_pool(name="stat", bufs=1))
+        keep = ctx.enter_context(tc.tile_pool(name="keep", bufs=1))
         work = ctx.enter_context(tc.tile_pool(name="work", bufs=1))
         psum = ctx.enter_context(tc.psum_pool(name="psum", bufs=1))
+        ctx.enter_context(tc.manual_schedule())
 
         ident = const.tile([P, P], F32, name="ident")
         make_identity(nc, ident[:])
+        minus_half = const.tile([P, 4], F32, name="minus_half")
+        nc.gpsimd.memset(minus_half[:], -0.5)
 
-        xs = [xin.tile([P, TILES, K], BF16, name="x%d" % c) for c in range(COMMUNITIES)]
-        st = stat.tile([P, ALL_TILES, K // BN_CHUNK, BN_STATS_DIM], F32, name="st")
-        mv = stat.tile([P, ALL_TILES, 2], F32, name="mv")
-        sd = stat.tile([P, ALL_TILES], F32, name="sd")
-        inv = stat.tile([P, ALL_TILES], F32, name="inv")
+        xs = [keep.tile([P, TILES, K], BF16, name="x%d" % c) for c in range(COMMUNITIES)]
+        results = [keep.tile([P, TILES, ROWS], F32, name="r%d" % c) for c in range(COMMUNITIES)]
+        st = keep.tile([P, ALL_TILES, K // BN_CHUNK, BN_STATS_DIM], F32, name="st")
+        mv = keep.tile([P, ALL_TILES, 2], F32, name="mv")
+        ssq = keep.tile([P, ALL_TILES], F32, name="ssq")
+        sd = keep.tile([P, ALL_TILES], F32, name="sd")
+        inv = keep.tile([P, ALL_TILES], F32, name="inv")
 
         normalised = {}
-        transposed = {}
         grouped = {}
         quantised = {}
-        sums = {}
-        results = {}
+        fill_count = [0]
 
-        def copy_out_of_psum(on_vector, dst, src):
-            if on_vector:
-                nc.vector.tensor_copy(out=dst, in_=src)
-            else:
-                nc.scalar.copy(out=dst, in_=src)
-
-        def load(k):
-            c, a0 = divmod(loads[k][0], TILES)
-            n = loads[k][1]
+        for j0, n in spans(LOAD_SIZES):
+            c, a0 = divmod(j0, TILES)
             src = feat_gated[c, P * a0 : P * (a0 + n), :].rearrange("(a p) k -> p a k", p=P)
             nc.sync.dma_start(out=xs[c][:, a0 : a0 + n, :], in_=src)
 
-        def stats(j):
+        def stats_half(j, h):
             c, a = divmod(j, TILES)
-            for h in range(K // BN_CHUNK):
-                nc.vector.bn_stats(out=st[:, j, h, :], in_=xs[c][:, a, BN_CHUNK * h : BN_CHUNK * h + BN_CHUNK])
+            nc.vector.bn_stats(out=st[:, j, h, :], in_=xs[c][:, a, BN_CHUNK * h : BN_CHUNK * h + BN_CHUNK])
+
+        def stats_on_scalar(j):
+            c, a = divmod(j, TILES)
+            for func, scale, bias, total in (
+                (ACT.Copy, 1.0 / K, 0.0, mv[:, j, 0:1]),
+                (ACT.Square, -1.0, mv[:, j, 0:1], ssq[:, j : j + 1]),
+            ):
+                unused = work.tile([P, K], BF16, name="unused", tag="unused")
+                nc.scalar.activation(out=unused[:], in_=xs[c][:, a, :], func=func, scale=scale, bias=bias, accum_out=total)
+            nc.scalar.activation(out=mv[:, j, 1:2], in_=ssq[:, j : j + 1], func=ACT.Copy, scale=1.0 / K)
+
+        def aggregate(j):
             nc.vector.bn_aggr(out=mv[:, j, :], in_=st[:, j, :, :].rearrange("p a b -> p (a b)"))
 
-        def sqrt(b):
-            j0, n = batches[b]
-            nc.scalar.activation(out=sd[:, j0 : j0 + n], in_=mv[:, j0 : j0 + n, 1], func=ACT.Sqrt, scale=float(K))
-
-        def recip(b):
-            j0, n = batches[b]
-            nc.vector.reciprocal(out=inv[:, j0 : j0 + n], in_=sd[:, j0 : j0 + n])
+        def invert(piece):
+            j0, n = piece
+            nc.gpsimd.tensor_tensor(
+                out=sd[:, j0 : j0 + n], in0=mv[:, j0 : j0 + n, 1], in1=minus_half[:, 0:n], op=ALU.pow
+            )
+            nc.gpsimd.tensor_scalar(
+                out=inv[:, j0 : j0 + n], in0=sd[:, j0 : j0 + n], scalar1=K ** -0.5, scalar2=0.0, op0=ALU.mult, op1=ALU.add
+            )
 
         def norm(j):
             c, a = divmod(j, TILES)
-            normalised[j] = work.tile([P, K], BF16, name="fn", tag="fn%d" % (j % FN_BUFS))
+            normalised[j] = work.tile([P, K], BF16, name="fn", tag="fn%d" % (j % 4))
             nc.vector.tensor_scalar(
                 out=normalised[j][:], in0=xs[c][:, a, :], scalar1=mv[:, j, 0:1], scalar2=inv[:, j : j + 1],
                 op0=ALU.subtract, op1=ALU.mult,
             )
 
-        def transp(j):
-            transposed[j] = psum.tile([P, K // 2 // P, P], F32, name="pt", tag="pt%d" % (j % T_BANKS))
-            words = normalised[j][:].bitcast(F32)
-            for b in range(K // 2 // P):
-                nc.tensor.transpose(transposed[j][:, b, :], words[:, P * b : P * b + P], ident[:])
-
-        def regroup(j):
-            pi = piece_of[j]
-            j0, n = pieces[pi]
-            if pi not in grouped:
-                grouped[pi] = work.tile(
-                    [P, PASSES, P * n, PACK // 2], F32, name="gr", tag="gr%d" % (pi % GR_BUFS), align_bytes=64
+        def transpose_and_regroup(piece, i):
+            j0, n = piece
+            grouped[i] = work.tile([P, PASSES, P * n, 2], F32, name="gr", tag="gr%d" % (i % 2), align_bytes=64)
+            for j in range(j0, j0 + n):
+                bank = psum.tile([P, WORDS // P, P], F32, name="pt", tag="pt%d" % (j % T_BANKS))
+                words = normalised[j][:].bitcast(F32)
+                for b in range(WORDS // P):
+                    nc.tensor.transpose(bank[:, b, :], words[:, P * b : P * b + P], ident[:])
+                nc.scalar.copy(
+                    out=grouped[i][:, :, P * (j - j0) : P * (j - j0) + P, :],
+                    in_=bank[:].rearrange("p (g u) r -> p g r u", g=PASSES),
                 )
-            copy_out_of_psum(
-                j in REGROUPED_BY_VECTOR,
-                grouped[pi][:, :, P * (j - j0) : P * (j - j0) + P, :],
-                transposed[j][:].rearrange("p (g u) r -> p g r u", g=PASSES),
-            )
 
-        def quant(piece_and_pass):
-            pi, g = divmod(piece_and_pass, PASSES)
-            j0, n = pieces[pi]
+        def quantise(piece, i, g):
+            j0, n = piece
             c, a0 = divmod(j0, TILES)
             if c not in quantised:
                 quantised[c] = (
@@ -241,43 +167,100 @@ def tile_generator_pb_t_kernel(tc, feat_gated, out):
             nc.vector.quantize_mx(
                 out=quantised[c][0][:, g, cols].bitcast(FP8X4),
                 scales=quantised[c][1][:, g, cols],
-                in_=grouped[pi][:, g, :, :].rearrange("p r u -> p (r u)").bitcast(BF16),
+                in_=grouped[i][:, g, :, :].rearrange("p r u -> p (r u)").bitcast(BF16),
             )
 
-        def mx(gi):
-            c, i, x, w = groups[gi]
-            sums[gi] = psum.tile([P, 512], F32, name="pm", tag="pm%d" % (gi % MX_BANKS))
+        def multiply(item, on_vector):
+            c, i0, h, x, w = item[0]
+            n = P * w
+            sums = psum.tile([P, BANK], F32, name="pm", tag="pm%d" % (fill_count[0] % MX_BANKS))
+            fill_count[0] += 1
             codes, scales = quantised[c]
-            for g in range(PASSES):
-                nc.tensor.matmul_mx(
-                    out=sums[gi][:, 0 : P * w],
-                    lhsT=codes[:, g, P * i : P * i + P].bitcast(FP8X4),
-                    lhsT_scale=scales[:, g, P * i : P * i + P],
-                    rhs=codes[:, g, P * x : P * (x + w)].bitcast(FP8X4),
-                    rhs_scale=scales[:, g, P * x : P * (x + w)],
-                    start=(g == 0),
-                    stop=(g == PASSES - 1),
-                )
+            for i in range(i0, i0 + h):
+                for g in range(PASSES):
+                    nc.tensor.matmul_mx(
+                        out=sums[:, n * (i - i0) : n * (i - i0) + n],
+                        lhsT=codes[:, g, P * i : P * i + P].bitcast(FP8X4),
+                        lhsT_scale=scales[:, g, P * i : P * i + P],
+                        rhs=codes[:, g, P * x : P * x + n].bitcast(FP8X4),
+                        rhs_scale=scales[:, g, P * x : P * x + n],
+                        start=(g == 0),
+                        stop=(g == PASSES - 1),
+                    )
+            dst = results[c][:, i0 : i0 + h, P * x : P * x + n]
+            src = sums[:, 0 : n * h].rearrange("p (h n) -> p h n", h=h)
+            if on_vector:
+                nc.vector.tensor_copy(out=dst, in_=src)
+            else:
+                nc.scalar.copy(out=dst, in_=src)
+            if len(item) > 1:
+                store(*item[1])
 
-        def result(gi):
-            c, i, x, w = groups[gi]
-            key = TILES * c + i
-            if key not in results:
-                results[key] = work.tile([P, ROWS], F32, name="ot", tag="ot%d" % (key % OT_BUFS))
-            copy_out_of_psum(
-                gi in RESULTS_COPIED_BY_VECTOR, results[key][:, P * x : P * (x + w)], sums[gi][:, 0 : P * w]
-            )
-
-        def store(k):
-            c, i, x, w = stores[k]
+        def store(c, i0, i1, x0, x1):
             nc.sync.dma_start(
-                out=out[c, P * i : P * i + P, P * x : P * (x + w)],
-                in_=results[TILES * c + i][:, P * x : P * (x + w)],
+                out=out[c, P * i0 : P * i1, P * x0 : P * x1].rearrange("(a p) x -> p a x", p=P),
+                in_=results[c][:, i0:i1, P * x0 : P * x1],
             )
 
-        actions = {
-            "load": load, "stats": stats, "sqrt": sqrt, "recip": recip, "norm": norm, "transp": transp,
-            "regroup": regroup, "quant": quant, "mx": mx, "result": result, "store": store,
-        }
-        for kind, index in ORDER:
-            actions[kind](index)
+        waiting = []
+        last = len(pieces) - 1
+        chunks = [(j, h) for j in range(ALL_TILES) for h in range(2) if j not in STATS_ON_SCALAR]
+        halves_before = [2 * j for j in range(ALL_TILES + 1)]
+        for j in STATS_ON_SCALAR:
+            for t in range(j + 1, ALL_TILES + 1):
+                halves_before[t] -= 2
+        position = [0]
+        unaggregated = []
+
+        def aggregate_all():
+            for j in unaggregated:
+                aggregate(j)
+            unaggregated.clear()
+
+        def advance(until):
+            while position[0] < min(until, len(chunks)):
+                j, h = chunks[position[0]]
+                position[0] += 1
+                stats_half(j, h)
+                aggregate_all()
+                if h == 1:
+                    unaggregated.append(j)
+            if position[0] == len(chunks):
+                aggregate_all()
+
+        for j in STATS_ON_SCALAR:
+            if j < 8:
+                stats_on_scalar(j)
+        for i in range(-1, last + 2):
+            tail = i > last - LAST_STEPS
+            if 0 <= i <= last:
+                transpose_and_regroup(pieces[i], i)
+            if i + 1 <= last:
+                end = pieces[i + 1][0] + pieces[i + 1][1]
+                extra = 2
+                target = halves_before[end] + extra
+
+                for j in range(pieces[i + 1][0], end):
+                    if j in STATS_ON_SCALAR and j >= 8:
+                        stats_on_scalar(j)
+                advance(target - 1)
+                if unaggregated and unaggregated[0] < end:
+                    aggregate_all()
+                invert(pieces[i + 1])
+            if 0 <= i <= last:
+                for g in range(PASSES):
+                    quantise(pieces[i], i, g)
+            if i + 1 <= last:
+                advance(target)
+                for j in range(pieces[i + 1][0], end):
+                    norm(j)
+            done = 0
+            count = 0
+            quota = COLUMN_TILES_A_STEP
+            while waiting and (i > last or done < quota):
+                item = waiting.pop(0)
+                done += item[0][2] * item[0][4]
+                count += 1
+                multiply(item, tail and count % 2 == 0)
+            if 0 <= i <= last:
+                waiting.extend(fills_of(pieces[i], i > last - FINE_STORES))

@@ -87,15 +87,12 @@ def tile_generator_pb_t_kernel(tc, feat_gated, out):
 
         ident = const.tile([P, P], F32, name="ident")
         make_identity(nc, ident[:])
-        minus_half = const.tile([P, 4], F32, name="minus_half")
-        nc.gpsimd.memset(minus_half[:], -0.5)
 
         xs = [keep.tile([P, TILES, K], BF16, name="x%d" % c) for c in range(COMMUNITIES)]
         results = [keep.tile([P, TILES, ROWS], F32, name="r%d" % c) for c in range(COMMUNITIES)]
         st = keep.tile([P, ALL_TILES, K // BN_CHUNK, BN_STATS_DIM], F32, name="st")
         mv = keep.tile([P, ALL_TILES, 2], F32, name="mv")
         ssq = keep.tile([P, ALL_TILES], F32, name="ssq")
-        sd = keep.tile([P, ALL_TILES], F32, name="sd")
         inv = keep.tile([P, ALL_TILES], F32, name="inv")
 
         normalised = {}
@@ -127,11 +124,8 @@ def tile_generator_pb_t_kernel(tc, feat_gated, out):
 
         def invert(piece):
             j0, n = piece
-            nc.gpsimd.tensor_tensor(
-                out=sd[:, j0 : j0 + n], in0=mv[:, j0 : j0 + n, 1], in1=minus_half[:, 0:n], op=ALU.pow
-            )
-            nc.gpsimd.tensor_scalar(
-                out=inv[:, j0 : j0 + n], in0=sd[:, j0 : j0 + n], scalar1=K ** -0.5, scalar2=0.0, op0=ALU.mult, op1=ALU.add
+            nc.scalar.activation(
+                out=inv[:, j0 : j0 + n], in_=mv[:, j0 : j0 + n, 1], func=ACT.Abs_reciprocal_sqrt, scale=float(K)
             )
 
         def norm(j):

@@ -223,7 +223,7 @@ def tile_generator_pb_t_kernel(tc, feat_gated, out):
                 aggregate_all()
 
         for j in STATS_ON_SCALAR:
-            if j < 8:
+            if j < 0:
                 stats_on_scalar(j)
         for i in range(-1, last + 2):
             tail = i > last - LAST_STEPS
@@ -235,9 +235,9 @@ def tile_generator_pb_t_kernel(tc, feat_gated, out):
                 target = halves_before[end] + extra
 
                 for j in range(pieces[i + 1][0], end):
-                    if j in STATS_ON_SCALAR and j >= 8:
+                    if j in STATS_ON_SCALAR and j >= 0:
                         stats_on_scalar(j)
-                advance(target - 1)
+                advance(target - 0)
                 if unaggregated and unaggregated[0] < end:
                     aggregate_all()
                 invert(pieces[i + 1])

@@ -231,7 +231,7 @@ def tile_generator_pb_t_kernel(tc, feat_gated, out):
                 transpose_and_regroup(pieces[i], i)
             if i + 1 <= last:
                 end = pieces[i + 1][0] + pieces[i + 1][1]
-                extra = 2
+                extra = 3
                 target = halves_before[end] + extra
 
                 for j in range(pieces[i + 1][0], end):
@@ -241,13 +241,13 @@ def tile_generator_pb_t_kernel(tc, feat_gated, out):
                 if unaggregated and unaggregated[0] < end:
                     aggregate_all()
                 invert(pieces[i + 1])
+            if i + 1 <= last:
+                for j in range(pieces[i + 1][0], end):
+                    norm(j)
+                advance(target + 0)
             if 0 <= i <= last:
                 for g in range(PASSES):
                     quantise(pieces[i], i, g)
-            if i + 1 <= last:
-                advance(target)
-                for j in range(pieces[i + 1][0], end):
-                    norm(j)
             done = 0
             count = 0
             quota = COLUMN_TILES_A_STEP

@@ -34,7 +34,7 @@ PIECE_SIZES = (2,) * 16
 COLUMN_TILES_A_STEP = 16
 LAST_STEPS = 2
 FINE_STORES = 3
-STATS_ON_SCALAR = ()
+STATS_ON_SCALAR = (1, 3)
 
 
 def spans(sizes):
@@ -222,25 +222,27 @@ def tile_generator_pb_t_kernel(tc, feat_gated, out):
             if position[0] == len(chunks):
                 aggregate_all()
 
-        for j in STATS_ON_SCALAR:
-            if j < 0:
-                stats_on_scalar(j)
+        splan = {-2: (1,), -1: (3,)}
+        for j in splan.get(-2, ()):
+            stats_on_scalar(j)
         for i in range(-1, last + 2):
             tail = i > last - LAST_STEPS
             if 0 <= i <= last:
                 transpose_and_regroup(pieces[i], i)
             if i + 1 <= last:
                 end = pieces[i + 1][0] + pieces[i + 1][1]
-                extra = 3
+                extra = (4, 7, 6, 5, 4)[i + 1] if i < 4 else 3
                 target = halves_before[end] + extra
 
                 for j in range(pieces[i + 1][0], end):
-                    if j in STATS_ON_SCALAR and j >= 0:
+                    if j in STATS_ON_SCALAR and j >= 99:
                         stats_on_scalar(j)
                 advance(target - 0)
                 if unaggregated and unaggregated[0] < end:
                     aggregate_all()
                 invert(pieces[i + 1])
+            for j in splan.get(i, ()):
+                stats_on_scalar(j)
             if i + 1 <= last:
                 for j in range(pieces[i + 1][0], end):
                     norm(j)

@@ -86,6 +86,8 @@ def tile_generator_pb_t_kernel(tc, feat_gated, out):
         ctx.enter_context(tc.manual_schedule())
 
         ident = const.tile([P, P], F32, name="ident")
+        one = const.tile([P, 1], F32, name="one")
+        nc.gpsimd.memset(one[:], 1.0)
         make_identity(nc, ident[:])
 
         xs = [keep.tile([P, TILES, K], BF16, name="x%d" % c) for c in range(COMMUNITIES)]
@@ -94,6 +96,9 @@ def tile_generator_pb_t_kernel(tc, feat_gated, out):
         mv = keep.tile([P, ALL_TILES, 2], F32, name="mv")
         ssq = keep.tile([P, ALL_TILES], F32, name="ssq")
         inv = keep.tile([P, ALL_TILES], F32, name="inv")
+
+        unused_root = keep.tile([P, 1], F32, name="unused_root")
+        nc.scalar.activation(out=unused_root[:], in_=one[:], func=ACT.Abs_reciprocal_sqrt)
 
         normalised = {}
         grouped = {}

@@ -154,19 +154,18 @@ def tile_generator_pb_t_kernel(tc, feat_gated, out):
                     in_=bank[:].rearrange("p (g u) r -> p g r u", g=PASSES),
                 )
 
-        def quantise(piece, i, g):
+        def quantise(piece, i):
             j0, n = piece
             c, a0 = divmod(j0, TILES)
             if c not in quantised:
                 quantised[c] = (
-                    work.tile([P, PASSES, ROWS], U32, name="codes", tag="codes%d" % (c % 2), align_bytes=64),
-                    work.tile([P, PASSES, ROWS], U8, name="scales", tag="scales%d" % (c % 2), align_bytes=64),
+                    work.tile([P, TILES // 2, PASSES, 2 * P], U32, name="codes", tag="codes%d" % (c % 2), align_bytes=64),
+                    work.tile([P, TILES // 2, PASSES, 2 * P], U8, name="scales", tag="scales%d" % (c % 2), align_bytes=64),
                 )
-            cols = slice(P * a0, P * (a0 + n))
             nc.vector.quantize_mx(
-                out=quantised[c][0][:, g, cols].bitcast(FP8X4),
-                scales=quantised[c][1][:, g, cols],
-                in_=grouped[i][:, g, :, :].rearrange("p r u -> p (r u)").bitcast(BF16),
+                out=quantised[c][0][:, a0 // 2, :, :].rearrange("p g r -> p (g r)").bitcast(FP8X4),
+                scales=quantised[c][1][:, a0 // 2, :, :].rearrange("p g r -> p (g r)"),
+                in_=grouped[i][:].rearrange("p g r u -> p (g r u)").bitcast(BF16),
             )
 
         def multiply(item, on_vector):
@@ -176,16 +175,19 @@ def tile_generator_pb_t_kernel(tc, feat_gated, out):
             fill_count[0] += 1
             codes, scales = quantised[c]
             for i in range(i0, i0 + h):
-                for g in range(PASSES):
-                    nc.tensor.matmul_mx(
-                        out=sums[:, n * (i - i0) : n * (i - i0) + n],
-                        lhsT=codes[:, g, P * i : P * i + P].bitcast(FP8X4),
-                        lhsT_scale=scales[:, g, P * i : P * i + P],
-                        rhs=codes[:, g, P * x : P * x + n].bitcast(FP8X4),
-                        rhs_scale=scales[:, g, P * x : P * x + n],
-                        start=(g == 0),
-                        stop=(g == PASSES - 1),
-                    )
+                rows = slice(P * (i % 2), P * (i % 2) + P)
+                for pair in range(x // 2, (x + w) // 2):
+                    at = n * (i - i0) + 2 * P * (pair - x // 2)
+                    for g in range(PASSES):
+                        nc.tensor.matmul_mx(
+                            out=sums[:, at : at + 2 * P],
+                            lhsT=codes[:, i // 2, g, rows].bitcast(FP8X4),
+                            lhsT_scale=scales[:, i // 2, g, rows],
+                            rhs=codes[:, pair, g, :].bitcast(FP8X4),
+                            rhs_scale=scales[:, pair, g, :],
+                            start=(g == 0),
+                            stop=(g == PASSES - 1),
+                        )
             dst = results[c][:, i0 : i0 + h, P * x : P * x + n]
             src = sums[:, 0 : n * h].rearrange("p (h n) -> p h n", h=h)
             if on_vector:
@@ -253,8 +255,7 @@ def tile_generator_pb_t_kernel(tc, feat_gated, out):
                     norm(j)
                 advance(target + 0)
             if 0 <= i <= last:
-                for g in range(PASSES):
-                    quantise(pieces[i], i, g)
+                quantise(pieces[i], i)
             done = 0
             count = 0
             quota = COLUMN_TILES_A_STEP

@@ -238,7 +238,7 @@ def tile_generator_pb_t_kernel(tc, feat_gated, out):
                 transpose_and_regroup(pieces[i], i)
             if i + 1 <= last:
                 end = pieces[i + 1][0] + pieces[i + 1][1]
-                extra = (4, 7, 6, 5, 4)[i + 1] if i < 4 else 3
+                extra = 4 if i < 0 else max(4 if i < 8 else 3, 7 - i)
                 target = halves_before[end] + extra
 
                 for j in range(pieces[i + 1][0], end):
@@ -258,7 +258,7 @@ def tile_generator_pb_t_kernel(tc, feat_gated, out):
                 quantise(pieces[i], i)
             done = 0
             count = 0
-            quota = COLUMN_TILES_A_STEP
+            quota = 20 if i > 9 else 16
             while waiting and (i > last or done < quota):
                 item = waiting.pop(0)
                 done += item[0][2] * item[0][4]

from contextlib import ExitStack

import concourse.mybir as mybir
from concourse.masks import make_identity

FLOPS = 2 * 4 * 1024 * 1024 * 1024

BF16 = mybir.dt.bfloat16
F32 = mybir.dt.float32
U32 = mybir.dt.uint32
U8 = mybir.dt.uint8
FP8X4 = mybir.dt.float8_e4m3fn_x4
ALU = mybir.AluOpType
ACT = mybir.ActivationFunctionType

P = 128
K = 1024
K_PASS = 512
PASSES = K // K_PASS
ROWS = 1024
COMMUNITIES = 4
TILES = ROWS // P
ALL_TILES = COMMUNITIES * TILES
BN_CHUNK = 512
BN_STATS_DIM = 6
BANK = 512
WORDS = K // 2

T_BANKS = 2
MX_BANKS = 8 - T_BANKS

LOAD_SIZES = (1, 1, 2, 2, 2, 4, 4, 4, 4, 4, 4)
PIECE_SIZES = (2,) * 16
COLUMN_TILES_A_STEP = 16
LAST_STEPS = 2
FINE_STORES = 3
STATS_ON_SCALAR = (1, 3)


def spans(sizes):
    pairs = []
    first = 0
    for n in sizes:
        pairs.append((first, n))
        first += n
    return pairs


def bank_fills(c, i0, i1, x0, x1):
    fills = []
    x = x0
    while x < x1:
        w = 4 if x1 - x >= 4 else (2 if x1 - x >= 2 else 1)
        i = i0
        while i < i1:
            h = min(4 // w, i1 - i)
            fills.append((c, i, h, x, w))
            i += h
        x += w
    return fills


def fills_of(piece, fine):
    j0, n = piece
    c, a0 = divmod(j0, TILES)
    items = []
    for i0, i1, x0, x1 in ((0, a0, a0, a0 + n), (a0, a0 + n, 0, a0 + n)):
        fills = bank_fills(c, i0, i1, x0, x1)
        if fine:
            items.extend([(f, (c, f[1], f[1] + f[2], f[3], f[3] + f[4])) for f in fills])
        elif fills:
            items.extend([(f,) for f in fills[:-1]])
            items.append((fills[-1], (c, i0, i1, x0, x1)))
    return items


def tile_generator_pb_t_kernel(tc, feat_gated, out):
    nc = tc.nc
    pieces = spans(PIECE_SIZES)

    with ExitStack() as ctx:
        const = ctx.enter_context(tc.tile_pool(name="const", bufs=1))
        keep = ctx.enter_context(tc.tile_pool(name="keep", bufs=1))
        work = ctx.enter_context(tc.tile_pool(name="work", bufs=1))
        psum = ctx.enter_context(tc.psum_pool(name="psum", bufs=1))
        ctx.enter_context(tc.manual_schedule())

        ident = const.tile([P, P], F32, name="ident")
        one = const.tile([P, 1], F32, name="one")
        nc.gpsimd.memset(one[:], 1.0)
        make_identity(nc, ident[:])

        xs = [keep.tile([P, TILES, K], BF16, name="x%d" % c) for c in range(COMMUNITIES)]
        results = [keep.tile([P, TILES, ROWS], F32, name="r%d" % c) for c in range(COMMUNITIES)]
        st = keep.tile([P, ALL_TILES, K // BN_CHUNK, BN_STATS_DIM], F32, name="st")
        mv = keep.tile([P, ALL_TILES, 2], F32, name="mv")
        ssq = keep.tile([P, ALL_TILES], F32, name="ssq")
        inv = keep.tile([P, ALL_TILES], F32, name="inv")

        unused_root = keep.tile([P, 1], F32, name="unused_root")
        nc.scalar.activation(out=unused_root[:], in_=one[:], func=ACT.Abs_reciprocal_sqrt)

        normalised = {}
        grouped = {}
        quantised = {}
        fill_count = [0]

        for j0, n in spans(LOAD_SIZES):
            c, a0 = divmod(j0, TILES)
            src = feat_gated[c, P * a0 : P * (a0 + n), :].rearrange("(a p) k -> p a k", p=P)
            nc.sync.dma_start(out=xs[c][:, a0 : a0 + n, :], in_=src)

        def stats_half(j, h):
            c, a = divmod(j, TILES)
            nc.vector.bn_stats(out=st[:, j, h, :], in_=xs[c][:, a, BN_CHUNK * h : BN_CHUNK * h + BN_CHUNK])

        def stats_on_scalar(j):
            c, a = divmod(j, TILES)
            for func, scale, bias, total in (
                (ACT.Copy, 1.0 / K, 0.0, mv[:, j, 0:1]),
                (ACT.Square, -1.0, mv[:, j, 0:1], ssq[:, j : j + 1]),
            ):
                unused = work.tile([P, K], BF16, name="unused", tag="unused")
                nc.scalar.activation(out=unused[:], in_=xs[c][:, a, :], func=func, scale=scale, bias=bias, accum_out=total)
            nc.scalar.activation(out=mv[:, j, 1:2], in_=ssq[:, j : j + 1], func=ACT.Copy, scale=1.0 / K)

        def aggregate(j):
            nc.vector.bn_aggr(out=mv[:, j, :], in_=st[:, j, :, :].rearrange("p a b -> p (a b)"))

        def invert(piece):
            j0, n = piece
            nc.scalar.activation(
                out=inv[:, j0 : j0 + n], in_=mv[:, j0 : j0 + n, 1], func=ACT.Abs_reciprocal_sqrt, scale=float(K)
            )

        def norm(j):
            c, a = divmod(j, TILES)
            normalised[j] = work.tile([P, K], BF16, name="fn", tag="fn%d" % (j % 4))
            nc.vector.tensor_scalar(
                out=normalised[j][:], in0=xs[c][:, a, :], scalar1=mv[:, j, 0:1], scalar2=inv[:, j : j + 1],
                op0=ALU.subtract, op1=ALU.mult,
            )

        def transpose_and_regroup(piece, i):
            j0, n = piece
            grouped[i] = work.tile([P, PASSES, P * n, 2], F32, name="gr", tag="gr%d" % (i % 2), align_bytes=64)
            for j in range(j0, j0 + n):
                bank = psum.tile([P, WORDS // P, P], F32, name="pt", tag="pt%d" % (j % T_BANKS))
                words = normalised[j][:].bitcast(F32)
                for b in range(WORDS // P):
                    nc.tensor.transpose(bank[:, b, :], words[:, P * b : P * b + P], ident[:])
                nc.scalar.copy(
                    out=grouped[i][:, :, P * (j - j0) : P * (j - j0) + P, :],
                    in_=bank[:].rearrange("p (g u) r -> p g r u", g=PASSES),
                )

        def quantise(piece, i):
            j0, n = piece
            c, a0 = divmod(j0, TILES)
            if c not in quantised:
                quantised[c] = (
                    work.tile([P, TILES // 2, PASSES, 2 * P], U32, name="codes", tag="codes%d" % (c % 2), align_bytes=64),
                    work.tile([P, TILES // 2, PASSES, 2 * P], U8, name="scales", tag="scales%d" % (c % 2), align_bytes=64),
                )
            nc.vector.quantize_mx(
                out=quantised[c][0][:, a0 // 2, :, :].rearrange("p g r -> p (g r)").bitcast(FP8X4),
                scales=quantised[c][1][:, a0 // 2, :, :].rearrange("p g r -> p (g r)"),
                in_=grouped[i][:].rearrange("p g r u -> p (g r u)").bitcast(BF16),
            )

        def multiply(item, on_vector):
            c, i0, h, x, w = item[0]
            n = P * w
            sums = psum.tile([P, BANK], F32, name="pm", tag="pm%d" % (fill_count[0] % MX_BANKS))
            fill_count[0] += 1
            codes, scales = quantised[c]
            for i in range(i0, i0 + h):
                rows = slice(P * (i % 2), P * (i % 2) + P)
                for pair in range(x // 2, (x + w) // 2):
                    at = n * (i - i0) + 2 * P * (pair - x // 2)
                    for g in range(PASSES):
                        nc.tensor.matmul_mx(
                            out=sums[:, at : at + 2 * P],
                            lhsT=codes[:, i // 2, g, rows].bitcast(FP8X4),
                            lhsT_scale=scales[:, i // 2, g, rows],
                            rhs=codes[:, pair, g, :].bitcast(FP8X4),
                            rhs_scale=scales[:, pair, g, :],
                            start=(g == 0),
                            stop=(g == PASSES - 1),
                        )
            dst = results[c][:, i0 : i0 + h, P * x : P * x + n]
            src = sums[:, 0 : n * h].rearrange("p (h n) -> p h n", h=h)
            if on_vector:
                nc.vector.tensor_copy(out=dst, in_=src)
            else:
                nc.scalar.copy(out=dst, in_=src)
            if len(item) > 1:
                store(*item[1])

        def store(c, i0, i1, x0, x1):
            nc.sync.dma_start(
                out=out[c, P * i0 : P * i1, P * x0 : P * x1].rearrange("(a p) x -> p a x", p=P),
                in_=results[c][:, i0:i1, P * x0 : P * x1],
            )

        waiting = []
        last = len(pieces) - 1
        chunks = [(j, h) for j in range(ALL_TILES) for h in range(2) if j not in STATS_ON_SCALAR]
        halves_before = [2 * j for j in range(ALL_TILES + 1)]
        for j in STATS_ON_SCALAR:
            for t in range(j + 1, ALL_TILES + 1):
                halves_before[t] -= 2
        position = [0]
        unaggregated = []

        def aggregate_all():
            for j in unaggregated:
                aggregate(j)
            unaggregated.clear()

        def advance(until):
            while position[0] < min(until, len(chunks)):
                j, h = chunks[position[0]]
                position[0] += 1
                stats_half(j, h)
                aggregate_all()
                if h == 1:
                    unaggregated.append(j)
            if position[0] == len(chunks):
                aggregate_all()

        splan = {-2: (1,), -1: (3,)}
        for j in splan.get(-2, ()):
            stats_on_scalar(j)
        for i in range(-1, last + 2):
            tail = i > last - LAST_STEPS
            if 0 <= i <= last:
                transpose_and_regroup(pieces[i], i)
            if i + 1 <= last:
                end = pieces[i + 1][0] + pieces[i + 1][1]
                extra = 4 if i < 0 else max(4 if i < 8 else 3, 7 - i)
                target = halves_before[end] + extra

                for j in range(pieces[i + 1][0], end):
                    if j in STATS_ON_SCALAR and j >= 99:
                        stats_on_scalar(j)
                advance(target - 0)
                if unaggregated and unaggregated[0] < end:
                    aggregate_all()
                invert(pieces[i + 1])
            for j in splan.get(i, ()):
                stats_on_scalar(j)
            if i + 1 <= last:
                for j in range(pieces[i + 1][0], end):
                    norm(j)
                advance(target + 0)
            if 0 <= i <= last:
                quantise(pieces[i], i)
            done = 0
            count = 0
            quota = 20 if i > 9 else 16
            while waiting and (i > last or done < quota):
                item = waiting.pop(0)
                done += item[0][2] * item[0][4]
                count += 1
                multiply(item, tail and count % 2 == 0)
            if 0 <= i <= last:
                waiting.extend(fills_of(pieces[i], i > last - FINE_STORES))
